import numpy as np
import ml_dtypes


def mxq(x, axis, fmt="e4m3"):
    dtype, down = {"e4m3": (ml_dtypes.float8_e4m3fn, 7), "e5m2": (ml_dtypes.float8_e5m2, 14)}[fmt]
    v = np.moveaxis(np.asarray(x, np.float32).astype(ml_dtypes.bfloat16).astype(np.float64), axis, -1)
    blocks = v.reshape(v.shape[:-1] + (-1, 32))
    amax = np.abs(blocks).max(-1, keepdims=True)
    byte = np.maximum(np.where(amax > 0, np.frexp(amax)[1] - 1 + 127, 0) - down, 1)
    scale = np.exp2(byte - 127.0)
    codes = (blocks / scale).astype(np.float32).astype(dtype).astype(np.float64)
    return np.moveaxis((codes * scale).reshape(v.shape), -1, axis)


WIDE = False


def mx_kscale(k):
    if not WIDE:
        return np.ones(k)
    levels = np.array([10, -10, 5, -5, 0])
    a = np.random.permutation(np.resize(levels, k // 512 * 4)).reshape(k // 512, 4)
    idx = np.arange(k)
    return np.exp2(a[idx // 512, idx % 128 // 32])


BF16 = ml_dtypes.bfloat16


def bf(x):
    return np.asarray(x, np.float32).astype(BF16)


def f64(x):
    return np.asarray(x).astype(np.float64)


N, T, U, H, J, V = 16, 16, 8, 512, 1024, 2048
TEMP = 1.0


def log_softmax(v):
    d = v - v.max(-1, keepdims=True)
    return d - np.log(np.exp(d).sum(-1, keepdims=True))


def setup_inputs():
    s = mx_kscale(2 * H)
    return {"h_pred": bf(np.random.standard_normal((N, U, H)) * s[:H]),
            "h_enc": bf(np.random.standard_normal((N, T, H)) * s[H:]),
            "W1": bf(np.random.standard_normal((2 * H, J)) / np.sqrt(2 * H) / s[:, None]),
            "b1": bf(np.random.standard_normal(J) * 0.1),
            "W2": bf(np.random.standard_normal((J, V)) * 2.0 / np.sqrt(J)),
            "b2": bf(np.random.standard_normal(V) * 0.1)}


def reference(h_pred, h_enc, W1, b1, W2, b2):
    H_p = h_pred.shape[-1]
    w1q = mxq(f64(W1), 0, "e4m3")
    pred_proj = mxq(f64(h_pred), 2, "e4m3") @ w1q[:H_p]
    enc_proj = mxq(f64(h_enc), 2, "e4m3") @ w1q[H_p:]
    z = pred_proj[:, None, :, :] + enc_proj[:, :, None, :] + f64(b1)
    x = np.tanh(z)
    logits = (mxq(x, 3, "e4m3") @ mxq(f64(W2), 0, "e4m3")) + f64(b2)
    return log_softmax(logits / TEMP)

@@ -1,0 +1,289 @@
+import math
+from contextlib import ExitStack
+
+import concourse.mybir as mybir
+from concourse.masks import make_identity
+
+F32 = mybir.dt.float32
+BF16 = mybir.dt.bfloat16
+U32 = mybir.dt.uint32
+U8 = mybir.dt.uint8
+I32 = mybir.dt.int32
+FP8X4 = mybir.dt.float8_e4m3fn_x4
+ALU = mybir.AluOpType
+ACT = mybir.ActivationFunctionType
+AX = mybir.AxisListType
+
+P = 128
+N_B, T_E, U_P, H, J, V = 16, 16, 8, 512, 1024, 2048
+FLOPS = 2 * (N_B * U_P * H * J + N_B * T_E * H * J + N_B * T_E * U_P * J * V)
+LN2 = math.log(2.0)
+NEWTON = 4
+D_GPS = 1536
+
+
+def tile_joint_kernel(tc, h_pred, h_enc, W1, b1, W2, b2, out):
+    nc = tc.nc
+    out_rows = out.rearrange("n t u v -> (n t u) v")
+    with ExitStack() as ctx:
+        const = ctx.enter_context(tc.tile_pool(name="const", bufs=1))
+        rawp = ctx.enter_context(tc.tile_pool(name="rawp", bufs=6))
+        grpp = ctx.enter_context(tc.tile_pool(name="grpp", bufs=3))
+        zp = ctx.enter_context(tc.tile_pool(name="zp", bufs=3))
+        xp = ctx.enter_context(tc.tile_pool(name="xp", bufs=3))
+        xqp = ctx.enter_context(tc.tile_pool(name="xqp", bufs=6))
+        yp = ctx.enter_context(tc.tile_pool(name="yp", bufs=6))
+        jp = ctx.enter_context(tc.tile_pool(name="jp", bufs=2))
+        st = ctx.enter_context(tc.tile_pool(name="st", bufs=6))
+        psum = ctx.enter_context(tc.psum_pool(name="psum", bufs=8))
+
+        b2row = const.tile([P, V], BF16, name="b2row")
+        nc.vector.memset(b2row[:].bitcast(I32), 0)
+        b1rows = const.tile([P, P], BF16, name="b1rows")
+        nc.vector.memset(b1rows[:].bitcast(I32), 0)
+        ones = const.tile([P, P], BF16, name="ones")
+        nc.vector.memset(ones[:], 1.0)
+        kb = const.tile([P, NEWTON], F32, name="kb")
+        for k in range(NEWTON):
+            nc.vector.memset(kb[:, k : k + 1], float(k - NEWTON))
+        identf = const.tile([P, P], F32, name="identf")
+        make_identity(nc, identf[:])
+        identb = const.tile([P, P], BF16, name="identb")
+        make_identity(nc, identb[:])
+
+        hp_sb = const.tile([P, H], BF16, name="hp_sb")
+        nc.sync.dma_start(out=hp_sb[:], in_=h_pred.rearrange("n u h -> (n u) h"))
+        he_sb = const.tile([P, 2, H], BF16, name="he_sb")
+        nc.sync.dma_start(
+            out=he_sb[:],
+            in_=h_enc.rearrange("n t h -> (n t) h").rearrange("(a p) h -> p a h", p=P),
+        )
+        nc.scalar.dma_start(out=b1rows[0:8, :], in_=b1.rearrange("(a m) -> a m", a=8))
+        nc.scalar.dma_start(out=b2row[0:1, :], in_=b2.rearrange("(o v) -> o v", o=1))
+
+        raw1 = []
+        for half in range(2):
+            raw = rawp.tile([P, 4, J], BF16, name="raw1_%d" % half, tag="raw")
+            nc.sync.dma_start(
+                out=raw[:].rearrange("p (u e) c -> p u (e c)", u=2),
+                in_=W1[half * H : (half + 1) * H, :].rearrange(
+                    "(u q e) c -> q u (e c)", u=2, q=P, e=2
+                ),
+            )
+            raw1.append(raw)
+        raw2 = []
+        for vb in range(4):
+            raw = rawp.tile([P, 8, 512], BF16, name="raw2_%d" % vb, tag="raw")
+            nc.sync.dma_start(
+                out=raw[:],
+                in_=W2[:, vb * 512 : (vb + 1) * 512].rearrange("(g p) v -> p g v", p=P),
+            )
+            raw2.append(raw)
+
+        hpT = psum.tile([P, 2, P], F32, name="hpT", tag="bank")
+        for u in range(2):
+            nc.tensor.transpose(
+                hpT[:, u, :], hp_sb[:].bitcast(F32)[:, u * P : (u + 1) * P], identf[:]
+            )
+        heT = psum.tile([P, 2, 2, P], F32, name="heT", tag="bank")
+        for a in range(2):
+            for u in range(2):
+                nc.tensor.transpose(
+                    heT[:, a, u, :],
+                    he_sb[:, a, :].bitcast(F32)[:, u * P : (u + 1) * P],
+                    identf[:],
+                )
+        hp_g = const.tile([P, P, 2], F32, name="hp_g", align_bytes=64)
+        nc.vector.tensor_copy(out=hp_g[:], in_=hpT[:].rearrange("p u r -> p r u"))
+        he_g = const.tile([P, 2, P, 2], F32, name="he_g", align_bytes=64)
+        nc.vector.tensor_copy(out=he_g[:], in_=heT[:].rearrange("p a u r -> p a r u"))
+        hp_q = const.tile([P, P], U32, name="hp_q", align_bytes=64)
+        hp_s = const.tile([P, P], U8, name="hp_s", align_bytes=64)
+        he_q = const.tile([P, 2 * P], U32, name="he_q", align_bytes=64)
+        he_s = const.tile([P, 2 * P], U8, name="he_s", align_bytes=64)
+        nc.vector.quantize_mx(
+            out=hp_q[:].bitcast(FP8X4),
+            scales=hp_s[:],
+            in_=hp_g[:].rearrange("p r u -> p (r u)").bitcast(BF16),
+        )
+        nc.vector.quantize_mx(
+            out=he_q[:].bitcast(FP8X4),
+            scales=he_s[:],
+            in_=he_g[:].rearrange("p a r u -> p (a r u)").bitcast(BF16),
+        )
+
+        b1ps = psum.tile([P, P], BF16, name="b1ps", tag="bank")
+        nc.tensor.transpose(b1ps[:], b1rows[:], identb[:])
+        b1T = const.tile([P, 8], F32, name="b1T")
+        nc.vector.tensor_copy(out=b1T[:], in_=b1ps[:, 0:8])
+        b2bc = const.tile([P, V], BF16, name="b2bc")
+        for vb in range(4):
+            b2ps = psum.tile([P, 512], F32, name="b2ps", tag="bank")
+            nc.tensor.matmul(
+                out=b2ps[:], lhsT=ones[:], rhs=b2row[:, vb * 512 : (vb + 1) * 512],
+                start=True, stop=True,
+            )
+            nc.scalar.copy(out=b2bc[:, vb * 512 : (vb + 1) * 512], in_=b2ps[:])
+
+        w1_q = const.tile([P, 2, J], U32, name="w1_q", align_bytes=64)
+        w1_s = const.tile([P, 2, J], U8, name="w1_s", align_bytes=64)
+        SPLIT1 = 640
+        for half in range(2):
+            grp = grpp.tile([P, J, 4], BF16, name="grp1", tag="grp", align_bytes=64)
+            nc.vector.tensor_copy(
+                out=grp[:, 0:SPLIT1, :].rearrange("p (c i) t -> p c t i", i=4),
+                in_=raw1[half][:, :, 0:SPLIT1].rearrange("p t (c i) -> p c t i", i=4),
+            )
+            nc.scalar.copy(
+                out=grp[:, SPLIT1:J, :].rearrange("p (c i) t -> p c t i", i=4),
+                in_=raw1[half][:, :, SPLIT1:J].rearrange("p t (c i) -> p c t i", i=4),
+            )
+            nc.vector.quantize_mx(
+                out=w1_q[:, half, :].bitcast(FP8X4),
+                scales=w1_s[:, half, :],
+                in_=grp[:].rearrange("p c t -> p (c t)"),
+            )
+
+        predb = const.tile([P, 2, P, 4], F32, name="predb")
+        encs = const.tile([P, 2, 2 * P, 4], F32, name="encs")
+        for c in range(2):
+            for blk in range(3):
+                half = 0 if blk == 0 else 1
+                bank = psum.tile([P, 4, P], F32, name="s1bank", tag="bank")
+                for t in range(4):
+                    jt = 4 * c + t
+                    if blk == 0:
+                        rq, rs = hp_q[:, :], hp_s[:, :]
+                    else:
+                        rq = he_q[:, (blk - 1) * P : blk * P]
+                        rs = he_s[:, (blk - 1) * P : blk * P]
+                    nc.tensor.matmul_mx(
+                        out=bank[:, t, :],
+                        lhsT=w1_q[:, half, jt * P : (jt + 1) * P].bitcast(FP8X4),
+                        lhsT_scale=w1_s[:, half, jt * P : (jt + 1) * P],
+                        rhs=rq.bitcast(FP8X4),
+                        rhs_scale=rs,
+                        start=True,
+                        stop=True,
+                    )
+                if blk == 0:
+                    nc.vector.tensor_tensor(
+                        out=predb[:, c],
+                        in0=bank[:].rearrange("p t r -> p r t"),
+                        in1=b1T[:, 4 * c : 4 * c + 4].unsqueeze(1).to_broadcast([P, P, 4]),
+                        op=ALU.add,
+                    )
+                else:
+                    nc.scalar.copy(
+                        out=encs[:, c, (blk - 1) * P : blk * P, :],
+                        in_=bank[:].rearrange("p t r -> p r t"),
+                    )
+
+        xq_t = {}
+
+        def make_x(n):
+            z = zp.tile([P, 2, P, 4], F32, name="z", tag="z")
+            for c in range(2):
+                nc.gpsimd.tensor_tensor(
+                    out=z[:, c].rearrange("p (a u) t -> p a u t", u=U_P),
+                    in0=predb[:, c, n * U_P : (n + 1) * U_P, :]
+                    .unsqueeze(1)
+                    .to_broadcast([P, T_E, U_P, 4]),
+                    in1=encs[:, c, n * T_E : (n + 1) * T_E, :]
+                    .unsqueeze(2)
+                    .to_broadcast([P, T_E, U_P, 4]),
+                    op=ALU.add,
+                )
+            x = xp.tile([P, 2 * P * 4], BF16, name="x", tag="x", align_bytes=64)
+            nc.scalar.activation(
+                out=x[:], in_=z[:].rearrange("p c w t -> p (c w t)"), func=ACT.Tanh
+            )
+            xq = xqp.tile([P, 2 * P], U32, name="xq", tag="xq", align_bytes=64)
+            xs = xqp.tile([P, 2 * P], U8, name="xs", tag="xs", align_bytes=64)
+            nc.vector.quantize_mx(out=xq[:].bitcast(FP8X4), scales=xs[:], in_=x[:])
+            xq_t[n] = (xq, xs)
+
+        make_x(0)
+        make_x(1)
+
+        w2_q = const.tile([P, 4, 2, 512], U32, name="w2_q", align_bytes=64)
+        w2_s = const.tile([P, 4, 2, 512], U8, name="w2_s", align_bytes=64)
+        for vb in range(4):
+            grp = grpp.tile([P, 2, 512, 4], BF16, name="grp2", tag="grp", align_bytes=64)
+            nc.vector.tensor_copy(
+                out=grp[:, 0].rearrange("p (v i) t -> p v t i", i=4),
+                in_=raw2[vb][:, 0:4, :].rearrange("p t (v i) -> p v t i", i=4),
+            )
+            nc.scalar.copy(
+                out=grp[:, 1].rearrange("p (v i) t -> p v t i", i=4),
+                in_=raw2[vb][:, 4:8, :].rearrange("p t (v i) -> p v t i", i=4),
+            )
+            nc.vector.quantize_mx(
+                out=w2_q[:, vb].rearrange("p c v -> p (c v)").bitcast(FP8X4),
+                scales=w2_s[:, vb].rearrange("p c v -> p (c v)"),
+                in_=grp[:].rearrange("p c v t -> p (c v t)"),
+            )
+
+        for n in range(N_B):
+            if n + 2 < N_B:
+                make_x(n + 2)
+            xq, xs = xq_t[n]
+            banks = []
+            for vb in range(4):
+                banks.append(psum.tile([P, 512], F32, name="lg%d" % vb, tag="bank"))
+            for c in range(2):
+                for vb in range(4):
+                    nc.tensor.matmul_mx(
+                        out=banks[vb][:],
+                        lhsT=xq[:, c * P : (c + 1) * P].bitcast(FP8X4),
+                        lhsT_scale=xs[:, c * P : (c + 1) * P],
+                        rhs=w2_q[:, vb, c, :].bitcast(FP8X4),
+                        rhs_scale=w2_s[:, vb, c, :],
+                        start=(c == 0),
+                        stop=(c == 1),
+                    )
+            y = yp.tile([P, V], F32, name="y", tag="y")
+            for vb in range(4):
+                nc.vector.tensor_tensor(
+                    out=y[:, vb * 512 : (vb + 1) * 512],
+                    in0=banks[vb][:],
+                    in1=b2bc[:, vb * 512 : (vb + 1) * 512],
+                    op=ALU.add,
+                )
+            negm = st.tile([P, 1], F32, name="negm", tag="negm")
+            nc.vector.tensor_reduce(out=negm[:], in_=y[:], axis=AX.X, op=ALU.max, negate=True)
+            junk = jp.tile([P, V], BF16, name="junk", tag="junk")
+            ssum = st.tile([P, 1], F32, name="ssum", tag="ssum")
+            nc.scalar.activation(
+                out=junk[:], in_=y[:], func=ACT.Exp, bias=negm[:, 0:1], scale=1.0,
+                accum_out=ssum[:, 0:1],
+            )
+            r = st.tile([P, 1], F32, name="r0", tag="r0")
+            nc.vector.tensor_scalar(
+                out=r[:], in0=ssum[:].bitcast(I32),
+                scalar1=LN2 / 8388608.0, scalar2=LN2 * (0.043 - 127.0) - float(NEWTON),
+                op0=ALU.mult, op1=ALU.add,
+            )
+            for k in range(NEWTON):
+                e = st.tile([P, 1], F32, name="e%d" % k, tag="e%d" % k)
+                nc.scalar.activation(
+                    out=e[:], in_=r[:], func=ACT.Exp, bias=kb[:, k : k + 1], scale=-1.0
+                )
+                r2 = st.tile([P, 1], F32, name="r%d" % (k + 1), tag="r%d" % (k + 1))
+                nc.scalar.activation(
+                    out=r2[:], in_=e[:], func=ACT.Identity, bias=r[:, 0:1], scale=ssum[:, 0:1]
+                )
+                r = r2
+            negk = st.tile([P, 1], F32, name="negk", tag="negk")
+            nc.scalar.activation(
+                out=negk[:], in_=r[:], func=ACT.Identity, bias=negm[:, 0:1], scale=-1.0
+            )
+            nc.gpsimd.tensor_scalar(
+                out=y[:, 0:D_GPS], in0=y[:, 0:D_GPS], scalar1=negk[:, 0:1], scalar2=1.0,
+                op0=ALU.add, op1=ALU.mult,
+            )
+            nc.scalar.activation(
+                out=y[:, D_GPS:V], in_=y[:, D_GPS:V], func=ACT.Identity, bias=negk[:, 0:1],
+                scale=1.0,
+            )
+            nc.sync.dma_start(out=out_rows[n * P : (n + 1) * P, :], in_=y[:])

@@ -19,7 +19,7 @@ N_B, T_E, U_P, H, J, V = 16, 16, 8, 512, 1024, 2048
 FLOPS = 2 * (N_B * U_P * H * J + N_B * T_E * H * J + N_B * T_E * U_P * J * V)
 LN2 = math.log(2.0)
 NEWTON = 4
-D_GPS = 1536
+SPLIT1 = 640
 
 
 def tile_joint_kernel(tc, h_pred, h_enc, W1, b1, W2, b2, out):
@@ -31,11 +31,12 @@ def tile_joint_kernel(tc, h_pred, h_enc, W1, b1, W2, b2, out):
         grpp = ctx.enter_context(tc.tile_pool(name="grpp", bufs=3))
         zp = ctx.enter_context(tc.tile_pool(name="zp", bufs=3))
         xp = ctx.enter_context(tc.tile_pool(name="xp", bufs=3))
-        xqp = ctx.enter_context(tc.tile_pool(name="xqp", bufs=6))
+        xqp = ctx.enter_context(tc.tile_pool(name="xqp", bufs=4))
         yp = ctx.enter_context(tc.tile_pool(name="yp", bufs=6))
         jp = ctx.enter_context(tc.tile_pool(name="jp", bufs=2))
-        st = ctx.enter_context(tc.tile_pool(name="st", bufs=6))
+        st = ctx.enter_context(tc.tile_pool(name="st", bufs=8))
         psum = ctx.enter_context(tc.psum_pool(name="psum", bufs=8))
+        ctx.enter_context(tc.manual_schedule())
 
         b2row = const.tile([P, V], BF16, name="b2row")
         nc.vector.memset(b2row[:].bitcast(I32), 0)
@@ -43,26 +44,19 @@ def tile_joint_kernel(tc, h_pred, h_enc, W1, b1, W2, b2, out):
         nc.vector.memset(b1rows[:].bitcast(I32), 0)
         ones = const.tile([P, P], BF16, name="ones")
         nc.vector.memset(ones[:], 1.0)
-        kb = const.tile([P, NEWTON], F32, name="kb")
+        kb = const.tile([P, NEWTON + 1], F32, name="kb")
         for k in range(NEWTON):
             nc.vector.memset(kb[:, k : k + 1], float(k - NEWTON))
+        nc.vector.memset(kb[:, NEWTON : NEWTON + 1], LN2 * (0.043 - 127.0) - float(NEWTON))
         identf = const.tile([P, P], F32, name="identf")
         make_identity(nc, identf[:])
         identb = const.tile([P, P], BF16, name="identb")
         make_identity(nc, identb[:])
 
-        hp_sb = const.tile([P, H], BF16, name="hp_sb")
-        nc.sync.dma_start(out=hp_sb[:], in_=h_pred.rearrange("n u h -> (n u) h"))
-        he_sb = const.tile([P, 2, H], BF16, name="he_sb")
-        nc.sync.dma_start(
-            out=he_sb[:],
-            in_=h_enc.rearrange("n t h -> (n t) h").rearrange("(a p) h -> p a h", p=P),
-        )
-        nc.scalar.dma_start(out=b1rows[0:8, :], in_=b1.rearrange("(a m) -> a m", a=8))
         nc.scalar.dma_start(out=b2row[0:1, :], in_=b2.rearrange("(o v) -> o v", o=1))
+        nc.scalar.dma_start(out=b1rows[0:8, :], in_=b1.rearrange("(a m) -> a m", a=8))
 
-        raw1 = []
-        for half in range(2):
+        def load_w1(half):
             raw = rawp.tile([P, 4, J], BF16, name="raw1_%d" % half, tag="raw")
             nc.sync.dma_start(
                 out=raw[:].rearrange("p (u e) c -> p u (e c)", u=2),
@@ -70,7 +64,17 @@ def tile_joint_kernel(tc, h_pred, h_enc, W1, b1, W2, b2, out):
                     "(u q e) c -> q u (e c)", u=2, q=P, e=2
                 ),
             )
-            raw1.append(raw)
+            return raw
+
+        raw1 = [load_w1(0)]
+        hp_sb = const.tile([P, H], BF16, name="hp_sb")
+        nc.sync.dma_start(out=hp_sb[:], in_=h_pred.rearrange("n u h -> (n u) h"))
+        he_sb = const.tile([P, 2, H], BF16, name="he_sb")
+        nc.sync.dma_start(
+            out=he_sb[:],
+            in_=h_enc.rearrange("n t h -> (n t) h").rearrange("(a p) h -> p a h", p=P),
+        )
+        raw1.append(load_w1(1))
         raw2 = []
         for vb in range(4):
             raw = rawp.tile([P, 8, 512], BF16, name="raw2_%d" % vb, tag="raw")
@@ -80,6 +84,39 @@ def tile_joint_kernel(tc, h_pred, h_enc, W1, b1, W2, b2, out):
             )
             raw2.append(raw)
 
+        b2bc = const.tile([P, V], BF16, name="b2bc")
+        for vb in range(4):
+            b2ps = psum.tile([P, 512], F32, name="b2ps", tag="bank")
+            nc.tensor.matmul(
+                out=b2ps[:], lhsT=ones[:], rhs=b2row[:, vb * 512 : (vb + 1) * 512],
+                start=True, stop=True,
+            )
+            nc.scalar.copy(out=b2bc[:, vb * 512 : (vb + 1) * 512], in_=b2ps[:])
+
+        w1_q = const.tile([P, 2, J], U32, name="w1_q", align_bytes=64)
+        w1_s = const.tile([P, 2, J], U8, name="w1_s", align_bytes=64)
+        grp1 = []
+        for half in range(2):
+            grp1.append(grpp.tile([P, J, 4], BF16, name="grp1_%d" % half, tag="grp", align_bytes=64))
+
+        def regroup_w1(eng_copy, half, c0, c1):
+            eng_copy(
+                out=grp1[half][:, c0:c1, :].rearrange("p (c i) t -> p c t i", i=4),
+                in_=raw1[half][:, :, c0:c1].rearrange("p t (c i) -> p c t i", i=4),
+            )
+
+        def quant_w1(half):
+            nc.vector.quantize_mx(
+                out=w1_q[:, half, :].bitcast(FP8X4),
+                scales=w1_s[:, half, :],
+                in_=grp1[half][:].rearrange("p c t -> p (c t)"),
+            )
+
+        regroup_w1(nc.vector.tensor_copy, 0, 0, SPLIT1)
+        regroup_w1(nc.scalar.copy, 0, SPLIT1, J)
+
+        b1ps = psum.tile([P, P], BF16, name="b1ps", tag="bank")
+        nc.tensor.transpose(b1ps[:], b1rows[:], identb[:])
         hpT = psum.tile([P, 2, P], F32, name="hpT", tag="bank")
         for u in range(2):
             nc.tensor.transpose(
@@ -93,6 +130,8 @@ def tile_joint_kernel(tc, h_pred, h_enc, W1, b1, W2, b2, out):
                     he_sb[:, a, :].bitcast(F32)[:, u * P : (u + 1) * P],
                     identf[:],
                 )
+        b1T = const.tile([P, 8], F32, name="b1T")
+        nc.vector.tensor_copy(out=b1T[:], in_=b1ps[:, 0:8])
         hp_g = const.tile([P, P, 2], F32, name="hp_g", align_bytes=64)
         nc.vector.tensor_copy(out=hp_g[:], in_=hpT[:].rearrange("p u r -> p r u"))
         he_g = const.tile([P, 2, P, 2], F32, name="he_g", align_bytes=64)
@@ -111,78 +150,83 @@ def tile_joint_kernel(tc, h_pred, h_enc, W1, b1, W2, b2, out):
             scales=he_s[:],
             in_=he_g[:].rearrange("p a r u -> p (a r u)").bitcast(BF16),
         )
+        quant_w1(0)
+        regroup_w1(nc.vector.tensor_copy, 1, 0, SPLIT1)
+        regroup_w1(nc.scalar.copy, 1, SPLIT1, J)
+        quant_w1(1)
 
-        b1ps = psum.tile([P, P], BF16, name="b1ps", tag="bank")
-        nc.tensor.transpose(b1ps[:], b1rows[:], identb[:])
-        b1T = const.tile([P, 8], F32, name="b1T")
-        nc.vector.tensor_copy(out=b1T[:], in_=b1ps[:, 0:8])
-        b2bc = const.tile([P, V], BF16, name="b2bc")
-        for vb in range(4):
-            b2ps = psum.tile([P, 512], F32, name="b2ps", tag="bank")
-            nc.tensor.matmul(
-                out=b2ps[:], lhsT=ones[:], rhs=b2row[:, vb * 512 : (vb + 1) * 512],
-                start=True, stop=True,
-            )
-            nc.scalar.copy(out=b2bc[:, vb * 512 : (vb + 1) * 512], in_=b2ps[:])
+        w2_q = const.tile([P, 4, 2, 512], U32, name="w2_q", align_bytes=64)
+        w2_s = const.tile([P, 4, 2, 512], U8, name="w2_s", align_bytes=64)
+        grp2 = {}
 
-        w1_q = const.tile([P, 2, J], U32, name="w1_q", align_bytes=64)
-        w1_s = const.tile([P, 2, J], U8, name="w1_s", align_bytes=64)
-        SPLIT1 = 640
-        for half in range(2):
-            grp = grpp.tile([P, J, 4], BF16, name="grp1", tag="grp", align_bytes=64)
-            nc.vector.tensor_copy(
-                out=grp[:, 0:SPLIT1, :].rearrange("p (c i) t -> p c t i", i=4),
-                in_=raw1[half][:, :, 0:SPLIT1].rearrange("p t (c i) -> p c t i", i=4),
+        def regroup_w2(eng_copy, vb, c, v0, v1):
+            if vb not in grp2:
+                grp2[vb] = grpp.tile(
+                    [P, 2, 512, 4], BF16, name="grp2_%d" % vb, tag="grp", align_bytes=64
+                )
+            eng_copy(
+                out=grp2[vb][:, c, v0:v1, :].rearrange("p (v i) t -> p v t i", i=4),
+                in_=raw2[vb][:, 4 * c : 4 * c + 4, v0:v1].rearrange("p t (v i) -> p v t i", i=4),
             )
-            nc.scalar.copy(
-                out=grp[:, SPLIT1:J, :].rearrange("p (c i) t -> p c t i", i=4),
-                in_=raw1[half][:, :, SPLIT1:J].rearrange("p t (c i) -> p c t i", i=4),
-            )
+
+        def quant_w2(vb):
             nc.vector.quantize_mx(
-                out=w1_q[:, half, :].bitcast(FP8X4),
-                scales=w1_s[:, half, :],
-                in_=grp[:].rearrange("p c t -> p (c t)"),
+                out=w2_q[:, vb].rearrange("p c v -> p (c v)").bitcast(FP8X4),
+                scales=w2_s[:, vb].rearrange("p c v -> p (c v)"),
+                in_=grp2[vb][:].rearrange("p c v t -> p (c v t)"),
             )
 
         predb = const.tile([P, 2, P, 4], F32, name="predb")
         encs = const.tile([P, 2, 2 * P, 4], F32, name="encs")
-        for c in range(2):
-            for blk in range(3):
-                half = 0 if blk == 0 else 1
-                bank = psum.tile([P, 4, P], F32, name="s1bank", tag="bank")
-                for t in range(4):
-                    jt = 4 * c + t
-                    if blk == 0:
-                        rq, rs = hp_q[:, :], hp_s[:, :]
-                    else:
-                        rq = he_q[:, (blk - 1) * P : blk * P]
-                        rs = he_s[:, (blk - 1) * P : blk * P]
-                    nc.tensor.matmul_mx(
-                        out=bank[:, t, :],
-                        lhsT=w1_q[:, half, jt * P : (jt + 1) * P].bitcast(FP8X4),
-                        lhsT_scale=w1_s[:, half, jt * P : (jt + 1) * P],
-                        rhs=rq.bitcast(FP8X4),
-                        rhs_scale=rs,
-                        start=True,
-                        stop=True,
-                    )
+
+        def stage1(c, blk):
+            half = 0 if blk == 0 else 1
+            bank = psum.tile([P, 4, P], F32, name="s1bank", tag="bank")
+            for t in range(4):
+                jt = 4 * c + t
                 if blk == 0:
-                    nc.vector.tensor_tensor(
-                        out=predb[:, c],
-                        in0=bank[:].rearrange("p t r -> p r t"),
-                        in1=b1T[:, 4 * c : 4 * c + 4].unsqueeze(1).to_broadcast([P, P, 4]),
-                        op=ALU.add,
-                    )
+                    rq, rs = hp_q[:, :], hp_s[:, :]
                 else:
-                    nc.scalar.copy(
-                        out=encs[:, c, (blk - 1) * P : blk * P, :],
-                        in_=bank[:].rearrange("p t r -> p r t"),
-                    )
+                    rq = he_q[:, (blk - 1) * P : blk * P]
+                    rs = he_s[:, (blk - 1) * P : blk * P]
+                nc.tensor.matmul_mx(
+                    out=bank[:, t, :],
+                    lhsT=w1_q[:, half, jt * P : (jt + 1) * P].bitcast(FP8X4),
+                    lhsT_scale=w1_s[:, half, jt * P : (jt + 1) * P],
+                    rhs=rq.bitcast(FP8X4),
+                    rhs_scale=rs,
+                    start=True,
+                    stop=True,
+                )
+            return bank
 
-        xq_t = {}
+        def evac_enc(eng_copy, bank, c, blk):
+            eng_copy(
+                out=encs[:, c, (blk - 1) * P : blk * P, :],
+                in_=bank[:].rearrange("p t r -> p r t"),
+            )
 
-        def make_x(n):
+        pb = [stage1(0, 0), stage1(1, 0)]
+        for c in range(2):
+            nc.vector.tensor_tensor(
+                out=predb[:, c],
+                in0=pb[c][:].rearrange("p t r -> p r t"),
+                in1=b1T[:, 4 * c : 4 * c + 4].unsqueeze(1).to_broadcast([P, P, 4]),
+                op=ALU.add,
+            )
+        regroup_w2(nc.scalar.copy, 0, 1, 0, 256)
+        eb = [stage1(0, 1), stage1(1, 1)]
+        evac_enc(nc.scalar.copy, eb[0], 0, 1)
+        evac_enc(nc.scalar.copy, eb[1], 1, 1)
+        eb2 = [stage1(0, 2), stage1(1, 2)]
+        evac_enc(nc.vector.tensor_copy, eb2[0], 0, 2)
+        evac_enc(nc.vector.tensor_copy, eb2[1], 1, 2)
+
+        z_t, x_t, xq_t, bank_t, y_t, negm_t, ssum_t, chain_t, negk_t = {}, {}, {}, {}, {}, {}, {}, {}, {}
+
+        def zadd(n):
             z = zp.tile([P, 2, P, 4], F32, name="z", tag="z")
+            z_t[n] = z
             for c in range(2):
                 nc.gpsimd.tensor_tensor(
                     out=z[:, c].rearrange("p (a u) t -> p a u t", u=U_P),
@@ -194,96 +238,195 @@ def tile_joint_kernel(tc, h_pred, h_enc, W1, b1, W2, b2, out):
                     .to_broadcast([P, T_E, U_P, 4]),
                     op=ALU.add,
                 )
-            x = xp.tile([P, 2 * P * 4], BF16, name="x", tag="x", align_bytes=64)
+
+        def tanh(n, c):
+            if c == 0:
+                x_t[n] = xp.tile([P, 2, P * 4], BF16, name="x", tag="x", align_bytes=64)
             nc.scalar.activation(
-                out=x[:], in_=z[:].rearrange("p c w t -> p (c w t)"), func=ACT.Tanh
+                out=x_t[n][:, c, :], in_=z_t[n][:, c].rearrange("p w t -> p (w t)"), func=ACT.Tanh
             )
+
+        def quant_x(n):
             xq = xqp.tile([P, 2 * P], U32, name="xq", tag="xq", align_bytes=64)
             xs = xqp.tile([P, 2 * P], U8, name="xs", tag="xs", align_bytes=64)
-            nc.vector.quantize_mx(out=xq[:].bitcast(FP8X4), scales=xs[:], in_=x[:])
+            nc.vector.quantize_mx(
+                out=xq[:].bitcast(FP8X4), scales=xs[:], in_=x_t[n][:].rearrange("p c w -> p (c w)")
+            )
             xq_t[n] = (xq, xs)
 
-        make_x(0)
-        make_x(1)
-
-        w2_q = const.tile([P, 4, 2, 512], U32, name="w2_q", align_bytes=64)
-        w2_s = const.tile([P, 4, 2, 512], U8, name="w2_s", align_bytes=64)
-        for vb in range(4):
-            grp = grpp.tile([P, 2, 512, 4], BF16, name="grp2", tag="grp", align_bytes=64)
-            nc.vector.tensor_copy(
-                out=grp[:, 0].rearrange("p (v i) t -> p v t i", i=4),
-                in_=raw2[vb][:, 0:4, :].rearrange("p t (v i) -> p v t i", i=4),
-            )
-            nc.scalar.copy(
-                out=grp[:, 1].rearrange("p (v i) t -> p v t i", i=4),
-                in_=raw2[vb][:, 4:8, :].rearrange("p t (v i) -> p v t i", i=4),
-            )
-            nc.vector.quantize_mx(
-                out=w2_q[:, vb].rearrange("p c v -> p (c v)").bitcast(FP8X4),
-                scales=w2_s[:, vb].rearrange("p c v -> p (c v)"),
-                in_=grp[:].rearrange("p c v t -> p (c v t)"),
-            )
-
-        for n in range(N_B):
-            if n + 2 < N_B:
-                make_x(n + 2)
+        def mm(n, vb):
             xq, xs = xq_t[n]
-            banks = []
-            for vb in range(4):
-                banks.append(psum.tile([P, 512], F32, name="lg%d" % vb, tag="bank"))
+            bank = psum.tile([P, 512], F32, name="lg", tag="bank")
+            bank_t[(n, vb)] = bank
             for c in range(2):
-                for vb in range(4):
-                    nc.tensor.matmul_mx(
-                        out=banks[vb][:],
-                        lhsT=xq[:, c * P : (c + 1) * P].bitcast(FP8X4),
-                        lhsT_scale=xs[:, c * P : (c + 1) * P],
-                        rhs=w2_q[:, vb, c, :].bitcast(FP8X4),
-                        rhs_scale=w2_s[:, vb, c, :],
-                        start=(c == 0),
-                        stop=(c == 1),
-                    )
-            y = yp.tile([P, V], F32, name="y", tag="y")
-            for vb in range(4):
-                nc.vector.tensor_tensor(
-                    out=y[:, vb * 512 : (vb + 1) * 512],
-                    in0=banks[vb][:],
-                    in1=b2bc[:, vb * 512 : (vb + 1) * 512],
-                    op=ALU.add,
+                nc.tensor.matmul_mx(
+                    out=bank[:],
+                    lhsT=xq[:, c * P : (c + 1) * P].bitcast(FP8X4),
+                    lhsT_scale=xs[:, c * P : (c + 1) * P],
+                    rhs=w2_q[:, vb, c, :].bitcast(FP8X4),
+                    rhs_scale=w2_s[:, vb, c, :],
+                    start=(c == 0),
+                    stop=(c == 1),
                 )
+
+        def add_b2(n, vb):
+            if vb == 0:
+                y_t[n] = yp.tile([P, V], F32, name="y", tag="y")
+            nc.vector.tensor_tensor(
+                out=y_t[n][:, vb * 512 : (vb + 1) * 512],
+                in0=bank_t[(n, vb)][:],
+                in1=b2bc[:, vb * 512 : (vb + 1) * 512],
+                op=ALU.add,
+            )
+
+        def row_max(n):
             negm = st.tile([P, 1], F32, name="negm", tag="negm")
-            nc.vector.tensor_reduce(out=negm[:], in_=y[:], axis=AX.X, op=ALU.max, negate=True)
+            negm_t[n] = negm
+            nc.vector.tensor_reduce(out=negm[:], in_=y_t[n][:], axis=AX.X, op=ALU.max, negate=True)
+
+        def exp_sum(n):
             junk = jp.tile([P, V], BF16, name="junk", tag="junk")
             ssum = st.tile([P, 1], F32, name="ssum", tag="ssum")
+            ssum_t[n] = ssum
             nc.scalar.activation(
-                out=junk[:], in_=y[:], func=ACT.Exp, bias=negm[:, 0:1], scale=1.0,
+                out=junk[:], in_=y_t[n][:], func=ACT.Exp, bias=negm_t[n][:, 0:1], scale=1.0,
                 accum_out=ssum[:, 0:1],
             )
-            r = st.tile([P, 1], F32, name="r0", tag="r0")
-            nc.vector.tensor_scalar(
-                out=r[:], in0=ssum[:].bitcast(I32),
-                scalar1=LN2 / 8388608.0, scalar2=LN2 * (0.043 - 127.0) - float(NEWTON),
-                op0=ALU.mult, op1=ALU.add,
-            )
-            for k in range(NEWTON):
-                e = st.tile([P, 1], F32, name="e%d" % k, tag="e%d" % k)
+
+        def step(n, k):
+            if n < 0 or n >= N_B:
+                return
+            if k == 1:
+                r = st.tile([P, 1], F32, name="nr", tag="nr")
                 nc.scalar.activation(
-                    out=e[:], in_=r[:], func=ACT.Exp, bias=kb[:, k : k + 1], scale=-1.0
+                    out=r[:], in_=ssum_t[n][:].bitcast(U32), func=ACT.Identity,
+                    bias=kb[:, NEWTON : NEWTON + 1], scale=LN2 / 8388608.0,
                 )
-                r2 = st.tile([P, 1], F32, name="r%d" % (k + 1), tag="r%d" % (k + 1))
+                chain_t[n] = (r, None)
+            elif k == 2 * NEWTON + 2:
+                r, e = chain_t[n]
+                negk = st.tile([P, 1], F32, name="negk", tag="negk")
                 nc.scalar.activation(
-                    out=r2[:], in_=e[:], func=ACT.Identity, bias=r[:, 0:1], scale=ssum[:, 0:1]
+                    out=negk[:], in_=r[:], func=ACT.Identity, bias=negm_t[n][:, 0:1], scale=-1.0
                 )
-                r = r2
-            negk = st.tile([P, 1], F32, name="negk", tag="negk")
-            nc.scalar.activation(
-                out=negk[:], in_=r[:], func=ACT.Identity, bias=negm[:, 0:1], scale=-1.0
-            )
+                negk_t[n] = negk
+            elif k % 2 == 0:
+                r, e = chain_t[n]
+                i = k // 2 - 1
+                e = st.tile([P, 1], F32, name="ne", tag="ne")
+                nc.scalar.activation(
+                    out=e[:], in_=r[:], func=ACT.Exp, bias=kb[:, i : i + 1], scale=-1.0
+                )
+                chain_t[n] = (r, e)
+            else:
+                r, e = chain_t[n]
+                r2 = st.tile([P, 1], F32, name="nr", tag="nr")
+                nc.scalar.activation(
+                    out=r2[:], in_=e[:], func=ACT.Identity, bias=r[:, 0:1], scale=ssum_t[n][:, 0:1]
+                )
+                chain_t[n] = (r2, None)
+
+        def sub_gps(n, c0, c1):
             nc.gpsimd.tensor_scalar(
-                out=y[:, 0:D_GPS], in0=y[:, 0:D_GPS], scalar1=negk[:, 0:1], scalar2=1.0,
+                out=y_t[n][:, c0:c1], in0=y_t[n][:, c0:c1], scalar1=negk_t[n][:, 0:1], scalar2=1.0,
                 op0=ALU.add, op1=ALU.mult,
             )
+
+        def sub_act(n, c0, c1):
             nc.scalar.activation(
-                out=y[:, D_GPS:V], in_=y[:, D_GPS:V], func=ACT.Identity, bias=negk[:, 0:1],
-                scale=1.0,
+                out=y_t[n][:, c0:c1], in_=y_t[n][:, c0:c1], func=ACT.Identity,
+                bias=negk_t[n][:, 0:1], scale=1.0,
             )
-            nc.sync.dma_start(out=out_rows[n * P : (n + 1) * P, :], in_=y[:])
+
+        def sub_vec(n, c0, c1):
+            nc.vector.tensor_scalar(
+                out=y_t[n][:, c0:c1], in0=y_t[n][:, c0:c1], scalar1=negk_t[n][:, 0:1], scalar2=None,
+                op0=ALU.add,
+            )
+
+        def store(n):
+            nc.sync.dma_start(out=out_rows[n * P : (n + 1) * P, :], in_=y_t[n][:])
+
+        zadd(0)
+        regroup_w2(nc.vector.tensor_copy, 0, 0, 0, 512)
+        regroup_w2(nc.scalar.copy, 0, 1, 256, 512)
+        quant_w2(0)
+        zadd(1)
+        tanh(0, 0)
+        tanh(0, 1)
+        quant_x(0)
+        mm(0, 0)
+        regroup_w2(nc.vector.tensor_copy, 1, 0, 0, 512)
+        regroup_w2(nc.scalar.copy, 1, 1, 0, 256)
+        regroup_w2(nc.scalar.copy, 1, 1, 256, 512)
+        add_b2(0, 0)
+        quant_w2(1)
+        mm(0, 1)
+        zadd(2)
+        tanh(1, 0)
+        tanh(1, 1)
+        regroup_w2(nc.vector.tensor_copy, 2, 0, 0, 512)
+        regroup_w2(nc.scalar.copy, 2, 1, 0, 256)
+        regroup_w2(nc.scalar.copy, 2, 1, 256, 512)
+        quant_x(1)
+        mm(1, 0)
+        mm(1, 1)
+        add_b2(0, 1)
+        quant_w2(2)
+        mm(0, 2)
+        mm(1, 2)
+        zadd(3)
+        tanh(2, 0)
+        tanh(2, 1)
+        regroup_w2(nc.vector.tensor_copy, 3, 0, 0, 512)
+        regroup_w2(nc.scalar.copy, 3, 1, 0, 256)
+        regroup_w2(nc.scalar.copy, 3, 1, 256, 512)
+        add_b2(0, 2)
+        quant_w2(3)
+        mm(0, 3)
+        mm(1, 3)
+        add_b2(0, 3)
+        row_max(0)
+
+        for s in range(1, N_B + 5):
+            d = s - 4
+            if 0 <= d < 12:
+                sub_gps(d, 0, 1536)
+            elif 12 <= d < 15:
+                sub_gps(d, 1024, V)
+            elif d == 15:
+                sub_gps(d, 1024, 1536)
+            if s + 3 < N_B:
+                zadd(s + 3)
+            if s + 1 < N_B:
+                quant_x(s + 1)
+                for vb in range(4):
+                    mm(s + 1, vb)
+            if s < N_B:
+                for vb in range(4):
+                    add_b2(s, vb)
+                row_max(s)
+            if 12 <= d < N_B:
+                sub_vec(d, 0, 1024)
+            if s - 1 < N_B:
+                exp_sum(s - 1)
+            step(s - 2, 4)
+            step(s - 3, 8)
+            if s + 2 < N_B:
+                tanh(s + 2, 0)
+            step(s - 1, 1)
+            step(s - 2, 5)
+            step(s - 3, 9)
+            if s + 2 < N_B:
+                tanh(s + 2, 1)
+            step(s - 1, 2)
+            step(s - 2, 6)
+            step(s - 3, 10)
+            if 0 <= d < 12:
+                sub_act(d, 1536, V)
+            elif d == 15:
+                sub_act(d, 1536, V)
+            step(s - 1, 3)
+            step(s - 2, 7)
+            if 0 <= d < N_B:
+                store(d)

@@ -38,12 +38,12 @@ def tile_joint_kernel(tc, h_pred, h_enc, W1, b1, W2, b2, out):
         psum = ctx.enter_context(tc.psum_pool(name="psum", bufs=8))
         ctx.enter_context(tc.manual_schedule())
 
-        b2row = const.tile([P, V], BF16, name="b2row")
-        nc.vector.memset(b2row[:].bitcast(I32), 0)
-        b1rows = const.tile([P, P], BF16, name="b1rows")
-        nc.vector.memset(b1rows[:].bitcast(I32), 0)
-        ones = const.tile([P, P], BF16, name="ones")
-        nc.vector.memset(ones[:], 1.0)
+        brows = const.tile([P, P], BF16, name="brows")
+        nc.sync.dma_start(out=brows[0:8, :], in_=b1.rearrange("(a m) -> a m", a=8))
+        nc.sync.dma_start(out=brows[8:24, :], in_=b2.rearrange("(a m) -> a m", a=16))
+        nc.sync.dma_start(out=brows[24:32, :], in_=b2[0:1024].rearrange("(a m) -> a m", a=8))
+        nc.vector.memset(brows[32:64, :].bitcast(I32), 0)
+        nc.vector.memset(brows[64:128, :].bitcast(I32), 0)
         kb = const.tile([P, NEWTON + 1], F32, name="kb")
         for k in range(NEWTON):
             nc.vector.memset(kb[:, k : k + 1], float(k - NEWTON))
@@ -53,8 +53,6 @@ def tile_joint_kernel(tc, h_pred, h_enc, W1, b1, W2, b2, out):
         identb = const.tile([P, P], BF16, name="identb")
         make_identity(nc, identb[:])
 
-        nc.scalar.dma_start(out=b2row[0:1, :], in_=b2.rearrange("(o v) -> o v", o=1))
-        nc.scalar.dma_start(out=b1rows[0:8, :], in_=b1.rearrange("(a m) -> a m", a=8))
 
         def load_w1(half):
             raw = rawp.tile([P, 4, J], BF16, name="raw1_%d" % half, tag="raw")
@@ -84,14 +82,25 @@ def tile_joint_kernel(tc, h_pred, h_enc, W1, b1, W2, b2, out):
             )
             raw2.append(raw)
 
+        bps = psum.tile([P, P], BF16, name="bps", tag="bank")
+        nc.tensor.transpose(bps[:], brows[:], identb[:])
+        b1T = const.tile([P, 8], F32, name="b1T")
+        nc.vector.tensor_copy(out=b1T[:], in_=bps[:, 0:8])
+        b2T = const.tile([P, 16], BF16, name="b2T")
+        nc.vector.tensor_copy(out=b2T[:], in_=bps[:, 8:24])
         b2bc = const.tile([P, V], BF16, name="b2bc")
         for vb in range(4):
-            b2ps = psum.tile([P, 512], F32, name="b2ps", tag="bank")
-            nc.tensor.matmul(
-                out=b2ps[:], lhsT=ones[:], rhs=b2row[:, vb * 512 : (vb + 1) * 512],
-                start=True, stop=True,
+            b2ps = psum.tile([P, 4, P], F32, name="b2ps", tag="bank")
+            for a in range(4):
+                nc.tensor.matmul(
+                    out=b2ps[:, a, :],
+                    lhsT=b2T[:, 4 * vb + a : 4 * vb + a + 1].to_broadcast([P, P]),
+                    rhs=identb[:],
+                    start=True, stop=True,
+                )
+            nc.scalar.copy(
+                out=b2bc[:, vb * 512 : (vb + 1) * 512], in_=b2ps[:].rearrange("p a m -> p (a m)")
             )
-            nc.scalar.copy(out=b2bc[:, vb * 512 : (vb + 1) * 512], in_=b2ps[:])
 
         w1_q = const.tile([P, 2, J], U32, name="w1_q", align_bytes=64)
         w1_s = const.tile([P, 2, J], U8, name="w1_s", align_bytes=64)
@@ -115,8 +124,6 @@ def tile_joint_kernel(tc, h_pred, h_enc, W1, b1, W2, b2, out):
         regroup_w1(nc.vector.tensor_copy, 0, 0, SPLIT1)
         regroup_w1(nc.scalar.copy, 0, SPLIT1, J)
 
-        b1ps = psum.tile([P, P], BF16, name="b1ps", tag="bank")
-        nc.tensor.transpose(b1ps[:], b1rows[:], identb[:])
         hpT = psum.tile([P, 2, P], F32, name="hpT", tag="bank")
         for u in range(2):
             nc.tensor.transpose(
@@ -130,8 +137,6 @@ def tile_joint_kernel(tc, h_pred, h_enc, W1, b1, W2, b2, out):
                     he_sb[:, a, :].bitcast(F32)[:, u * P : (u + 1) * P],
                     identf[:],
                 )
-        b1T = const.tile([P, 8], F32, name="b1T")
-        nc.vector.tensor_copy(out=b1T[:], in_=b1ps[:, 0:8])
         hp_g = const.tile([P, P, 2], F32, name="hp_g", align_bytes=64)
         nc.vector.tensor_copy(out=hp_g[:], in_=hpT[:].rearrange("p u r -> p r u"))
         he_g = const.tile([P, 2, P, 2], F32, name="he_g", align_bytes=64)

@@ -20,6 +20,8 @@ FLOPS = 2 * (N_B * U_P * H * J + N_B * T_E * H * J + N_B * T_E * U_P * J * V)
 LN2 = math.log(2.0)
 NEWTON = 4
 SPLIT1 = 640
+Y0 = 8
+D_GPS = 2048
 
 
 def tile_joint_kernel(tc, h_pred, h_enc, W1, b1, W2, b2, out):
@@ -34,6 +36,7 @@ def tile_joint_kernel(tc, h_pred, h_enc, W1, b1, W2, b2, out):
         xqp = ctx.enter_context(tc.tile_pool(name="xqp", bufs=4))
         yp = ctx.enter_context(tc.tile_pool(name="yp", bufs=6))
         jp = ctx.enter_context(tc.tile_pool(name="jp", bufs=2))
+        ytp = ctx.enter_context(tc.tile_pool(name="ytp", bufs=2))
         st = ctx.enter_context(tc.tile_pool(name="st", bufs=8))
         psum = ctx.enter_context(tc.psum_pool(name="psum", bufs=8))
         ctx.enter_context(tc.manual_schedule())
@@ -228,6 +231,7 @@ def tile_joint_kernel(tc, h_pred, h_enc, W1, b1, W2, b2, out):
         evac_enc(nc.vector.tensor_copy, eb2[1], 1, 2)
 
         z_t, x_t, xq_t, bank_t, y_t, negm_t, ssum_t, chain_t, negk_t = {}, {}, {}, {}, {}, {}, {}, {}, {}
+        lt_t, yt_t, yfull_t = {}, {}, {}
 
         def zadd(n):
             z = zp.tile([P, 2, P, 4], F32, name="z", tag="z")
@@ -274,27 +278,69 @@ def tile_joint_kernel(tc, h_pred, h_enc, W1, b1, W2, b2, out):
                     stop=(c == 1),
                 )
 
+        def mm_t(n):
+            xq, xs = xq_t[n]
+            lt = psum.tile([P, 4, P], F32, name="lt", tag="bank")
+            lt_t[n] = lt
+            for a in range(4):
+                for c in range(2):
+                    nc.tensor.matmul_mx(
+                        out=lt[:, a, :],
+                        lhsT=w2_q[:, 3, c, a * P : (a + 1) * P].bitcast(FP8X4),
+                        lhsT_scale=w2_s[:, 3, c, a * P : (a + 1) * P],
+                        rhs=xq[:, c * P : (c + 1) * P].bitcast(FP8X4),
+                        rhs_scale=xs[:, c * P : (c + 1) * P],
+                        start=(c == 0),
+                        stop=(c == 1),
+                    )
+
+        def bias_t(n):
+            yt = ytp.tile([P, 4, P], F32, name="yt", tag="yt")
+            yt_t[n] = yt
+            for a in range(4):
+                nc.scalar.activation(
+                    out=yt[:, a, :], in_=lt_t[n][:, a, :], func=ACT.Identity,
+                    bias=b2T[:, 12 + a : 13 + a], scale=1.0,
+                )
+
+        def back_t(n):
+            bank = psum.tile([P, 4, P], F32, name="lg3", tag="bank")
+            bank_t[(n, 3)] = bank
+            for a in range(4):
+                nc.tensor.transpose(bank[:, a, :], yt_t[n][:, a, :], identf[:])
+
         def add_b2(n, vb):
             if vb == 0:
-                y_t[n] = yp.tile([P, V], F32, name="y", tag="y")
-            nc.vector.tensor_tensor(
-                out=y_t[n][:, vb * 512 : (vb + 1) * 512],
-                in0=bank_t[(n, vb)][:],
-                in1=b2bc[:, vb * 512 : (vb + 1) * 512],
-                op=ALU.add,
-            )
+                yfull_t[n] = yp.tile([P, Y0 + V], F32, name="y", tag="y")
+                y_t[n] = yfull_t[n][:, Y0 : Y0 + V]
+            if vb < 3:
+                nc.vector.tensor_tensor(
+                    out=y_t[n][:, vb * 512 : (vb + 1) * 512],
+                    in0=bank_t[(n, vb)][:],
+                    in1=b2bc[:, vb * 512 : (vb + 1) * 512],
+                    op=ALU.add,
+                )
+            else:
+                nc.vector.tensor_scalar(
+                    out=y_t[n][:, 1536:V],
+                    in0=bank_t[(n, 3)][:].rearrange("p a m -> p (a m)"),
+                    scalar1=0.0, scalar2=None, op0=ALU.add, op1=ALU.max,
+                    accum_out=yfull_t[n][:, Y0 - 1 : Y0],
+                )
 
         def row_max(n):
             negm = st.tile([P, 1], F32, name="negm", tag="negm")
             negm_t[n] = negm
-            nc.vector.tensor_reduce(out=negm[:], in_=y_t[n][:], axis=AX.X, op=ALU.max, negate=True)
+            nc.vector.tensor_reduce(
+                out=negm[:], in_=yfull_t[n][:, Y0 - 1 : Y0 + 1536], axis=AX.X, op=ALU.max, negate=True
+            )
 
         def exp_sum(n):
             junk = jp.tile([P, V], BF16, name="junk", tag="junk")
             ssum = st.tile([P, 1], F32, name="ssum", tag="ssum")
             ssum_t[n] = ssum
             nc.scalar.activation(
-                out=junk[:], in_=y_t[n][:], func=ACT.Exp, bias=negm_t[n][:, 0:1], scale=1.0,
+                out=junk[:], in_=y_t[n], func=ACT.Exp, bias=negm_t[n][:, 0:1], scale=1.0,
                 accum_out=ssum[:, 0:1],
             )
 
@@ -350,7 +396,7 @@ def tile_joint_kernel(tc, h_pred, h_enc, W1, b1, W2, b2, out):
             )
 
         def store(n):
-            nc.sync.dma_start(out=out_rows[n * P : (n + 1) * P, :], in_=y_t[n][:])
+            nc.sync.dma_start(out=out_rows[n * P : (n + 1) * P, :], in_=y_t[n])
 
         zadd(0)
         regroup_w2(nc.vector.tensor_copy, 0, 0, 0, 512)
@@ -388,15 +434,19 @@ def tile_joint_kernel(tc, h_pred, h_enc, W1, b1, W2, b2, out):
         regroup_w2(nc.scalar.copy, 3, 1, 256, 512)
         add_b2(0, 2)
         quant_w2(3)
-        mm(0, 3)
-        mm(1, 3)
+        mm_t(0)
+        bias_t(0)
+        back_t(0)
+        mm_t(1)
+        bias_t(1)
+        back_t(1)
         add_b2(0, 3)
         row_max(0)
 
         for s in range(1, N_B + 5):
             d = s - 4
             if 0 <= d < 12:
-                sub_gps(d, 0, 1536)
+                sub_gps(d, 0, D_GPS)
             elif 12 <= d < 15:
                 sub_gps(d, 1024, V)
             elif d == 15:
@@ -405,7 +455,8 @@ def tile_joint_kernel(tc, h_pred, h_enc, W1, b1, W2, b2, out):
                 zadd(s + 3)
             if s + 1 < N_B:
                 quant_x(s + 1)
-                for vb in range(4):
+                mm_t(s + 1)
+                for vb in range(3):
                     mm(s + 1, vb)
             if s < N_B:
                 for vb in range(4):
@@ -417,6 +468,9 @@ def tile_joint_kernel(tc, h_pred, h_enc, W1, b1, W2, b2, out):
                 exp_sum(s - 1)
             step(s - 2, 4)
             step(s - 3, 8)
+            if s + 1 < N_B:
+                bias_t(s + 1)
+                back_t(s + 1)
             if s + 2 < N_B:
                 tanh(s + 2, 0)
             step(s - 1, 1)
@@ -427,8 +481,8 @@ def tile_joint_kernel(tc, h_pred, h_enc, W1, b1, W2, b2, out):
             step(s - 1, 2)
             step(s - 2, 6)
             step(s - 3, 10)
-            if 0 <= d < 12:
-                sub_act(d, 1536, V)
+            if 0 <= d < 12 and D_GPS < V:
+                sub_act(d, D_GPS, V)
             elif d == 15:
                 sub_act(d, 1536, V)
             step(s - 1, 3)

@@ -19,9 +19,12 @@ N_B, T_E, U_P, H, J, V = 16, 16, 8, 512, 1024, 2048
 FLOPS = 2 * (N_B * U_P * H * J + N_B * T_E * H * J + N_B * T_E * U_P * J * V)
 LN2 = math.log(2.0)
 NEWTON = 4
-SPLIT1 = 640
+SPLIT1 = 320
 Y0 = 8
-D_GPS = 2048
+D_GPS = 1792
+D_LAG = 5
+W2_ORDER = (3, 0, 1, 2)
+DENSE_FROM = 13
 
 
 def tile_joint_kernel(tc, h_pred, h_enc, W1, b1, W2, b2, out):
@@ -29,12 +32,14 @@ def tile_joint_kernel(tc, h_pred, h_enc, W1, b1, W2, b2, out):
     out_rows = out.rearrange("n t u v -> (n t u) v")
     with ExitStack() as ctx:
         const = ctx.enter_context(tc.tile_pool(name="const", bufs=1))
-        rawp = ctx.enter_context(tc.tile_pool(name="rawp", bufs=6))
-        grpp = ctx.enter_context(tc.tile_pool(name="grpp", bufs=3))
+        raw1p = ctx.enter_context(tc.tile_pool(name="raw1p", bufs=4))
+        raw2p = ctx.enter_context(tc.tile_pool(name="raw2p", bufs=4))
+        grp1p = ctx.enter_context(tc.tile_pool(name="grp1p", bufs=2))
+        grp2p = ctx.enter_context(tc.tile_pool(name="grp2p", bufs=3))
         zp = ctx.enter_context(tc.tile_pool(name="zp", bufs=3))
-        xp = ctx.enter_context(tc.tile_pool(name="xp", bufs=3))
+        xp = ctx.enter_context(tc.tile_pool(name="xp", bufs=4))
         xqp = ctx.enter_context(tc.tile_pool(name="xqp", bufs=4))
-        yp = ctx.enter_context(tc.tile_pool(name="yp", bufs=6))
+        yp = ctx.enter_context(tc.tile_pool(name="yp", bufs=7))
         jp = ctx.enter_context(tc.tile_pool(name="jp", bufs=2))
         ytp = ctx.enter_context(tc.tile_pool(name="ytp", bufs=2))
         st = ctx.enter_context(tc.tile_pool(name="st", bufs=8))
@@ -56,18 +61,22 @@ def tile_joint_kernel(tc, h_pred, h_enc, W1, b1, W2, b2, out):
         identb = const.tile([P, P], BF16, name="identb")
         make_identity(nc, identb[:])
 
+        raw1 = {}
 
-        def load_w1(half):
-            raw = rawp.tile([P, 4, J], BF16, name="raw1_%d" % half, tag="raw")
-            nc.sync.dma_start(
-                out=raw[:].rearrange("p (u e) c -> p u (e c)", u=2),
-                in_=W1[half * H : (half + 1) * H, :].rearrange(
-                    "(u q e) c -> q u (e c)", u=2, q=P, e=2
-                ),
-            )
-            return raw
+        def load_w1(half, cc):
+            raw = raw1p.tile([P, 4, 512], BF16, name="raw1_%d%d" % (half, cc), tag="raw1")
+            raw1[(half, cc)] = raw
+            for u in range(2):
+                r0 = half * H + u * 256
+                nc.sync.dma_start(
+                    out=raw[:, 2 * u : 2 * u + 2, :],
+                    in_=W1[r0 : r0 + 256, cc * 512 : (cc + 1) * 512].rearrange(
+                        "(q e) c -> q e c", e=2
+                    ),
+                )
 
-        raw1 = [load_w1(0)]
+        load_w1(0, 0)
+        load_w1(0, 1)
         hp_sb = const.tile([P, H], BF16, name="hp_sb")
         nc.sync.dma_start(out=hp_sb[:], in_=h_pred.rearrange("n u h -> (n u) h"))
         he_sb = const.tile([P, 2, H], BF16, name="he_sb")
@@ -75,15 +84,16 @@ def tile_joint_kernel(tc, h_pred, h_enc, W1, b1, W2, b2, out):
             out=he_sb[:],
             in_=h_enc.rearrange("n t h -> (n t) h").rearrange("(a p) h -> p a h", p=P),
         )
-        raw1.append(load_w1(1))
-        raw2 = []
-        for vb in range(4):
-            raw = rawp.tile([P, 8, 512], BF16, name="raw2_%d" % vb, tag="raw")
+        load_w1(1, 0)
+        load_w1(1, 1)
+        raw2 = {}
+        for vb in W2_ORDER:
+            raw = raw2p.tile([P, 8, 512], BF16, name="raw2_%d" % vb, tag="raw2")
+            raw2[vb] = raw
             nc.sync.dma_start(
                 out=raw[:],
                 in_=W2[:, vb * 512 : (vb + 1) * 512].rearrange("(g p) v -> p g v", p=P),
             )
-            raw2.append(raw)
 
         bps = psum.tile([P, P], BF16, name="bps", tag="bank")
         nc.tensor.transpose(bps[:], brows[:], identb[:])
@@ -91,8 +101,8 @@ def tile_joint_kernel(tc, h_pred, h_enc, W1, b1, W2, b2, out):
         nc.vector.tensor_copy(out=b1T[:], in_=bps[:, 0:8])
         b2T = const.tile([P, 16], BF16, name="b2T")
         nc.vector.tensor_copy(out=b2T[:], in_=bps[:, 8:24])
-        b2bc = const.tile([P, V], BF16, name="b2bc")
-        for vb in range(4):
+        b2bc = const.tile([P, 1536], BF16, name="b2bc")
+        for vb in range(3):
             b2ps = psum.tile([P, 4, P], F32, name="b2ps", tag="bank")
             for a in range(4):
                 nc.tensor.matmul(
@@ -107,25 +117,32 @@ def tile_joint_kernel(tc, h_pred, h_enc, W1, b1, W2, b2, out):
 
         w1_q = const.tile([P, 2, J], U32, name="w1_q", align_bytes=64)
         w1_s = const.tile([P, 2, J], U8, name="w1_s", align_bytes=64)
-        grp1 = []
-        for half in range(2):
-            grp1.append(grpp.tile([P, J, 4], BF16, name="grp1_%d" % half, tag="grp", align_bytes=64))
+        grp1 = {}
 
-        def regroup_w1(eng_copy, half, c0, c1):
-            eng_copy(
-                out=grp1[half][:, c0:c1, :].rearrange("p (c i) t -> p c t i", i=4),
-                in_=raw1[half][:, :, c0:c1].rearrange("p t (c i) -> p c t i", i=4),
+        def regroup_w1(half, cc):
+            grp = grp1p.tile([P, 512, 4], BF16, name="grp1_%d%d" % (half, cc), tag="grp1", align_bytes=64)
+            grp1[(half, cc)] = grp
+            raw = raw1[(half, cc)]
+            nc.vector.tensor_copy(
+                out=grp[:, 0:SPLIT1, :].rearrange("p (c i) t -> p c t i", i=4),
+                in_=raw[:, :, 0:SPLIT1].rearrange("p t (c i) -> p c t i", i=4),
+            )
+            nc.scalar.copy(
+                out=grp[:, SPLIT1:512, :].rearrange("p (c i) t -> p c t i", i=4),
+                in_=raw[:, :, SPLIT1:512].rearrange("p t (c i) -> p c t i", i=4),
             )
 
-        def quant_w1(half):
+        def quant_w1(half, cc):
             nc.vector.quantize_mx(
-                out=w1_q[:, half, :].bitcast(FP8X4),
-                scales=w1_s[:, half, :],
-                in_=grp1[half][:].rearrange("p c t -> p (c t)"),
+                out=w1_q[:, half, cc * 512 : (cc + 1) * 512].bitcast(FP8X4),
+                scales=w1_s[:, half, cc * 512 : (cc + 1) * 512],
+                in_=grp1[(half, cc)][:].rearrange("p c t -> p (c t)"),
             )
 
-        regroup_w1(nc.vector.tensor_copy, 0, 0, SPLIT1)
-        regroup_w1(nc.scalar.copy, 0, SPLIT1, J)
+        regroup_w1(0, 0)
+        regroup_w1(0, 1)
+        quant_w1(0, 0)
+        quant_w1(0, 1)
 
         hpT = psum.tile([P, 2, P], F32, name="hpT", tag="bank")
         for u in range(2):
@@ -148,6 +165,7 @@ def tile_joint_kernel(tc, h_pred, h_enc, W1, b1, W2, b2, out):
         hp_s = const.tile([P, P], U8, name="hp_s", align_bytes=64)
         he_q = const.tile([P, 2 * P], U32, name="he_q", align_bytes=64)
         he_s = const.tile([P, 2 * P], U8, name="he_s", align_bytes=64)
+        regroup_w1(1, 0)
         nc.vector.quantize_mx(
             out=hp_q[:].bitcast(FP8X4),
             scales=hp_s[:],
@@ -158,10 +176,9 @@ def tile_joint_kernel(tc, h_pred, h_enc, W1, b1, W2, b2, out):
             scales=he_s[:],
             in_=he_g[:].rearrange("p a r u -> p (a r u)").bitcast(BF16),
         )
-        quant_w1(0)
-        regroup_w1(nc.vector.tensor_copy, 1, 0, SPLIT1)
-        regroup_w1(nc.scalar.copy, 1, SPLIT1, J)
-        quant_w1(1)
+        regroup_w1(1, 1)
+        quant_w1(1, 0)
+        quant_w1(1, 1)
 
         w2_q = const.tile([P, 4, 2, 512], U32, name="w2_q", align_bytes=64)
         w2_s = const.tile([P, 4, 2, 512], U8, name="w2_s", align_bytes=64)
@@ -169,8 +186,8 @@ def tile_joint_kernel(tc, h_pred, h_enc, W1, b1, W2, b2, out):
 
         def regroup_w2(eng_copy, vb, c, v0, v1):
             if vb not in grp2:
-                grp2[vb] = grpp.tile(
-                    [P, 2, 512, 4], BF16, name="grp2_%d" % vb, tag="grp", align_bytes=64
+                grp2[vb] = grp2p.tile(
+                    [P, 2, 512, 4], BF16, name="grp2_%d" % vb, tag="grp2", align_bytes=64
                 )
             eng_copy(
                 out=grp2[vb][:, c, v0:v1, :].rearrange("p (v i) t -> p v t i", i=4),
@@ -208,8 +225,8 @@ def tile_joint_kernel(tc, h_pred, h_enc, W1, b1, W2, b2, out):
                 )
             return bank
 
-        def evac_enc(eng_copy, bank, c, blk):
-            eng_copy(
+        def evac_enc(bank, c, blk):
+            nc.scalar.copy(
                 out=encs[:, c, (blk - 1) * P : blk * P, :],
                 in_=bank[:].rearrange("p t r -> p r t"),
             )
@@ -222,16 +239,15 @@ def tile_joint_kernel(tc, h_pred, h_enc, W1, b1, W2, b2, out):
                 in1=b1T[:, 4 * c : 4 * c + 4].unsqueeze(1).to_broadcast([P, P, 4]),
                 op=ALU.add,
             )
-        regroup_w2(nc.scalar.copy, 0, 1, 0, 256)
+        regroup_w2(nc.scalar.copy, 3, 1, 0, 256)
         eb = [stage1(0, 1), stage1(1, 1)]
-        evac_enc(nc.scalar.copy, eb[0], 0, 1)
-        evac_enc(nc.scalar.copy, eb[1], 1, 1)
+        evac_enc(eb[0], 0, 1)
+        evac_enc(eb[1], 1, 1)
         eb2 = [stage1(0, 2), stage1(1, 2)]
-        evac_enc(nc.vector.tensor_copy, eb2[0], 0, 2)
-        evac_enc(nc.vector.tensor_copy, eb2[1], 1, 2)
 
         z_t, x_t, xq_t, bank_t, y_t, negm_t, ssum_t, chain_t, negk_t = {}, {}, {}, {}, {}, {}, {}, {}, {}
         lt_t, yt_t, yfull_t = {}, {}, {}
+        done = set()
 
         def zadd(n):
             z = zp.tile([P, 2, P, 4], F32, name="z", tag="z")
@@ -310,7 +326,10 @@ def tile_joint_kernel(tc, h_pred, h_enc, W1, b1, W2, b2, out):
                 nc.tensor.transpose(bank[:, a, :], yt_t[n][:, a, :], identf[:])
 
         def add_b2(n, vb):
-            if vb == 0:
+            if (n, vb) in done:
+                return
+            done.add((n, vb))
+            if n not in y_t:
                 yfull_t[n] = yp.tile([P, Y0 + V], F32, name="y", tag="y")
                 y_t[n] = yfull_t[n][:, Y0 : Y0 + V]
             if vb < 3:
@@ -399,60 +418,91 @@ def tile_joint_kernel(tc, h_pred, h_enc, W1, b1, W2, b2, out):
             nc.sync.dma_start(out=out_rows[n * P : (n + 1) * P, :], in_=y_t[n])
 
         zadd(0)
-        regroup_w2(nc.vector.tensor_copy, 0, 0, 0, 512)
-        regroup_w2(nc.scalar.copy, 0, 1, 256, 512)
-        quant_w2(0)
+        regroup_w2(nc.vector.tensor_copy, 3, 0, 0, 512)
+        regroup_w2(nc.scalar.copy, 3, 1, 256, 512)
         zadd(1)
         tanh(0, 0)
+        quant_w2(3)
         tanh(0, 1)
         quant_x(0)
-        mm(0, 0)
-        regroup_w2(nc.vector.tensor_copy, 1, 0, 0, 512)
-        regroup_w2(nc.scalar.copy, 1, 1, 0, 256)
-        regroup_w2(nc.scalar.copy, 1, 1, 256, 512)
-        add_b2(0, 0)
-        quant_w2(1)
-        mm(0, 1)
+        mm_t(0)
+        regroup_w2(nc.scalar.copy, 0, 1, 0, 256)
+        evac_enc(eb2[0], 0, 2)
+        bias_t(0)
+        back_t(0)
+        regroup_w2(nc.vector.tensor_copy, 0, 0, 0, 512)
+        regroup_w2(nc.scalar.copy, 0, 1, 256, 512)
+        evac_enc(eb2[1], 1, 2)
         zadd(2)
         tanh(1, 0)
         tanh(1, 1)
-        regroup_w2(nc.vector.tensor_copy, 2, 0, 0, 512)
-        regroup_w2(nc.scalar.copy, 2, 1, 0, 256)
-        regroup_w2(nc.scalar.copy, 2, 1, 256, 512)
+        quant_w2(0)
+        mm(0, 0)
         quant_x(1)
-        mm(1, 0)
-        mm(1, 1)
-        add_b2(0, 1)
-        quant_w2(2)
-        mm(0, 2)
-        mm(1, 2)
-        zadd(3)
-        tanh(2, 0)
-        tanh(2, 1)
-        regroup_w2(nc.vector.tensor_copy, 3, 0, 0, 512)
-        regroup_w2(nc.scalar.copy, 3, 1, 0, 256)
-        regroup_w2(nc.scalar.copy, 3, 1, 256, 512)
-        add_b2(0, 2)
-        quant_w2(3)
-        mm_t(0)
-        bias_t(0)
-        back_t(0)
         mm_t(1)
+        mm(1, 0)
         bias_t(1)
         back_t(1)
         add_b2(0, 3)
+        add_b2(0, 0)
+        regroup_w2(nc.vector.tensor_copy, 1, 0, 0, 512)
+        regroup_w2(nc.scalar.copy, 1, 1, 0, 256)
+        regroup_w2(nc.scalar.copy, 1, 1, 256, 512)
+        zadd(3)
+        tanh(2, 0)
+        tanh(2, 1)
+        add_b2(1, 3)
+        add_b2(1, 0)
+        quant_w2(1)
+        mm(0, 1)
+        mm(1, 1)
+        regroup_w2(nc.vector.tensor_copy, 2, 0, 0, 512)
+        regroup_w2(nc.scalar.copy, 2, 1, 0, 256)
+        regroup_w2(nc.scalar.copy, 2, 1, 256, 512)
+        zadd(4)
+        tanh(3, 0)
+        tanh(3, 1)
+        add_b2(0, 1)
+        add_b2(1, 1)
+        quant_w2(2)
+        mm(0, 2)
+        mm(1, 2)
+        add_b2(0, 2)
         row_max(0)
 
-        for s in range(1, N_B + 5):
-            d = s - 4
-            if 0 <= d < 12:
-                sub_gps(d, 0, D_GPS)
-            elif 12 <= d < 15:
-                sub_gps(d, 1024, V)
-            elif d == 15:
-                sub_gps(d, 1024, 1536)
-            if s + 3 < N_B:
-                zadd(s + 3)
+        last_step = 2 * NEWTON + 2
+        nxt = {}
+        ready = []
+        count = {"subtracted": 0}
+
+        def advance(n):
+            if n < 0 or n >= N_B or n not in ssum_t:
+                return
+            k = nxt.get(n, 1)
+            if k > last_step:
+                return
+            step(n, k)
+            nxt[n] = k + 1
+            if k == last_step:
+                ready.append(n)
+
+        for s in range(1, N_B + D_LAG + 1):
+            dense = s >= DENSE_FROM
+            todo = []
+            while count["subtracted"] < len(ready) and (
+                dense or ready[count["subtracted"]] <= s - D_LAG
+            ):
+                todo.append(ready[count["subtracted"]])
+                count["subtracted"] += 1
+            for d in todo:
+                if d < 14:
+                    sub_gps(d, 0, D_GPS)
+                elif d == 14:
+                    sub_gps(d, 1024, V)
+                else:
+                    sub_gps(d, 1024, 1536)
+            if s + 4 < N_B:
+                zadd(s + 4)
             if s + 1 < N_B:
                 quant_x(s + 1)
                 mm_t(s + 1)
@@ -462,30 +512,40 @@ def tile_joint_kernel(tc, h_pred, h_enc, W1, b1, W2, b2, out):
                 for vb in range(4):
                     add_b2(s, vb)
                 row_max(s)
-            if 12 <= d < N_B:
-                sub_vec(d, 0, 1024)
+            for d in todo:
+                if d >= 14:
+                    sub_vec(d, 0, 1024)
             if s - 1 < N_B:
                 exp_sum(s - 1)
-            step(s - 2, 4)
-            step(s - 3, 8)
+            advance(s - 3)
+            advance(s - 2)
             if s + 1 < N_B:
                 bias_t(s + 1)
                 back_t(s + 1)
-            if s + 2 < N_B:
-                tanh(s + 2, 0)
-            step(s - 1, 1)
-            step(s - 2, 5)
-            step(s - 3, 9)
-            if s + 2 < N_B:
-                tanh(s + 2, 1)
-            step(s - 1, 2)
-            step(s - 2, 6)
-            step(s - 3, 10)
-            if 0 <= d < 12 and D_GPS < V:
-                sub_act(d, D_GPS, V)
-            elif d == 15:
-                sub_act(d, 1536, V)
-            step(s - 1, 3)
-            step(s - 2, 7)
-            if 0 <= d < N_B:
+            if dense:
+                for i in range(6 if s + 1 < N_B else last_step):
+                    advance(s - 3)
+                    advance(s - 2)
+                    advance(s - 1)
+            if s + 3 < N_B:
+                tanh(s + 3, 0)
+            if not dense:
+                advance(s - 3)
+                advance(s - 2)
+                advance(s - 1)
+            if s + 3 < N_B:
+                tanh(s + 3, 1)
+            if not dense:
+                advance(s - 3)
+                advance(s - 2)
+                advance(s - 1)
+            for d in todo:
+                if d < 14 and D_GPS < V:
+                    sub_act(d, D_GPS, V)
+                elif d == 15:
+                    sub_act(d, 1536, V)
+            if not dense:
+                advance(s - 2)
+                advance(s - 1)
+            for d in todo:
                 store(d)

@@ -19,12 +19,10 @@ N_B, T_E, U_P, H, J, V = 16, 16, 8, 512, 1024, 2048
 FLOPS = 2 * (N_B * U_P * H * J + N_B * T_E * H * J + N_B * T_E * U_P * J * V)
 LN2 = math.log(2.0)
 NEWTON = 4
-SPLIT1 = 320
+SPLIT1 = 640
 Y0 = 8
-D_GPS = 1792
-D_LAG = 5
-W2_ORDER = (3, 0, 1, 2)
-DENSE_FROM = 13
+D_GPS = 2048
+LN_TILES = 12
 
 
 def tile_joint_kernel(tc, h_pred, h_enc, W1, b1, W2, b2, out):
@@ -32,17 +30,16 @@ def tile_joint_kernel(tc, h_pred, h_enc, W1, b1, W2, b2, out):
     out_rows = out.rearrange("n t u v -> (n t u) v")
     with ExitStack() as ctx:
         const = ctx.enter_context(tc.tile_pool(name="const", bufs=1))
-        raw1p = ctx.enter_context(tc.tile_pool(name="raw1p", bufs=4))
-        raw2p = ctx.enter_context(tc.tile_pool(name="raw2p", bufs=4))
-        grp1p = ctx.enter_context(tc.tile_pool(name="grp1p", bufs=2))
-        grp2p = ctx.enter_context(tc.tile_pool(name="grp2p", bufs=3))
+        rawp = ctx.enter_context(tc.tile_pool(name="rawp", bufs=6))
+        grpp = ctx.enter_context(tc.tile_pool(name="grpp", bufs=3))
         zp = ctx.enter_context(tc.tile_pool(name="zp", bufs=3))
-        xp = ctx.enter_context(tc.tile_pool(name="xp", bufs=4))
+        xp = ctx.enter_context(tc.tile_pool(name="xp", bufs=3))
         xqp = ctx.enter_context(tc.tile_pool(name="xqp", bufs=4))
         yp = ctx.enter_context(tc.tile_pool(name="yp", bufs=7))
         jp = ctx.enter_context(tc.tile_pool(name="jp", bufs=2))
         ytp = ctx.enter_context(tc.tile_pool(name="ytp", bufs=2))
         st = ctx.enter_context(tc.tile_pool(name="st", bufs=8))
+        st4 = ctx.enter_context(tc.tile_pool(name="st4", bufs=3))
         psum = ctx.enter_context(tc.psum_pool(name="psum", bufs=8))
         ctx.enter_context(tc.manual_schedule())
 
@@ -61,22 +58,18 @@ def tile_joint_kernel(tc, h_pred, h_enc, W1, b1, W2, b2, out):
         identb = const.tile([P, P], BF16, name="identb")
         make_identity(nc, identb[:])
 
-        raw1 = {}
 
-        def load_w1(half, cc):
-            raw = raw1p.tile([P, 4, 512], BF16, name="raw1_%d%d" % (half, cc), tag="raw1")
-            raw1[(half, cc)] = raw
-            for u in range(2):
-                r0 = half * H + u * 256
-                nc.sync.dma_start(
-                    out=raw[:, 2 * u : 2 * u + 2, :],
-                    in_=W1[r0 : r0 + 256, cc * 512 : (cc + 1) * 512].rearrange(
-                        "(q e) c -> q e c", e=2
-                    ),
-                )
+        def load_w1(half):
+            raw = rawp.tile([P, 4, J], BF16, name="raw1_%d" % half, tag="raw")
+            nc.sync.dma_start(
+                out=raw[:].rearrange("p (u e) c -> p u (e c)", u=2),
+                in_=W1[half * H : (half + 1) * H, :].rearrange(
+                    "(u q e) c -> q u (e c)", u=2, q=P, e=2
+                ),
+            )
+            return raw
 
-        load_w1(0, 0)
-        load_w1(0, 1)
+        raw1 = [load_w1(0)]
         hp_sb = const.tile([P, H], BF16, name="hp_sb")
         nc.sync.dma_start(out=hp_sb[:], in_=h_pred.rearrange("n u h -> (n u) h"))
         he_sb = const.tile([P, 2, H], BF16, name="he_sb")
@@ -84,16 +77,15 @@ def tile_joint_kernel(tc, h_pred, h_enc, W1, b1, W2, b2, out):
             out=he_sb[:],
             in_=h_enc.rearrange("n t h -> (n t) h").rearrange("(a p) h -> p a h", p=P),
         )
-        load_w1(1, 0)
-        load_w1(1, 1)
-        raw2 = {}
-        for vb in W2_ORDER:
-            raw = raw2p.tile([P, 8, 512], BF16, name="raw2_%d" % vb, tag="raw2")
-            raw2[vb] = raw
+        raw1.append(load_w1(1))
+        raw2 = []
+        for vb in range(4):
+            raw = rawp.tile([P, 8, 512], BF16, name="raw2_%d" % vb, tag="raw")
             nc.sync.dma_start(
                 out=raw[:],
                 in_=W2[:, vb * 512 : (vb + 1) * 512].rearrange("(g p) v -> p g v", p=P),
             )
+            raw2.append(raw)
 
         bps = psum.tile([P, P], BF16, name="bps", tag="bank")
         nc.tensor.transpose(bps[:], brows[:], identb[:])
@@ -101,8 +93,8 @@ def tile_joint_kernel(tc, h_pred, h_enc, W1, b1, W2, b2, out):
         nc.vector.tensor_copy(out=b1T[:], in_=bps[:, 0:8])
         b2T = const.tile([P, 16], BF16, name="b2T")
         nc.vector.tensor_copy(out=b2T[:], in_=bps[:, 8:24])
-        b2bc = const.tile([P, 1536], BF16, name="b2bc")
-        for vb in range(3):
+        b2bc = const.tile([P, V], BF16, name="b2bc")
+        for vb in range(4):
             b2ps = psum.tile([P, 4, P], F32, name="b2ps", tag="bank")
             for a in range(4):
                 nc.tensor.matmul(
@@ -117,32 +109,25 @@ def tile_joint_kernel(tc, h_pred, h_enc, W1, b1, W2, b2, out):
 
         w1_q = const.tile([P, 2, J], U32, name="w1_q", align_bytes=64)
         w1_s = const.tile([P, 2, J], U8, name="w1_s", align_bytes=64)
-        grp1 = {}
+        grp1 = []
+        for half in range(2):
+            grp1.append(grpp.tile([P, J, 4], BF16, name="grp1_%d" % half, tag="grp", align_bytes=64))
 
-        def regroup_w1(half, cc):
-            grp = grp1p.tile([P, 512, 4], BF16, name="grp1_%d%d" % (half, cc), tag="grp1", align_bytes=64)
-            grp1[(half, cc)] = grp
-            raw = raw1[(half, cc)]
-            nc.vector.tensor_copy(
-                out=grp[:, 0:SPLIT1, :].rearrange("p (c i) t -> p c t i", i=4),
-                in_=raw[:, :, 0:SPLIT1].rearrange("p t (c i) -> p c t i", i=4),
-            )
-            nc.scalar.copy(
-                out=grp[:, SPLIT1:512, :].rearrange("p (c i) t -> p c t i", i=4),
-                in_=raw[:, :, SPLIT1:512].rearrange("p t (c i) -> p c t i", i=4),
+        def regroup_w1(eng_copy, half, c0, c1):
+            eng_copy(
+                out=grp1[half][:, c0:c1, :].rearrange("p (c i) t -> p c t i", i=4),
+                in_=raw1[half][:, :, c0:c1].rearrange("p t (c i) -> p c t i", i=4),
             )
 
-        def quant_w1(half, cc):
+        def quant_w1(half):
             nc.vector.quantize_mx(
-                out=w1_q[:, half, cc * 512 : (cc + 1) * 512].bitcast(FP8X4),
-                scales=w1_s[:, half, cc * 512 : (cc + 1) * 512],
-                in_=grp1[(half, cc)][:].rearrange("p c t -> p (c t)"),
+                out=w1_q[:, half, :].bitcast(FP8X4),
+                scales=w1_s[:, half, :],
+                in_=grp1[half][:].rearrange("p c t -> p (c t)"),
             )
 
-        regroup_w1(0, 0)
-        regroup_w1(0, 1)
-        quant_w1(0, 0)
-        quant_w1(0, 1)
+        regroup_w1(nc.vector.tensor_copy, 0, 0, SPLIT1)
+        regroup_w1(nc.scalar.copy, 0, SPLIT1, J)
 
         hpT = psum.tile([P, 2, P], F32, name="hpT", tag="bank")
         for u in range(2):
@@ -165,7 +150,6 @@ def tile_joint_kernel(tc, h_pred, h_enc, W1, b1, W2, b2, out):
         hp_s = const.tile([P, P], U8, name="hp_s", align_bytes=64)
         he_q = const.tile([P, 2 * P], U32, name="he_q", align_bytes=64)
         he_s = const.tile([P, 2 * P], U8, name="he_s", align_bytes=64)
-        regroup_w1(1, 0)
         nc.vector.quantize_mx(
             out=hp_q[:].bitcast(FP8X4),
             scales=hp_s[:],
@@ -176,9 +160,10 @@ def tile_joint_kernel(tc, h_pred, h_enc, W1, b1, W2, b2, out):
             scales=he_s[:],
             in_=he_g[:].rearrange("p a r u -> p (a r u)").bitcast(BF16),
         )
-        regroup_w1(1, 1)
-        quant_w1(1, 0)
-        quant_w1(1, 1)
+        quant_w1(0)
+        regroup_w1(nc.vector.tensor_copy, 1, 0, SPLIT1)
+        regroup_w1(nc.scalar.copy, 1, SPLIT1, J)
+        quant_w1(1)
 
         w2_q = const.tile([P, 4, 2, 512], U32, name="w2_q", align_bytes=64)
         w2_s = const.tile([P, 4, 2, 512], U8, name="w2_s", align_bytes=64)
@@ -186,8 +171,8 @@ def tile_joint_kernel(tc, h_pred, h_enc, W1, b1, W2, b2, out):
 
         def regroup_w2(eng_copy, vb, c, v0, v1):
             if vb not in grp2:
-                grp2[vb] = grp2p.tile(
-                    [P, 2, 512, 4], BF16, name="grp2_%d" % vb, tag="grp2", align_bytes=64
+                grp2[vb] = grpp.tile(
+                    [P, 2, 512, 4], BF16, name="grp2_%d" % vb, tag="grp", align_bytes=64
                 )
             eng_copy(
                 out=grp2[vb][:, c, v0:v1, :].rearrange("p (v i) t -> p v t i", i=4),
@@ -225,8 +210,8 @@ def tile_joint_kernel(tc, h_pred, h_enc, W1, b1, W2, b2, out):
                 )
             return bank
 
-        def evac_enc(bank, c, blk):
-            nc.scalar.copy(
+        def evac_enc(eng_copy, bank, c, blk):
+            eng_copy(
                 out=encs[:, c, (blk - 1) * P : blk * P, :],
                 in_=bank[:].rearrange("p t r -> p r t"),
             )
@@ -239,15 +224,16 @@ def tile_joint_kernel(tc, h_pred, h_enc, W1, b1, W2, b2, out):
                 in1=b1T[:, 4 * c : 4 * c + 4].unsqueeze(1).to_broadcast([P, P, 4]),
                 op=ALU.add,
             )
-        regroup_w2(nc.scalar.copy, 3, 1, 0, 256)
+        regroup_w2(nc.scalar.copy, 0, 1, 0, 256)
         eb = [stage1(0, 1), stage1(1, 1)]
-        evac_enc(eb[0], 0, 1)
-        evac_enc(eb[1], 1, 1)
+        evac_enc(nc.scalar.copy, eb[0], 0, 1)
+        evac_enc(nc.scalar.copy, eb[1], 1, 1)
         eb2 = [stage1(0, 2), stage1(1, 2)]
+        evac_enc(nc.vector.tensor_copy, eb2[0], 0, 2)
+        evac_enc(nc.vector.tensor_copy, eb2[1], 1, 2)
 
         z_t, x_t, xq_t, bank_t, y_t, negm_t, ssum_t, chain_t, negk_t = {}, {}, {}, {}, {}, {}, {}, {}, {}
-        lt_t, yt_t, yfull_t = {}, {}, {}
-        done = set()
+        lt_t, yt_t, yfull_t, grp_t = {}, {}, {}, {}
 
         def zadd(n):
             z = zp.tile([P, 2, P, 4], F32, name="z", tag="z")
@@ -326,10 +312,7 @@ def tile_joint_kernel(tc, h_pred, h_enc, W1, b1, W2, b2, out):
                 nc.tensor.transpose(bank[:, a, :], yt_t[n][:, a, :], identf[:])
 
         def add_b2(n, vb):
-            if (n, vb) in done:
-                return
-            done.add((n, vb))
-            if n not in y_t:
+            if vb == 0:
                 yfull_t[n] = yp.tile([P, Y0 + V], F32, name="y", tag="y")
                 y_t[n] = yfull_t[n][:, Y0 : Y0 + V]
             if vb < 3:
@@ -348,15 +331,33 @@ def tile_joint_kernel(tc, h_pred, h_enc, W1, b1, W2, b2, out):
                 )
 
         def row_max(n):
-            negm = st.tile([P, 1], F32, name="negm", tag="negm")
+            if n < LN_TILES:
+                if n % 4 == 0:
+                    negm4 = st4.tile([P, 4], F32, name="negm4", tag="negm4")
+                    ssum4 = st4.tile([P, 4], F32, name="ssum4", tag="ssum4")
+                    grp_t[n // 4] = (negm4, ssum4)
+                negm = grp_t[n // 4][0][:, n % 4 : n % 4 + 1]
+            else:
+                negm = st.tile([P, 1], F32, name="negm", tag="negm")
             negm_t[n] = negm
             nc.vector.tensor_reduce(
-                out=negm[:], in_=yfull_t[n][:, Y0 - 1 : Y0 + 1536], axis=AX.X, op=ALU.max, negate=True
+                out=negm, in_=yfull_t[n][:, Y0 - 1 : Y0 + 1536], axis=AX.X, op=ALU.max, negate=True
             )
+
+        def ln_group(b):
+            lns4 = st4.tile([P, 4], F32, name="lns4", tag="lns4")
+            nc.scalar.activation(out=lns4[:], in_=grp_t[b][1][:], func=ACT.Ln)
+            negk4 = st4.tile([P, 4], F32, name="negk4", tag="negk4")
+            nc.vector.tensor_tensor(out=negk4[:], in0=grp_t[b][0][:], in1=lns4[:], op=ALU.subtract)
+            for i in range(4):
+                negk_t[4 * b + i] = negk4[:, i : i + 1]
 
         def exp_sum(n):
             junk = jp.tile([P, V], BF16, name="junk", tag="junk")
-            ssum = st.tile([P, 1], F32, name="ssum", tag="ssum")
+            if n < LN_TILES:
+                ssum = grp_t[n // 4][1][:, n % 4 : n % 4 + 1]
+            else:
+                ssum = st.tile([P, 1], F32, name="ssum", tag="ssum")
             ssum_t[n] = ssum
             nc.scalar.activation(
                 out=junk[:], in_=y_t[n], func=ACT.Exp, bias=negm_t[n][:, 0:1], scale=1.0,
@@ -364,7 +365,7 @@ def tile_joint_kernel(tc, h_pred, h_enc, W1, b1, W2, b2, out):
             )
 
         def step(n, k):
-            if n < 0 or n >= N_B:
+            if n < LN_TILES or n >= N_B:
                 return
             if k == 1:
                 r = st.tile([P, 1], F32, name="nr", tag="nr")
@@ -418,91 +419,65 @@ def tile_joint_kernel(tc, h_pred, h_enc, W1, b1, W2, b2, out):
             nc.sync.dma_start(out=out_rows[n * P : (n + 1) * P, :], in_=y_t[n])
 
         zadd(0)
-        regroup_w2(nc.vector.tensor_copy, 3, 0, 0, 512)
-        regroup_w2(nc.scalar.copy, 3, 1, 256, 512)
-        zadd(1)
-        tanh(0, 0)
-        quant_w2(3)
-        tanh(0, 1)
-        quant_x(0)
-        mm_t(0)
-        regroup_w2(nc.scalar.copy, 0, 1, 0, 256)
-        evac_enc(eb2[0], 0, 2)
-        bias_t(0)
-        back_t(0)
         regroup_w2(nc.vector.tensor_copy, 0, 0, 0, 512)
         regroup_w2(nc.scalar.copy, 0, 1, 256, 512)
-        evac_enc(eb2[1], 1, 2)
-        zadd(2)
-        tanh(1, 0)
-        tanh(1, 1)
         quant_w2(0)
+        zadd(1)
+        tanh(0, 0)
+        tanh(0, 1)
+        quant_x(0)
         mm(0, 0)
-        quant_x(1)
-        mm_t(1)
-        mm(1, 0)
-        bias_t(1)
-        back_t(1)
-        add_b2(0, 3)
-        add_b2(0, 0)
         regroup_w2(nc.vector.tensor_copy, 1, 0, 0, 512)
         regroup_w2(nc.scalar.copy, 1, 1, 0, 256)
         regroup_w2(nc.scalar.copy, 1, 1, 256, 512)
-        zadd(3)
-        tanh(2, 0)
-        tanh(2, 1)
-        add_b2(1, 3)
-        add_b2(1, 0)
+        add_b2(0, 0)
         quant_w2(1)
         mm(0, 1)
-        mm(1, 1)
+        zadd(2)
+        tanh(1, 0)
+        tanh(1, 1)
         regroup_w2(nc.vector.tensor_copy, 2, 0, 0, 512)
         regroup_w2(nc.scalar.copy, 2, 1, 0, 256)
         regroup_w2(nc.scalar.copy, 2, 1, 256, 512)
-        zadd(4)
-        tanh(3, 0)
-        tanh(3, 1)
+        quant_x(1)
+        mm(1, 0)
+        mm(1, 1)
         add_b2(0, 1)
-        add_b2(1, 1)
         quant_w2(2)
         mm(0, 2)
         mm(1, 2)
+        zadd(3)
+        tanh(2, 0)
+        tanh(2, 1)
+        regroup_w2(nc.vector.tensor_copy, 3, 0, 0, 512)
+        regroup_w2(nc.scalar.copy, 3, 1, 0, 256)
+        regroup_w2(nc.scalar.copy, 3, 1, 256, 512)
         add_b2(0, 2)
+        quant_w2(3)
+        mm_t(0)
+        bias_t(0)
+        back_t(0)
+        mm_t(1)
+        bias_t(1)
+        back_t(1)
+        add_b2(0, 3)
         row_max(0)
 
-        last_step = 2 * NEWTON + 2
-        nxt = {}
-        ready = []
-        count = {"subtracted": 0}
-
-        def advance(n):
-            if n < 0 or n >= N_B or n not in ssum_t:
-                return
-            k = nxt.get(n, 1)
-            if k > last_step:
-                return
-            step(n, k)
-            nxt[n] = k + 1
-            if k == last_step:
-                ready.append(n)
-
-        for s in range(1, N_B + D_LAG + 1):
-            dense = s >= DENSE_FROM
+        for s in range(1, N_B + 5):
             todo = []
-            while count["subtracted"] < len(ready) and (
-                dense or ready[count["subtracted"]] <= s - D_LAG
-            ):
-                todo.append(ready[count["subtracted"]])
-                count["subtracted"] += 1
+            if 0 <= s - 5 < LN_TILES:
+                todo.append(s - 5)
+            if LN_TILES <= s - 4 < N_B:
+                todo.append(s - 4)
             for d in todo:
-                if d < 14:
-                    sub_gps(d, 0, D_GPS)
-                elif d == 14:
+                if d < 12:
+                    sub_gps(d, 0, V)
+                elif d < 15:
                     sub_gps(d, 1024, V)
                 else:
                     sub_gps(d, 1024, 1536)
-            if s + 4 < N_B:
-                zadd(s + 4)
+            if s + 3 < N_B:
+                zadd(s + 3)
             if s + 1 < N_B:
                 quant_x(s + 1)
                 mm_t(s + 1)
@@ -513,39 +488,31 @@ def tile_joint_kernel(tc, h_pred, h_enc, W1, b1, W2, b2, out):
                     add_b2(s, vb)
                 row_max(s)
             for d in todo:
-                if d >= 14:
+                if d >= 12:
                     sub_vec(d, 0, 1024)
             if s - 1 < N_B:
                 exp_sum(s - 1)
-            advance(s - 3)
-            advance(s - 2)
+            if s - 1 < LN_TILES and (s - 1) % 4 == 3:
+                ln_group((s - 1) // 4)
+            step(s - 2, 4)
+            step(s - 3, 8)
             if s + 1 < N_B:
                 bias_t(s + 1)
                 back_t(s + 1)
-            if dense:
-                for i in range(6 if s + 1 < N_B else last_step):
-                    advance(s - 3)
-                    advance(s - 2)
-                    advance(s - 1)
-            if s + 3 < N_B:
-                tanh(s + 3, 0)
-            if not dense:
-                advance(s - 3)
-                advance(s - 2)
-                advance(s - 1)
-            if s + 3 < N_B:
-                tanh(s + 3, 1)
-            if not dense:
-                advance(s - 3)
-                advance(s - 2)
-                advance(s - 1)
+            if s + 2 < N_B:
+                tanh(s + 2, 0)
+            step(s - 1, 1)
+            step(s - 2, 5)
+            step(s - 3, 9)
+            if s + 2 < N_B:
+                tanh(s + 2, 1)
+            step(s - 1, 2)
+            step(s - 2, 6)
+            step(s - 3, 10)
             for d in todo:
-                if d < 14 and D_GPS < V:
-                    sub_act(d, D_GPS, V)
-                elif d == 15:
+                if d == 15:
                     sub_act(d, 1536, V)
-            if not dense:
-                advance(s - 2)
-                advance(s - 1)
+            step(s - 1, 3)
+            step(s - 2, 7)
             for d in todo:
                 store(d)

@@ -22,7 +22,6 @@ NEWTON = 4
 SPLIT1 = 640
 Y0 = 8
 D_GPS = 2048
-LN_TILES = 12
 
 
 def tile_joint_kernel(tc, h_pred, h_enc, W1, b1, W2, b2, out):
@@ -33,13 +32,12 @@ def tile_joint_kernel(tc, h_pred, h_enc, W1, b1, W2, b2, out):
         rawp = ctx.enter_context(tc.tile_pool(name="rawp", bufs=6))
         grpp = ctx.enter_context(tc.tile_pool(name="grpp", bufs=3))
         zp = ctx.enter_context(tc.tile_pool(name="zp", bufs=3))
-        xp = ctx.enter_context(tc.tile_pool(name="xp", bufs=3))
+        xp = ctx.enter_context(tc.tile_pool(name="xp", bufs=4))
         xqp = ctx.enter_context(tc.tile_pool(name="xqp", bufs=4))
-        yp = ctx.enter_context(tc.tile_pool(name="yp", bufs=7))
+        yp = ctx.enter_context(tc.tile_pool(name="yp", bufs=6))
         jp = ctx.enter_context(tc.tile_pool(name="jp", bufs=2))
         ytp = ctx.enter_context(tc.tile_pool(name="ytp", bufs=2))
         st = ctx.enter_context(tc.tile_pool(name="st", bufs=8))
-        st4 = ctx.enter_context(tc.tile_pool(name="st4", bufs=3))
         psum = ctx.enter_context(tc.psum_pool(name="psum", bufs=8))
         ctx.enter_context(tc.manual_schedule())
 
@@ -233,7 +231,7 @@ def tile_joint_kernel(tc, h_pred, h_enc, W1, b1, W2, b2, out):
         evac_enc(nc.vector.tensor_copy, eb2[1], 1, 2)
 
         z_t, x_t, xq_t, bank_t, y_t, negm_t, ssum_t, chain_t, negk_t = {}, {}, {}, {}, {}, {}, {}, {}, {}
-        lt_t, yt_t, yfull_t, grp_t = {}, {}, {}, {}
+        lt_t, yt_t, yfull_t = {}, {}, {}
 
         def zadd(n):
             z = zp.tile([P, 2, P, 4], F32, name="z", tag="z")
@@ -331,33 +329,15 @@ def tile_joint_kernel(tc, h_pred, h_enc, W1, b1, W2, b2, out):
                 )
 
         def row_max(n):
-            if n < LN_TILES:
-                if n % 4 == 0:
-                    negm4 = st4.tile([P, 4], F32, name="negm4", tag="negm4")
-                    ssum4 = st4.tile([P, 4], F32, name="ssum4", tag="ssum4")
-                    grp_t[n // 4] = (negm4, ssum4)
-                negm = grp_t[n // 4][0][:, n % 4 : n % 4 + 1]
-            else:
-                negm = st.tile([P, 1], F32, name="negm", tag="negm")
+            negm = st.tile([P, 1], F32, name="negm", tag="negm")
             negm_t[n] = negm
             nc.vector.tensor_reduce(
-                out=negm, in_=yfull_t[n][:, Y0 - 1 : Y0 + 1536], axis=AX.X, op=ALU.max, negate=True
+                out=negm[:], in_=yfull_t[n][:, Y0 - 1 : Y0 + 1536], axis=AX.X, op=ALU.max, negate=True
             )
-
-        def ln_group(b):
-            lns4 = st4.tile([P, 4], F32, name="lns4", tag="lns4")
-            nc.scalar.activation(out=lns4[:], in_=grp_t[b][1][:], func=ACT.Ln)
-            negk4 = st4.tile([P, 4], F32, name="negk4", tag="negk4")
-            nc.vector.tensor_tensor(out=negk4[:], in0=grp_t[b][0][:], in1=lns4[:], op=ALU.subtract)
-            for i in range(4):
-                negk_t[4 * b + i] = negk4[:, i : i + 1]
 
         def exp_sum(n):
             junk = jp.tile([P, V], BF16, name="junk", tag="junk")
-            if n < LN_TILES:
-                ssum = grp_t[n // 4][1][:, n % 4 : n % 4 + 1]
-            else:
-                ssum = st.tile([P, 1], F32, name="ssum", tag="ssum")
+            ssum = st.tile([P, 1], F32, name="ssum", tag="ssum")
             ssum_t[n] = ssum
             nc.scalar.activation(
                 out=junk[:], in_=y_t[n], func=ACT.Exp, bias=negm_t[n][:, 0:1], scale=1.0,
@@ -365,7 +345,7 @@ def tile_joint_kernel(tc, h_pred, h_enc, W1, b1, W2, b2, out):
             )
 
         def step(n, k):
-            if n < LN_TILES or n >= N_B:
+            if n < 0 or n >= N_B:
                 return
             if k == 1:
                 r = st.tile([P, 1], F32, name="nr", tag="nr")
@@ -462,22 +442,20 @@ def tile_joint_kernel(tc, h_pred, h_enc, W1, b1, W2, b2, out):
         back_t(1)
         add_b2(0, 3)
         row_max(0)
+        zadd(4)
+        tanh(3, 0)
+        tanh(3, 1)
 
         for s in range(1, N_B + 5):
-            todo = []
-            if 0 <= s - 5 < LN_TILES:
-                todo.append(s - 5)
-            if LN_TILES <= s - 4 < N_B:
-                todo.append(s - 4)
-            for d in todo:
-                if d < 12:
-                    sub_gps(d, 0, V)
-                elif d < 15:
-                    sub_gps(d, 1024, V)
-                else:
-                    sub_gps(d, 1024, 1536)
-            if s + 3 < N_B:
-                zadd(s + 3)
+            d = s - 4
+            if s + 4 < N_B:
+                zadd(s + 4)
+            if 0 <= d < 12:
+                sub_gps(d, 0, D_GPS)
+            elif 12 <= d < 15:
+                sub_gps(d, 1024, V)
+            elif d == 15:
+                sub_gps(d, 1024, 1536)
             if s + 1 < N_B:
                 quant_x(s + 1)
                 mm_t(s + 1)
@@ -487,32 +465,30 @@ def tile_joint_kernel(tc, h_pred, h_enc, W1, b1, W2, b2, out):
                 for vb in range(4):
                     add_b2(s, vb)
                 row_max(s)
-            for d in todo:
-                if d >= 12:
-                    sub_vec(d, 0, 1024)
+            if 12 <= d < N_B:
+                sub_vec(d, 0, 1024)
             if s - 1 < N_B:
                 exp_sum(s - 1)
-            if s - 1 < LN_TILES and (s - 1) % 4 == 3:
-                ln_group((s - 1) // 4)
             step(s - 2, 4)
             step(s - 3, 8)
             if s + 1 < N_B:
                 bias_t(s + 1)
                 back_t(s + 1)
-            if s + 2 < N_B:
-                tanh(s + 2, 0)
+            if s + 3 < N_B:
+                tanh(s + 3, 0)
             step(s - 1, 1)
             step(s - 2, 5)
             step(s - 3, 9)
-            if s + 2 < N_B:
-                tanh(s + 2, 1)
+            if s + 3 < N_B:
+                tanh(s + 3, 1)
             step(s - 1, 2)
             step(s - 2, 6)
             step(s - 3, 10)
-            for d in todo:
-                if d == 15:
-                    sub_act(d, 1536, V)
+            if 0 <= d < 12 and D_GPS < V:
+                sub_act(d, D_GPS, V)
+            elif d == 15:
+                sub_act(d, 1536, V)
             step(s - 1, 3)
             step(s - 2, 7)
-            for d in todo:
+            if 0 <= d < N_B:
                 store(d)

@@ -22,6 +22,7 @@ NEWTON = 4
 SPLIT1 = 640
 Y0 = 8
 D_GPS = 2048
+PLAIN_TILES = (1, 4, 7, 10, 13)
 
 
 def tile_joint_kernel(tc, h_pred, h_enc, W1, b1, W2, b2, out):
@@ -32,9 +33,9 @@ def tile_joint_kernel(tc, h_pred, h_enc, W1, b1, W2, b2, out):
         rawp = ctx.enter_context(tc.tile_pool(name="rawp", bufs=6))
         grpp = ctx.enter_context(tc.tile_pool(name="grpp", bufs=3))
         zp = ctx.enter_context(tc.tile_pool(name="zp", bufs=3))
-        xp = ctx.enter_context(tc.tile_pool(name="xp", bufs=4))
+        xp = ctx.enter_context(tc.tile_pool(name="xp", bufs=3))
         xqp = ctx.enter_context(tc.tile_pool(name="xqp", bufs=4))
-        yp = ctx.enter_context(tc.tile_pool(name="yp", bufs=6))
+        yp = ctx.enter_context(tc.tile_pool(name="yp", bufs=8))
         jp = ctx.enter_context(tc.tile_pool(name="jp", bufs=2))
         ytp = ctx.enter_context(tc.tile_pool(name="ytp", bufs=2))
         st = ctx.enter_context(tc.tile_pool(name="st", bufs=8))
@@ -313,7 +314,7 @@ def tile_joint_kernel(tc, h_pred, h_enc, W1, b1, W2, b2, out):
             if vb == 0:
                 yfull_t[n] = yp.tile([P, Y0 + V], F32, name="y", tag="y")
                 y_t[n] = yfull_t[n][:, Y0 : Y0 + V]
-            if vb < 3:
+            if vb < 3 or n in PLAIN_TILES:
                 nc.vector.tensor_tensor(
                     out=y_t[n][:, vb * 512 : (vb + 1) * 512],
                     in0=bank_t[(n, vb)][:],
@@ -331,9 +332,13 @@ def tile_joint_kernel(tc, h_pred, h_enc, W1, b1, W2, b2, out):
         def row_max(n):
             negm = st.tile([P, 1], F32, name="negm", tag="negm")
             negm_t[n] = negm
-            nc.vector.tensor_reduce(
-                out=negm[:], in_=yfull_t[n][:, Y0 - 1 : Y0 + 1536], axis=AX.X, op=ALU.max, negate=True
-            )
+            if n in PLAIN_TILES:
+                nc.vector.tensor_reduce(out=negm[:], in_=y_t[n], axis=AX.X, op=ALU.max, negate=True)
+            else:
+                nc.vector.tensor_reduce(
+                    out=negm[:], in_=yfull_t[n][:, Y0 - 1 : Y0 + 1536], axis=AX.X, op=ALU.max,
+                    negate=True,
+                )
 
         def exp_sum(n):
             junk = jp.tile([P, V], BF16, name="junk", tag="junk")
@@ -437,30 +442,29 @@ def tile_joint_kernel(tc, h_pred, h_enc, W1, b1, W2, b2, out):
         mm_t(0)
         bias_t(0)
         back_t(0)
-        mm_t(1)
-        bias_t(1)
-        back_t(1)
+        mm(1, 3)
         add_b2(0, 3)
         row_max(0)
-        zadd(4)
-        tanh(3, 0)
-        tanh(3, 1)
 
         for s in range(1, N_B + 5):
             d = s - 4
-            if s + 4 < N_B:
-                zadd(s + 4)
             if 0 <= d < 12:
                 sub_gps(d, 0, D_GPS)
             elif 12 <= d < 15:
                 sub_gps(d, 1024, V)
             elif d == 15:
                 sub_gps(d, 1024, 1536)
+            if s + 3 < N_B:
+                zadd(s + 3)
             if s + 1 < N_B:
                 quant_x(s + 1)
-                mm_t(s + 1)
-                for vb in range(3):
-                    mm(s + 1, vb)
+                if s + 1 in PLAIN_TILES:
+                    for vb in range(4):
+                        mm(s + 1, vb)
+                else:
+                    mm_t(s + 1)
+                    for vb in range(3):
+                        mm(s + 1, vb)
             if s < N_B:
                 for vb in range(4):
                     add_b2(s, vb)
@@ -471,22 +475,20 @@ def tile_joint_kernel(tc, h_pred, h_enc, W1, b1, W2, b2, out):
                 exp_sum(s - 1)
             step(s - 2, 4)
             step(s - 3, 8)
-            if s + 1 < N_B:
+            if s + 1 < N_B and s + 1 not in PLAIN_TILES:
                 bias_t(s + 1)
                 back_t(s + 1)
-            if s + 3 < N_B:
-                tanh(s + 3, 0)
+            if s + 2 < N_B:
+                tanh(s + 2, 0)
             step(s - 1, 1)
             step(s - 2, 5)
             step(s - 3, 9)
-            if s + 3 < N_B:
-                tanh(s + 3, 1)
+            if s + 2 < N_B:
+                tanh(s + 2, 1)
             step(s - 1, 2)
             step(s - 2, 6)
             step(s - 3, 10)
-            if 0 <= d < 12 and D_GPS < V:
-                sub_act(d, D_GPS, V)
-            elif d == 15:
+            if d == 15:
                 sub_act(d, 1536, V)
             step(s - 1, 3)
             step(s - 2, 7)

@@ -185,8 +185,8 @@ def tile_joint_kernel(tc, h_pred, h_enc, W1, b1, W2, b2, out):
                 in_=grp2[vb][:].rearrange("p c v t -> p (c v t)"),
             )
 
-        predb = const.tile([P, 2, P, 4], F32, name="predb")
-        encs = const.tile([P, 2, 2 * P, 4], F32, name="encs")
+        predb = const.tile([P, N_B, 2, U_P, 4], F32, name="predb")
+        encs = const.tile([P, N_B, 2, T_E, 4], F32, name="encs")
 
         def stage1(c, blk):
             half = 0 if blk == 0 else 1
@@ -211,16 +211,16 @@ def tile_joint_kernel(tc, h_pred, h_enc, W1, b1, W2, b2, out):
 
         def evac_enc(eng_copy, bank, c, blk):
             eng_copy(
-                out=encs[:, c, (blk - 1) * P : blk * P, :],
-                in_=bank[:].rearrange("p t r -> p r t"),
+                out=encs[:, (blk - 1) * 8 : blk * 8, c, :, :],
+                in_=bank[:].rearrange("p t (n a) -> p n a t", a=T_E),
             )
 
         pb = [stage1(0, 0), stage1(1, 0)]
         for c in range(2):
             nc.vector.tensor_tensor(
-                out=predb[:, c],
-                in0=pb[c][:].rearrange("p t r -> p r t"),
-                in1=b1T[:, 4 * c : 4 * c + 4].unsqueeze(1).to_broadcast([P, P, 4]),
+                out=predb[:, :, c, :, :],
+                in0=pb[c][:].rearrange("p t (n u) -> p n u t", u=U_P),
+                in1=b1T[:, 4 * c : 4 * c + 4].unsqueeze(1).unsqueeze(1).to_broadcast([P, N_B, U_P, 4]),
                 op=ALU.add,
             )
         regroup_w2(nc.scalar.copy, 0, 1, 0, 256)
@@ -237,17 +237,12 @@ def tile_joint_kernel(tc, h_pred, h_enc, W1, b1, W2, b2, out):
         def zadd(n):
             z = zp.tile([P, 2, P, 4], F32, name="z", tag="z")
             z_t[n] = z
-            for c in range(2):
-                nc.gpsimd.tensor_tensor(
-                    out=z[:, c].rearrange("p (a u) t -> p a u t", u=U_P),
-                    in0=predb[:, c, n * U_P : (n + 1) * U_P, :]
-                    .unsqueeze(1)
-                    .to_broadcast([P, T_E, U_P, 4]),
-                    in1=encs[:, c, n * T_E : (n + 1) * T_E, :]
-                    .unsqueeze(2)
-                    .to_broadcast([P, T_E, U_P, 4]),
-                    op=ALU.add,
-                )
+            nc.gpsimd.tensor_tensor(
+                out=z[:].rearrange("p c (a u) t -> p c a u t", u=U_P),
+                in0=predb[:, n].unsqueeze(2).to_broadcast([P, 2, T_E, U_P, 4]),
+                in1=encs[:, n].unsqueeze(3).to_broadcast([P, 2, T_E, U_P, 4]),
+                op=ALU.add,
+            )
 
         def tanh(n, c):
             if c == 0:

@@ -19,10 +19,12 @@ N_B, T_E, U_P, H, J, V = 16, 16, 8, 512, 1024, 2048
 FLOPS = 2 * (N_B * U_P * H * J + N_B * T_E * H * J + N_B * T_E * U_P * J * V)
 LN2 = math.log(2.0)
 NEWTON = 4
+STEPS = 2 * NEWTON + 1
 SPLIT1 = 640
-Y0 = 8
-D_GPS = 2048
-PLAIN_TILES = (1, 4, 7, 10, 13)
+NG = 4
+R_E = NG * U_P
+R_B = R_E + NG * T_E
+LAST = 12
 
 
 def tile_joint_kernel(tc, h_pred, h_enc, W1, b1, W2, b2, out):
@@ -32,31 +34,48 @@ def tile_joint_kernel(tc, h_pred, h_enc, W1, b1, W2, b2, out):
         const = ctx.enter_context(tc.tile_pool(name="const", bufs=1))
         rawp = ctx.enter_context(tc.tile_pool(name="rawp", bufs=6))
         grpp = ctx.enter_context(tc.tile_pool(name="grpp", bufs=3))
-        zp = ctx.enter_context(tc.tile_pool(name="zp", bufs=3))
         xp = ctx.enter_context(tc.tile_pool(name="xp", bufs=3))
         xqp = ctx.enter_context(tc.tile_pool(name="xqp", bufs=4))
-        yp = ctx.enter_context(tc.tile_pool(name="yp", bufs=8))
+        yp = ctx.enter_context(tc.tile_pool(name="yp", bufs=7))
         jp = ctx.enter_context(tc.tile_pool(name="jp", bufs=2))
-        ytp = ctx.enter_context(tc.tile_pool(name="ytp", bufs=2))
         st = ctx.enter_context(tc.tile_pool(name="st", bufs=8))
-        psum = ctx.enter_context(tc.psum_pool(name="psum", bufs=8))
+        psl = ctx.enter_context(tc.psum_pool(name="psl", bufs=6))
+        psz = ctx.enter_context(tc.psum_pool(name="psz", bufs=2))
         ctx.enter_context(tc.manual_schedule())
 
-        brows = const.tile([P, P], BF16, name="brows")
-        nc.sync.dma_start(out=brows[0:8, :], in_=b1.rearrange("(a m) -> a m", a=8))
-        nc.sync.dma_start(out=brows[8:24, :], in_=b2.rearrange("(a m) -> a m", a=16))
-        nc.sync.dma_start(out=brows[24:32, :], in_=b2[0:1024].rearrange("(a m) -> a m", a=8))
-        nc.vector.memset(brows[32:64, :].bitcast(I32), 0)
-        nc.vector.memset(brows[64:128, :].bitcast(I32), 0)
+        b1row = const.tile([P, J], BF16, name="b1row")
+        nc.sync.dma_start(out=b1row[R_B : R_B + 1, :], in_=b1.rearrange("(a m) -> a m", a=1))
+        stack = const.tile([P, NG, J], F32, name="stack")
+        nc.vector.memset(stack[R_B:P, :, :], 0.0)
         kb = const.tile([P, NEWTON + 1], F32, name="kb")
         for k in range(NEWTON):
             nc.vector.memset(kb[:, k : k + 1], float(k - NEWTON))
         nc.vector.memset(kb[:, NEWTON : NEWTON + 1], LN2 * (0.043 - 127.0) - float(NEWTON))
         identf = const.tile([P, P], F32, name="identf")
         make_identity(nc, identf[:])
-        identb = const.tile([P, P], BF16, name="identb")
-        make_identity(nc, identb[:])
-
+        sel = const.tile([P, NG, T_E, U_P], F32, name="sel")
+        nc.gpsimd.tensor_tensor(
+            out=sel[:],
+            in0=identf[:, 0:R_E]
+            .rearrange("p (q u) -> p q u", q=NG)
+            .unsqueeze(2)
+            .to_broadcast([P, NG, T_E, U_P]),
+            in1=identf[:, R_E:R_B]
+            .rearrange("p (q t) -> p q t", q=NG)
+            .unsqueeze(3)
+            .to_broadcast([P, NG, T_E, U_P]),
+            op=ALU.add,
+        )
+        nc.gpsimd.tensor_scalar(
+            out=sel[:].rearrange("p q t u -> p (q t u)"),
+            in0=sel[:].rearrange("p q t u -> p (q t u)"),
+            scalar1=identf[:, R_B : R_B + 1], scalar2=1.0, op0=ALU.add, op1=ALU.mult,
+        )
+        hp_g = const.tile([P, NG, P, 2], F32, name="hp_g", align_bytes=64)
+        he_g = const.tile([P, NG, P, 2], F32, name="he_g", align_bytes=64)
+        nc.vector.memset(hp_g[:, :, R_E:P, :], 0.0)
+        nc.vector.memset(he_g[:, :, 0:R_E, :], 0.0)
+        nc.vector.memset(he_g[:, :, R_B:P, :], 0.0)
 
         def load_w1(half):
             raw = rawp.tile([P, 4, J], BF16, name="raw1_%d" % half, tag="raw")
@@ -85,26 +104,13 @@ def tile_joint_kernel(tc, h_pred, h_enc, W1, b1, W2, b2, out):
                 in_=W2[:, vb * 512 : (vb + 1) * 512].rearrange("(g p) v -> p g v", p=P),
             )
             raw2.append(raw)
-
-        bps = psum.tile([P, P], BF16, name="bps", tag="bank")
-        nc.tensor.transpose(bps[:], brows[:], identb[:])
-        b1T = const.tile([P, 8], F32, name="b1T")
-        nc.vector.tensor_copy(out=b1T[:], in_=bps[:, 0:8])
-        b2T = const.tile([P, 16], BF16, name="b2T")
-        nc.vector.tensor_copy(out=b2T[:], in_=bps[:, 8:24])
         b2bc = const.tile([P, V], BF16, name="b2bc")
-        for vb in range(4):
-            b2ps = psum.tile([P, 4, P], F32, name="b2ps", tag="bank")
-            for a in range(4):
-                nc.tensor.matmul(
-                    out=b2ps[:, a, :],
-                    lhsT=b2T[:, 4 * vb + a : 4 * vb + a + 1].to_broadcast([P, P]),
-                    rhs=identb[:],
-                    start=True, stop=True,
-                )
-            nc.scalar.copy(
-                out=b2bc[:, vb * 512 : (vb + 1) * 512], in_=b2ps[:].rearrange("p a m -> p (a m)")
-            )
+        nc.sync.dma_start(out=b2bc[:], in_=b2.partition_broadcast(P))
+
+        def b1_to_stack(g):
+            nc.scalar.copy(out=stack[R_B : R_B + 1, g, :], in_=b1row[R_B : R_B + 1, :])
+
+        b1_to_stack(0)
 
         w1_q = const.tile([P, 2, J], U32, name="w1_q", align_bytes=64)
         w1_s = const.tile([P, 2, J], U8, name="w1_s", align_bytes=64)
@@ -128,40 +134,43 @@ def tile_joint_kernel(tc, h_pred, h_enc, W1, b1, W2, b2, out):
         regroup_w1(nc.vector.tensor_copy, 0, 0, SPLIT1)
         regroup_w1(nc.scalar.copy, 0, SPLIT1, J)
 
-        hpT = psum.tile([P, 2, P], F32, name="hpT", tag="bank")
+        hpT = psl.tile([P, 2, P], F32, name="hpT", tag="lg")
         for u in range(2):
             nc.tensor.transpose(
                 hpT[:, u, :], hp_sb[:].bitcast(F32)[:, u * P : (u + 1) * P], identf[:]
             )
-        heT = psum.tile([P, 2, 2, P], F32, name="heT", tag="bank")
+        nc.vector.tensor_copy(
+            out=hp_g[:, :, 0:R_E, :], in_=hpT[:].rearrange("p u (g r) -> p g r u", g=NG)
+        )
         for a in range(2):
+            heT = psl.tile([P, 2, P], F32, name="heT%d" % a, tag="lg")
             for u in range(2):
                 nc.tensor.transpose(
-                    heT[:, a, u, :],
+                    heT[:, u, :],
                     he_sb[:, a, :].bitcast(F32)[:, u * P : (u + 1) * P],
                     identf[:],
                 )
-        hp_g = const.tile([P, P, 2], F32, name="hp_g", align_bytes=64)
-        nc.vector.tensor_copy(out=hp_g[:], in_=hpT[:].rearrange("p u r -> p r u"))
-        he_g = const.tile([P, 2, P, 2], F32, name="he_g", align_bytes=64)
-        nc.vector.tensor_copy(out=he_g[:], in_=heT[:].rearrange("p a u r -> p a r u"))
-        hp_q = const.tile([P, P], U32, name="hp_q", align_bytes=64)
-        hp_s = const.tile([P, P], U8, name="hp_s", align_bytes=64)
-        he_q = const.tile([P, 2 * P], U32, name="he_q", align_bytes=64)
-        he_s = const.tile([P, 2 * P], U8, name="he_s", align_bytes=64)
+            nc.vector.tensor_copy(
+                out=he_g[:, 2 * a : 2 * a + 2, R_E:R_B, :],
+                in_=heT[:].rearrange("p u (g r) -> p g r u", g=2),
+            )
+        hp_q = const.tile([P, NG * P], U32, name="hp_q", align_bytes=64)
+        hp_s = const.tile([P, NG * P], U8, name="hp_s", align_bytes=64)
+        he_q = const.tile([P, NG * P], U32, name="he_q", align_bytes=64)
+        he_s = const.tile([P, NG * P], U8, name="he_s", align_bytes=64)
+        quant_w1(0)
         nc.vector.quantize_mx(
             out=hp_q[:].bitcast(FP8X4),
             scales=hp_s[:],
-            in_=hp_g[:].rearrange("p r u -> p (r u)").bitcast(BF16),
+            in_=hp_g[:].rearrange("p g r u -> p (g r u)").bitcast(BF16),
         )
+        regroup_w1(nc.vector.tensor_copy, 1, 0, SPLIT1)
+        regroup_w1(nc.scalar.copy, 1, SPLIT1, J)
         nc.vector.quantize_mx(
             out=he_q[:].bitcast(FP8X4),
             scales=he_s[:],
-            in_=he_g[:].rearrange("p a r u -> p (a r u)").bitcast(BF16),
+            in_=he_g[:].rearrange("p g r u -> p (g r u)").bitcast(BF16),
         )
-        quant_w1(0)
-        regroup_w1(nc.vector.tensor_copy, 1, 0, SPLIT1)
-        regroup_w1(nc.scalar.copy, 1, SPLIT1, J)
         quant_w1(1)
 
         w2_q = const.tile([P, 4, 2, 512], U32, name="w2_q", align_bytes=64)
@@ -185,83 +194,59 @@ def tile_joint_kernel(tc, h_pred, h_enc, W1, b1, W2, b2, out):
                 in_=grp2[vb][:].rearrange("p c v t -> p (c v t)"),
             )
 
-        predb = const.tile([P, N_B, 2, U_P, 4], F32, name="predb")
-        encs = const.tile([P, N_B, 2, T_E, 4], F32, name="encs")
-
-        def stage1(c, blk):
-            half = 0 if blk == 0 else 1
-            bank = psum.tile([P, 4, P], F32, name="s1bank", tag="bank")
-            for t in range(4):
-                jt = 4 * c + t
-                if blk == 0:
-                    rq, rs = hp_q[:, :], hp_s[:, :]
-                else:
-                    rq = he_q[:, (blk - 1) * P : blk * P]
-                    rs = he_s[:, (blk - 1) * P : blk * P]
-                nc.tensor.matmul_mx(
-                    out=bank[:, t, :],
-                    lhsT=w1_q[:, half, jt * P : (jt + 1) * P].bitcast(FP8X4),
-                    lhsT_scale=w1_s[:, half, jt * P : (jt + 1) * P],
-                    rhs=rq.bitcast(FP8X4),
-                    rhs_scale=rs,
-                    start=True,
-                    stop=True,
-                )
-            return bank
-
-        def evac_enc(eng_copy, bank, c, blk):
-            eng_copy(
-                out=encs[:, (blk - 1) * 8 : blk * 8, c, :, :],
-                in_=bank[:].rearrange("p t (n a) -> p n a t", a=T_E),
+        def stage1(g, half, eng_copy):
+            bank = psl.tile([P, 512], F32, name="s1bank", tag="lg")
+            cols = slice(half * 512, (half + 1) * 512)
+            rows = slice(g * P, (g + 1) * P)
+            nc.tensor.matmul_mx(
+                out=bank[:],
+                lhsT=hp_q[:, rows].bitcast(FP8X4), lhsT_scale=hp_s[:, rows],
+                rhs=w1_q[:, 0, cols].bitcast(FP8X4), rhs_scale=w1_s[:, 0, cols],
+                start=True, stop=False,
             )
-
-        pb = [stage1(0, 0), stage1(1, 0)]
-        for c in range(2):
-            nc.vector.tensor_tensor(
-                out=predb[:, :, c, :, :],
-                in0=pb[c][:].rearrange("p t (n u) -> p n u t", u=U_P),
-                in1=b1T[:, 4 * c : 4 * c + 4].unsqueeze(1).unsqueeze(1).to_broadcast([P, N_B, U_P, 4]),
-                op=ALU.add,
+            nc.tensor.matmul_mx(
+                out=bank[:],
+                lhsT=he_q[:, rows].bitcast(FP8X4), lhsT_scale=he_s[:, rows],
+                rhs=w1_q[:, 1, cols].bitcast(FP8X4), rhs_scale=w1_s[:, 1, cols],
+                start=False, stop=True,
             )
-        regroup_w2(nc.scalar.copy, 0, 1, 0, 256)
-        eb = [stage1(0, 1), stage1(1, 1)]
-        evac_enc(nc.scalar.copy, eb[0], 0, 1)
-        evac_enc(nc.scalar.copy, eb[1], 1, 1)
-        eb2 = [stage1(0, 2), stage1(1, 2)]
-        evac_enc(nc.vector.tensor_copy, eb2[0], 0, 2)
-        evac_enc(nc.vector.tensor_copy, eb2[1], 1, 2)
+            eng_copy(out=stack[0:R_B, g, cols], in_=bank[0:R_B, :])
 
         z_t, x_t, xq_t, bank_t, y_t, negm_t, ssum_t, chain_t, negk_t = {}, {}, {}, {}, {}, {}, {}, {}, {}
-        lt_t, yt_t, yfull_t = {}, {}, {}
 
-        def zadd(n):
-            z = zp.tile([P, 2, P, 4], F32, name="z", tag="z")
-            z_t[n] = z
-            nc.gpsimd.tensor_tensor(
-                out=z[:].rearrange("p c (a u) t -> p c a u t", u=U_P),
-                in0=predb[:, n].unsqueeze(2).to_broadcast([P, 2, T_E, U_P, 4]),
-                in1=encs[:, n].unsqueeze(3).to_broadcast([P, 2, T_E, U_P, 4]),
-                op=ALU.add,
-            )
+        def zsum(n):
+            g, q = n // NG, n % NG
+            for c in range(2):
+                bank = psz.tile([P, 4, P], F32, name="zb", tag="zb")
+                z_t[(n, c)] = bank
+                for t in range(4):
+                    j0 = (4 * c + t) * P
+                    nc.tensor.matmul(
+                        out=bank[:, t, :],
+                        lhsT=stack[:, g, j0 : j0 + P],
+                        rhs=sel[:, q].rearrange("p t u -> p (t u)"),
+                        start=True, stop=True,
+                    )
 
         def tanh(n, c):
             if c == 0:
-                x_t[n] = xp.tile([P, 2, P * 4], BF16, name="x", tag="x", align_bytes=64)
+                x_t[n] = xp.tile([P, 2, P, 4], BF16, name="x", tag="x", align_bytes=64)
             nc.scalar.activation(
-                out=x_t[n][:, c, :], in_=z_t[n][:, c].rearrange("p w t -> p (w t)"), func=ACT.Tanh
+                out=x_t[n][:, c], in_=z_t[(n, c)][:].rearrange("p t r -> p r t"), func=ACT.Tanh
             )
 
         def quant_x(n):
             xq = xqp.tile([P, 2 * P], U32, name="xq", tag="xq", align_bytes=64)
             xs = xqp.tile([P, 2 * P], U8, name="xs", tag="xs", align_bytes=64)
             nc.vector.quantize_mx(
-                out=xq[:].bitcast(FP8X4), scales=xs[:], in_=x_t[n][:].rearrange("p c w -> p (c w)")
+                out=xq[:].bitcast(FP8X4), scales=xs[:],
+                in_=x_t[n][:].rearrange("p c r t -> p (c r t)"),
             )
             xq_t[n] = (xq, xs)
 
         def mm(n, vb):
             xq, xs = xq_t[n]
-            bank = psum.tile([P, 512], F32, name="lg", tag="bank")
+            bank = psl.tile([P, 512], F32, name="lg", tag="lg")
             bank_t[(n, vb)] = bank
             for c in range(2):
                 nc.tensor.matmul_mx(
@@ -274,73 +259,27 @@ def tile_joint_kernel(tc, h_pred, h_enc, W1, b1, W2, b2, out):
                     stop=(c == 1),
                 )
 
-        def mm_t(n):
-            xq, xs = xq_t[n]
-            lt = psum.tile([P, 4, P], F32, name="lt", tag="bank")
-            lt_t[n] = lt
-            for a in range(4):
-                for c in range(2):
-                    nc.tensor.matmul_mx(
-                        out=lt[:, a, :],
-                        lhsT=w2_q[:, 3, c, a * P : (a + 1) * P].bitcast(FP8X4),
-                        lhsT_scale=w2_s[:, 3, c, a * P : (a + 1) * P],
-                        rhs=xq[:, c * P : (c + 1) * P].bitcast(FP8X4),
-                        rhs_scale=xs[:, c * P : (c + 1) * P],
-                        start=(c == 0),
-                        stop=(c == 1),
-                    )
-
-        def bias_t(n):
-            yt = ytp.tile([P, 4, P], F32, name="yt", tag="yt")
-            yt_t[n] = yt
-            for a in range(4):
-                nc.scalar.activation(
-                    out=yt[:, a, :], in_=lt_t[n][:, a, :], func=ACT.Identity,
-                    bias=b2T[:, 12 + a : 13 + a], scale=1.0,
-                )
-
-        def back_t(n):
-            bank = psum.tile([P, 4, P], F32, name="lg3", tag="bank")
-            bank_t[(n, 3)] = bank
-            for a in range(4):
-                nc.tensor.transpose(bank[:, a, :], yt_t[n][:, a, :], identf[:])
-
         def add_b2(n, vb):
             if vb == 0:
-                yfull_t[n] = yp.tile([P, Y0 + V], F32, name="y", tag="y")
-                y_t[n] = yfull_t[n][:, Y0 : Y0 + V]
-            if vb < 3 or n in PLAIN_TILES:
-                nc.vector.tensor_tensor(
-                    out=y_t[n][:, vb * 512 : (vb + 1) * 512],
-                    in0=bank_t[(n, vb)][:],
-                    in1=b2bc[:, vb * 512 : (vb + 1) * 512],
-                    op=ALU.add,
-                )
-            else:
-                nc.vector.tensor_scalar(
-                    out=y_t[n][:, 1536:V],
-                    in0=bank_t[(n, 3)][:].rearrange("p a m -> p (a m)"),
-                    scalar1=0.0, scalar2=None, op0=ALU.add, op1=ALU.max,
-                    accum_out=yfull_t[n][:, Y0 - 1 : Y0],
-                )
+                y_t[n] = yp.tile([P, V], F32, name="y", tag="y")
+            nc.vector.tensor_tensor(
+                out=y_t[n][:, vb * 512 : (vb + 1) * 512],
+                in0=bank_t[(n, vb)][:],
+                in1=b2bc[:, vb * 512 : (vb + 1) * 512],
+                op=ALU.add,
+            )
 
         def row_max(n):
             negm = st.tile([P, 1], F32, name="negm", tag="negm")
             negm_t[n] = negm
-            if n in PLAIN_TILES:
-                nc.vector.tensor_reduce(out=negm[:], in_=y_t[n], axis=AX.X, op=ALU.max, negate=True)
-            else:
-                nc.vector.tensor_reduce(
-                    out=negm[:], in_=yfull_t[n][:, Y0 - 1 : Y0 + 1536], axis=AX.X, op=ALU.max,
-                    negate=True,
-                )
+            nc.vector.tensor_reduce(out=negm[:], in_=y_t[n][:], axis=AX.X, op=ALU.max, negate=True)
 
         def exp_sum(n):
             junk = jp.tile([P, V], BF16, name="junk", tag="junk")
             ssum = st.tile([P, 1], F32, name="ssum", tag="ssum")
             ssum_t[n] = ssum
             nc.scalar.activation(
-                out=junk[:], in_=y_t[n], func=ACT.Exp, bias=negm_t[n][:, 0:1], scale=1.0,
+                out=junk[:], in_=y_t[n][:], func=ACT.Exp, bias=negm_t[n][:, 0:1], scale=1.0,
                 accum_out=ssum[:, 0:1],
             )
 
@@ -354,13 +293,6 @@ def tile_joint_kernel(tc, h_pred, h_enc, W1, b1, W2, b2, out):
                     bias=kb[:, NEWTON : NEWTON + 1], scale=LN2 / 8388608.0,
                 )
                 chain_t[n] = (r, None)
-            elif k == 2 * NEWTON + 2:
-                r, e = chain_t[n]
-                negk = st.tile([P, 1], F32, name="negk", tag="negk")
-                nc.scalar.activation(
-                    out=negk[:], in_=r[:], func=ACT.Identity, bias=negm_t[n][:, 0:1], scale=-1.0
-                )
-                negk_t[n] = negk
             elif k % 2 == 0:
                 r, e = chain_t[n]
                 i = k // 2 - 1
@@ -376,6 +308,13 @@ def tile_joint_kernel(tc, h_pred, h_enc, W1, b1, W2, b2, out):
                     out=r2[:], in_=e[:], func=ACT.Identity, bias=r[:, 0:1], scale=ssum_t[n][:, 0:1]
                 )
                 chain_t[n] = (r2, None)
+
+        def minus_lse(n):
+            negk = st.tile([P, 1], F32, name="negk", tag="negk")
+            nc.vector.tensor_tensor(
+                out=negk[:], in0=negm_t[n][:], in1=chain_t[n][0][:], op=ALU.subtract
+            )
+            negk_t[n] = negk
 
         def sub_gps(n, c0, c1):
             nc.gpsimd.tensor_scalar(
@@ -396,96 +335,83 @@ def tile_joint_kernel(tc, h_pred, h_enc, W1, b1, W2, b2, out):
             )
 
         def store(n):
-            nc.sync.dma_start(out=out_rows[n * P : (n + 1) * P, :], in_=y_t[n])
+            nc.sync.dma_start(out=out_rows[n * P : (n + 1) * P, :], in_=y_t[n][:])
 
-        zadd(0)
         regroup_w2(nc.vector.tensor_copy, 0, 0, 0, 512)
-        regroup_w2(nc.scalar.copy, 0, 1, 256, 512)
+        regroup_w2(nc.scalar.copy, 0, 1, 0, 512)
+        stage1(0, 0, nc.scalar.copy)
+        stage1(0, 1, nc.vector.tensor_copy)
+        zsum(0)
+        regroup_w2(nc.vector.tensor_copy, 1, 0, 0, 512)
         quant_w2(0)
-        zadd(1)
         tanh(0, 0)
         tanh(0, 1)
+        regroup_w2(nc.scalar.copy, 1, 1, 0, 512)
+        zsum(1)
+        regroup_w2(nc.vector.tensor_copy, 2, 0, 0, 512)
         quant_x(0)
         mm(0, 0)
-        regroup_w2(nc.vector.tensor_copy, 1, 0, 0, 512)
-        regroup_w2(nc.scalar.copy, 1, 1, 0, 256)
-        regroup_w2(nc.scalar.copy, 1, 1, 256, 512)
-        add_b2(0, 0)
-        quant_w2(1)
-        mm(0, 1)
-        zadd(2)
         tanh(1, 0)
         tanh(1, 1)
-        regroup_w2(nc.vector.tensor_copy, 2, 0, 0, 512)
-        regroup_w2(nc.scalar.copy, 2, 1, 0, 256)
-        regroup_w2(nc.scalar.copy, 2, 1, 256, 512)
+        quant_w2(1)
+        mm(0, 1)
+        regroup_w2(nc.scalar.copy, 2, 1, 0, 512)
+        zsum(2)
+        regroup_w2(nc.vector.tensor_copy, 3, 0, 0, 512)
         quant_x(1)
-        mm(1, 0)
-        mm(1, 1)
-        add_b2(0, 1)
-        quant_w2(2)
-        mm(0, 2)
-        mm(1, 2)
-        zadd(3)
+        regroup_w2(nc.scalar.copy, 3, 1, 0, 512)
         tanh(2, 0)
         tanh(2, 1)
-        regroup_w2(nc.vector.tensor_copy, 3, 0, 0, 512)
-        regroup_w2(nc.scalar.copy, 3, 1, 0, 256)
-        regroup_w2(nc.scalar.copy, 3, 1, 256, 512)
-        add_b2(0, 2)
+        zsum(3)
+        quant_w2(2)
+        mm(0, 2)
         quant_w2(3)
-        mm_t(0)
-        bias_t(0)
-        back_t(0)
-        mm(1, 3)
-        add_b2(0, 3)
-        row_max(0)
+        mm(0, 3)
+        mm(1, 0)
+        mm(1, 1)
 
-        for s in range(1, N_B + 5):
+        for s in range(0, N_B + 4):
             d = s - 4
-            if 0 <= d < 12:
-                sub_gps(d, 0, D_GPS)
-            elif 12 <= d < 15:
-                sub_gps(d, 1024, V)
-            elif d == 15:
-                sub_gps(d, 1024, 1536)
-            if s + 3 < N_B:
-                zadd(s + 3)
-            if s + 1 < N_B:
-                quant_x(s + 1)
-                if s + 1 in PLAIN_TILES:
-                    for vb in range(4):
-                        mm(s + 1, vb)
-                else:
-                    mm_t(s + 1)
-                    for vb in range(3):
-                        mm(s + 1, vb)
+            if 0 < s < N_B - 1:
+                mm(s + 1, 0)
+                mm(s + 1, 1)
             if s < N_B:
                 for vb in range(4):
                     add_b2(s, vb)
+                    if vb < 2 and s + 1 < N_B:
+                        mm(s + 1, vb + 2)
+            if s + 2 < N_B:
+                quant_x(s + 2)
+            if d >= 0:
+                minus_lse(d)
+            if s < N_B:
                 row_max(s)
-            if 12 <= d < N_B:
-                sub_vec(d, 0, 1024)
-            if s - 1 < N_B:
+            if 1 <= s <= N_B:
                 exp_sum(s - 1)
             step(s - 2, 4)
             step(s - 3, 8)
-            if s + 1 < N_B and s + 1 not in PLAIN_TILES:
-                bias_t(s + 1)
-                back_t(s + 1)
-            if s + 2 < N_B:
-                tanh(s + 2, 0)
+            if s + 3 < N_B:
+                tanh(s + 3, 0)
             step(s - 1, 1)
             step(s - 2, 5)
             step(s - 3, 9)
-            if s + 2 < N_B:
-                tanh(s + 2, 1)
+            if s + 3 < N_B:
+                tanh(s + 3, 1)
             step(s - 1, 2)
             step(s - 2, 6)
-            step(s - 3, 10)
-            if d == 15:
-                sub_act(d, 1536, V)
+            if s + 4 < N_B:
+                if s % NG == 0:
+                    b1_to_stack(s // NG + 1)
+                    for half in range(2):
+                        stage1(s // NG + 1, half, nc.scalar.copy)
+                zsum(s + 4)
             step(s - 1, 3)
             step(s - 2, 7)
-            if 0 <= d < N_B:
+            if 0 <= d < LAST:
+                sub_gps(d, 0, V)
+                store(d)
+            elif d >= 0:
+                sub_vec(d, 0, 1024)
+                sub_gps(d, 1024, 1536)
+                sub_act(d, 1536, V)
                 store(d)

@@ -21,10 +21,14 @@ LN2 = math.log(2.0)
 NEWTON = 4
 STEPS = 2 * NEWTON + 1
 SPLIT1 = 640
+SPLIT2 = 256
 NG = 4
 R_E = NG * U_P
 R_B = R_E + NG * T_E
-LAST = 12
+SHARED = ()
+SPLIT_END = 1280
+END = N_B - 3
+LATE = {END: (END - 4, END - 3), END + 1: (END - 2, END - 1), END + 2: (END,)}
 
 
 def tile_joint_kernel(tc, h_pred, h_enc, W1, b1, W2, b2, out):
@@ -107,10 +111,11 @@ def tile_joint_kernel(tc, h_pred, h_enc, W1, b1, W2, b2, out):
         b2bc = const.tile([P, V], BF16, name="b2bc")
         nc.sync.dma_start(out=b2bc[:], in_=b2.partition_broadcast(P))
 
-        def b1_to_stack(g):
-            nc.scalar.copy(out=stack[R_B : R_B + 1, g, :], in_=b1row[R_B : R_B + 1, :])
-
-        b1_to_stack(0)
+        nc.scalar.copy(out=stack[R_B : R_B + 1, 0, :], in_=b1row[R_B : R_B + 1, :])
+        nc.vector.tensor_copy(
+            out=stack[R_B : R_B + 1, 1:NG, :],
+            in_=b1row[R_B : R_B + 1, :].unsqueeze(1).to_broadcast([1, NG - 1, J]),
+        )
 
         w1_q = const.tile([P, 2, J], U32, name="w1_q", align_bytes=64)
         w1_s = const.tile([P, 2, J], U8, name="w1_s", align_bytes=64)
@@ -212,6 +217,7 @@ def tile_joint_kernel(tc, h_pred, h_enc, W1, b1, W2, b2, out):
             )
             eng_copy(out=stack[0:R_B, g, cols], in_=bank[0:R_B, :])
 
+        done_t = {}
         z_t, x_t, xq_t, bank_t, y_t, negm_t, ssum_t, chain_t, negk_t = {}, {}, {}, {}, {}, {}, {}, {}, {}
 
         def zsum(n):
@@ -259,9 +265,18 @@ def tile_joint_kernel(tc, h_pred, h_enc, W1, b1, W2, b2, out):
                     stop=(c == 1),
                 )
 
+        def new_y(n):
+            y_t[n] = yp.tile([P, V], F32, name="y", tag="y")
+
+        def copy_last(n):
+            nc.scalar.copy(out=y_t[n][:, 1536:V], in_=bank_t[(n, 3)][:])
+
+        def add_last(n):
+            nc.gpsimd.tensor_tensor(
+                out=y_t[n][:, 1536:V], in0=y_t[n][:, 1536:V], in1=b2bc[:, 1536:V], op=ALU.add
+            )
+
         def add_b2(n, vb):
-            if vb == 0:
-                y_t[n] = yp.tile([P, V], F32, name="y", tag="y")
             nc.vector.tensor_tensor(
                 out=y_t[n][:, vb * 512 : (vb + 1) * 512],
                 in0=bank_t[(n, vb)][:],
@@ -284,8 +299,9 @@ def tile_joint_kernel(tc, h_pred, h_enc, W1, b1, W2, b2, out):
             )
 
         def step(n, k):
-            if n < 0 or n >= N_B:
+            if n < 0:
                 return
+            done_t[n] = k
             if k == 1:
                 r = st.tile([P, 1], F32, name="nr", tag="nr")
                 nc.scalar.activation(
@@ -308,6 +324,21 @@ def tile_joint_kernel(tc, h_pred, h_enc, W1, b1, W2, b2, out):
                     out=r2[:], in_=e[:], func=ACT.Identity, bias=r[:, 0:1], scale=ssum_t[n][:, 0:1]
                 )
                 chain_t[n] = (r2, None)
+
+        def finish(rows):
+            for i in range(STEPS + 1):
+                for n in rows:
+                    k = done_t.get(n, 0) + 1
+                    if k <= STEPS:
+                        step(n, k)
+                    elif k == STEPS + 1:
+                        done_t[n] = k
+                        negk = st.tile([P, 1], F32, name="negk", tag="negk")
+                        nc.scalar.activation(
+                            out=negk[:], in_=chain_t[n][0][:], func=ACT.Identity,
+                            bias=negm_t[n][:, 0:1], scale=-1.0,
+                        )
+                        negk_t[n] = negk
 
         def minus_lse(n):
             negk = st.tile([P, 1], F32, name="negk", tag="negk")
@@ -341,13 +372,16 @@ def tile_joint_kernel(tc, h_pred, h_enc, W1, b1, W2, b2, out):
         regroup_w2(nc.scalar.copy, 0, 1, 0, 512)
         stage1(0, 0, nc.scalar.copy)
         stage1(0, 1, nc.vector.tensor_copy)
+        stage1(1, 0, nc.scalar.copy)
+        stage1(1, 1, nc.scalar.copy)
         zsum(0)
         regroup_w2(nc.vector.tensor_copy, 1, 0, 0, 512)
         quant_w2(0)
         tanh(0, 0)
         tanh(0, 1)
-        regroup_w2(nc.scalar.copy, 1, 1, 0, 512)
+        regroup_w2(nc.scalar.copy, 1, 1, SPLIT2, 512)
         zsum(1)
+        regroup_w2(nc.vector.tensor_copy, 1, 1, 0, SPLIT2)
         regroup_w2(nc.vector.tensor_copy, 2, 0, 0, 512)
         quant_x(0)
         mm(0, 0)
@@ -355,63 +389,88 @@ def tile_joint_kernel(tc, h_pred, h_enc, W1, b1, W2, b2, out):
         tanh(1, 1)
         quant_w2(1)
         mm(0, 1)
-        regroup_w2(nc.scalar.copy, 2, 1, 0, 512)
+        regroup_w2(nc.scalar.copy, 2, 1, SPLIT2, 512)
         zsum(2)
+        regroup_w2(nc.vector.tensor_copy, 2, 1, 0, SPLIT2)
         regroup_w2(nc.vector.tensor_copy, 3, 0, 0, 512)
         quant_x(1)
-        regroup_w2(nc.scalar.copy, 3, 1, 0, 512)
-        tanh(2, 0)
-        tanh(2, 1)
-        zsum(3)
+        new_y(0)
+        add_b2(0, 0)
+        stage1(2, 0, nc.scalar.copy)
+        regroup_w2(nc.scalar.copy, 3, 1, SPLIT2, 512)
         quant_w2(2)
         mm(0, 2)
+        mm(1, 0)
+        regroup_w2(nc.vector.tensor_copy, 3, 1, 0, SPLIT2)
+        add_b2(0, 1)
+        stage1(2, 1, nc.scalar.copy)
+        stage1(3, 0, nc.scalar.copy)
+        tanh(2, 0)
+        tanh(2, 1)
         quant_w2(3)
         mm(0, 3)
-        mm(1, 0)
         mm(1, 1)
+        stage1(3, 1, nc.scalar.copy)
+        zsum(3)
 
-        for s in range(0, N_B + 4):
-            d = s - 4
+        for s in range(N_B):
+            order = (3, 0, 1, 2) if s + 1 in SHARED else (0, 1, 2, 3)
+            if s + 1 < N_B:
+                new_y(s + 1)
             if 0 < s < N_B - 1:
-                mm(s + 1, 0)
-                mm(s + 1, 1)
-            if s < N_B:
-                for vb in range(4):
+                mm(s + 1, order[0])
+                mm(s + 1, order[1])
+            for vb in range(3 if s in SHARED else 4):
+                if s > 0 or vb > 1:
                     add_b2(s, vb)
-                    if vb < 2 and s + 1 < N_B:
-                        mm(s + 1, vb + 2)
+                if vb < 2 and s + 1 < N_B:
+                    mm(s + 1, order[vb + 2])
             if s + 2 < N_B:
                 quant_x(s + 2)
-            if d >= 0:
-                minus_lse(d)
-            if s < N_B:
-                row_max(s)
-            if 1 <= s <= N_B:
+            if 4 <= s < END:
+                minus_lse(s - 4)
+            row_max(s)
+            if s >= 1:
                 exp_sum(s - 1)
-            step(s - 2, 4)
-            step(s - 3, 8)
-            if s + 3 < N_B:
+            if s < END:
+                if s < END - 1:
+                    step(s - 2, 4)
+                    step(s - 3, 8)
                 tanh(s + 3, 0)
-            step(s - 1, 1)
-            step(s - 2, 5)
-            step(s - 3, 9)
-            if s + 3 < N_B:
+                step(s - 1, 1)
+                if s < END - 1:
+                    step(s - 2, 5)
+                    step(s - 3, 9)
                 tanh(s + 3, 1)
-            step(s - 1, 2)
-            step(s - 2, 6)
+                step(s - 1, 2)
+                if s < END - 1:
+                    step(s - 2, 6)
+            if s + 1 in SHARED:
+                copy_last(s + 1)
             if s + 4 < N_B:
-                if s % NG == 0:
-                    b1_to_stack(s // NG + 1)
-                    for half in range(2):
-                        stage1(s // NG + 1, half, nc.scalar.copy)
                 zsum(s + 4)
-            step(s - 1, 3)
-            step(s - 2, 7)
-            if 0 <= d < LAST:
-                sub_gps(d, 0, V)
-                store(d)
-            elif d >= 0:
-                sub_vec(d, 0, 1024)
-                sub_gps(d, 1024, 1536)
-                sub_act(d, 1536, V)
-                store(d)
+            if s < END:
+                step(s - 1, 3)
+            if s < END - 1:
+                step(s - 2, 7)
+            if s == END - 1:
+                finish(range(s - 3, s - 1))
+            if s >= END:
+                finish(range(END - 2, s))
+            if 4 <= s < END:
+                sub_gps(s - 4, 0, V)
+                store(s - 4)
+            elif s >= END:
+                for n in LATE[s]:
+                    sub_gps(n, 0, V)
+                    store(n)
+            if s + 1 in SHARED:
+                add_last(s + 1)
+
+        sub_vec(N_B - 2, 0, V)
+        store(N_B - 2)
+        exp_sum(N_B - 1)
+        finish(range(N_B - 1, N_B))
+        sub_vec(N_B - 1, 0, SPLIT_END)
+        sub_act(N_B - 1, SPLIT_END, V)
+        store(N_B - 1)

@@ -25,7 +25,8 @@ SPLIT2 = 256
 NG = 4
 R_E = NG * U_P
 R_B = R_E + NG * T_E
-SHARED = ()
+N_LG = 6
+SHARED = tuple(range(2, 13))
 SPLIT_END = 1280
 END = N_B - 3
 LATE = {END: (END - 4, END - 3), END + 1: (END - 2, END - 1), END + 2: (END,)}
@@ -43,22 +44,35 @@ def tile_joint_kernel(tc, h_pred, h_enc, W1, b1, W2, b2, out):
         yp = ctx.enter_context(tc.tile_pool(name="yp", bufs=7))
         jp = ctx.enter_context(tc.tile_pool(name="jp", bufs=2))
         st = ctx.enter_context(tc.tile_pool(name="st", bufs=8))
-        psl = ctx.enter_context(tc.psum_pool(name="psl", bufs=6))
-        psz = ctx.enter_context(tc.psum_pool(name="psz", bufs=2))
+        psum = ctx.enter_context(tc.psum_pool(name="psum", bufs=1))
         ctx.enter_context(tc.manual_schedule())
 
+        def bank(i, shape):
+            return psum.tile(shape, F32, name="bank%d" % i, tag="bank%d" % i)
+
         b1row = const.tile([P, J], BF16, name="b1row")
-        nc.sync.dma_start(out=b1row[R_B : R_B + 1, :], in_=b1.rearrange("(a m) -> a m", a=1))
+        nc.scalar.dma_start(out=b1row[R_B : R_B + 1, :], in_=b1.rearrange("(a m) -> a m", a=1))
+        b2row = const.tile([P, V], BF16, name="b2row")
+        nc.vector.memset(b2row[:].bitcast(I32), 0)
+        nc.scalar.dma_start(out=b2row[R_B : R_B + 1, :], in_=b2.rearrange("(a m) -> a m", a=1))
+        pick = const.tile([P, P], BF16, name="pick")
+        nc.vector.memset(pick[:].bitcast(I32), 0)
+        nc.vector.memset(pick[R_B : R_B + 1, :], 1.0)
         stack = const.tile([P, NG, J], F32, name="stack")
         nc.vector.memset(stack[R_B:P, :, :], 0.0)
         kb = const.tile([P, NEWTON + 1], F32, name="kb")
         for k in range(NEWTON):
             nc.vector.memset(kb[:, k : k + 1], float(k - NEWTON))
         nc.vector.memset(kb[:, NEWTON : NEWTON + 1], LN2 * (0.043 - 127.0) - float(NEWTON))
+        hp_g = const.tile([P, NG, P, 2], F32, name="hp_g", align_bytes=64)
+        he_g = const.tile([P, NG, P, 2], F32, name="he_g", align_bytes=64)
+        nc.gpsimd.memset(hp_g[:, :, R_E:P, :], 0.0)
+        nc.gpsimd.memset(he_g[:, :, 0:R_E, :], 0.0)
+        nc.gpsimd.memset(he_g[:, :, R_B:P, :], 0.0)
         identf = const.tile([P, P], F32, name="identf")
         make_identity(nc, identf[:])
         sel = const.tile([P, NG, T_E, U_P], F32, name="sel")
-        nc.gpsimd.tensor_tensor(
+        nc.vector.tensor_tensor(
             out=sel[:],
             in0=identf[:, 0:R_E]
             .rearrange("p (q u) -> p q u", q=NG)
@@ -70,16 +84,11 @@ def tile_joint_kernel(tc, h_pred, h_enc, W1, b1, W2, b2, out):
             .to_broadcast([P, NG, T_E, U_P]),
             op=ALU.add,
         )
-        nc.gpsimd.tensor_scalar(
+        nc.vector.tensor_scalar(
             out=sel[:].rearrange("p q t u -> p (q t u)"),
             in0=sel[:].rearrange("p q t u -> p (q t u)"),
-            scalar1=identf[:, R_B : R_B + 1], scalar2=1.0, op0=ALU.add, op1=ALU.mult,
+            scalar1=identf[:, R_B : R_B + 1], scalar2=None, op0=ALU.add,
         )
-        hp_g = const.tile([P, NG, P, 2], F32, name="hp_g", align_bytes=64)
-        he_g = const.tile([P, NG, P, 2], F32, name="he_g", align_bytes=64)
-        nc.vector.memset(hp_g[:, :, R_E:P, :], 0.0)
-        nc.vector.memset(he_g[:, :, 0:R_E, :], 0.0)
-        nc.vector.memset(he_g[:, :, R_B:P, :], 0.0)
 
         def load_w1(half):
             raw = rawp.tile([P, 4, J], BF16, name="raw1_%d" % half, tag="raw")
@@ -108,14 +117,15 @@ def tile_joint_kernel(tc, h_pred, h_enc, W1, b1, W2, b2, out):
                 in_=W2[:, vb * 512 : (vb + 1) * 512].rearrange("(g p) v -> p g v", p=P),
             )
             raw2.append(raw)
-        b2bc = const.tile([P, V], BF16, name="b2bc")
-        nc.sync.dma_start(out=b2bc[:], in_=b2.partition_broadcast(P))
 
-        nc.scalar.copy(out=stack[R_B : R_B + 1, 0, :], in_=b1row[R_B : R_B + 1, :])
-        nc.vector.tensor_copy(
-            out=stack[R_B : R_B + 1, 1:NG, :],
-            in_=b1row[R_B : R_B + 1, :].unsqueeze(1).to_broadcast([1, NG - 1, J]),
-        )
+        def b1_to_stack(copy, g0, g1):
+            copy(
+                out=stack[R_B : R_B + 1, g0:g1, :],
+                in_=b1row[R_B : R_B + 1, :].unsqueeze(1).to_broadcast([1, g1 - g0, J]),
+            )
+
+        b1_to_stack(nc.scalar.copy, 0, 2)
+        b1_to_stack(nc.vector.tensor_copy, 2, NG)
 
         w1_q = const.tile([P, 2, J], U32, name="w1_q", align_bytes=64)
         w1_s = const.tile([P, 2, J], U8, name="w1_s", align_bytes=64)
@@ -139,7 +149,14 @@ def tile_joint_kernel(tc, h_pred, h_enc, W1, b1, W2, b2, out):
         regroup_w1(nc.vector.tensor_copy, 0, 0, SPLIT1)
         regroup_w1(nc.scalar.copy, 0, SPLIT1, J)
 
-        hpT = psl.tile([P, 2, P], F32, name="hpT", tag="lg")
+        b2bc = const.tile([P, V], BF16, name="b2bc")
+        for vb in range(4):
+            cols = slice(vb * 512, (vb + 1) * 512)
+            acc = bank(3 + vb, [P, 512])
+            nc.tensor.matmul(out=acc[:], lhsT=pick[:], rhs=b2row[:, cols], start=True, stop=True)
+            nc.scalar.copy(out=b2bc[:, cols], in_=acc[:])
+
+        hpT = bank(0, [P, 2, P])
         for u in range(2):
             nc.tensor.transpose(
                 hpT[:, u, :], hp_sb[:].bitcast(F32)[:, u * P : (u + 1) * P], identf[:]
@@ -148,7 +165,7 @@ def tile_joint_kernel(tc, h_pred, h_enc, W1, b1, W2, b2, out):
             out=hp_g[:, :, 0:R_E, :], in_=hpT[:].rearrange("p u (g r) -> p g r u", g=NG)
         )
         for a in range(2):
-            heT = psl.tile([P, 2, P], F32, name="heT%d" % a, tag="lg")
+            heT = bank(1 + a, [P, 2, P])
             for u in range(2):
                 nc.tensor.transpose(
                     heT[:, u, :],
@@ -199,23 +216,23 @@ def tile_joint_kernel(tc, h_pred, h_enc, W1, b1, W2, b2, out):
                 in_=grp2[vb][:].rearrange("p c v t -> p (c v t)"),
             )
 
-        def stage1(g, half, eng_copy):
-            bank = psl.tile([P, 512], F32, name="s1bank", tag="lg")
+        def stage1(g, half, b, eng_copy):
+            acc = bank(b, [P, 512])
             cols = slice(half * 512, (half + 1) * 512)
             rows = slice(g * P, (g + 1) * P)
             nc.tensor.matmul_mx(
-                out=bank[:],
+                out=acc[:],
                 lhsT=hp_q[:, rows].bitcast(FP8X4), lhsT_scale=hp_s[:, rows],
                 rhs=w1_q[:, 0, cols].bitcast(FP8X4), rhs_scale=w1_s[:, 0, cols],
                 start=True, stop=False,
             )
             nc.tensor.matmul_mx(
-                out=bank[:],
+                out=acc[:],
                 lhsT=he_q[:, rows].bitcast(FP8X4), lhsT_scale=he_s[:, rows],
                 rhs=w1_q[:, 1, cols].bitcast(FP8X4), rhs_scale=w1_s[:, 1, cols],
                 start=False, stop=True,
             )
-            eng_copy(out=stack[0:R_B, g, cols], in_=bank[0:R_B, :])
+            eng_copy(out=stack[0:R_B, g, cols], in_=acc[0:R_B, :])
 
         done_t = {}
         z_t, x_t, xq_t, bank_t, y_t, negm_t, ssum_t, chain_t, negk_t = {}, {}, {}, {}, {}, {}, {}, {}, {}
@@ -223,12 +240,12 @@ def tile_joint_kernel(tc, h_pred, h_enc, W1, b1, W2, b2, out):
         def zsum(n):
             g, q = n // NG, n % NG
             for c in range(2):
-                bank = psz.tile([P, 4, P], F32, name="zb", tag="zb")
-                z_t[(n, c)] = bank
+                acc = bank(N_LG + c, [P, 4, P])
+                z_t[(n, c)] = acc
                 for t in range(4):
                     j0 = (4 * c + t) * P
                     nc.tensor.matmul(
-                        out=bank[:, t, :],
+                        out=acc[:, t, :],
                         lhsT=stack[:, g, j0 : j0 + P],
                         rhs=sel[:, q].rearrange("p t u -> p (t u)"),
                         start=True, stop=True,
@@ -250,13 +267,17 @@ def tile_joint_kernel(tc, h_pred, h_enc, W1, b1, W2, b2, out):
             )
             xq_t[n] = (xq, xs)
 
-        def mm(n, vb):
+        def order(n):
+            return (3, 0, 1, 2) if n in SHARED else (0, 1, 2, 3)
+
+        def mm(n, k):
+            vb = order(n)[k]
             xq, xs = xq_t[n]
-            bank = psl.tile([P, 512], F32, name="lg", tag="lg")
-            bank_t[(n, vb)] = bank
+            acc = bank((4 * n + k) % N_LG, [P, 512])
+            bank_t[(n, vb)] = acc
             for c in range(2):
                 nc.tensor.matmul_mx(
-                    out=bank[:],
+                    out=acc[:],
                     lhsT=xq[:, c * P : (c + 1) * P].bitcast(FP8X4),
                     lhsT_scale=xs[:, c * P : (c + 1) * P],
                     rhs=w2_q[:, vb, c, :].bitcast(FP8X4),
@@ -370,16 +391,18 @@ def tile_joint_kernel(tc, h_pred, h_enc, W1, b1, W2, b2, out):
 
         regroup_w2(nc.vector.tensor_copy, 0, 0, 0, 512)
         regroup_w2(nc.scalar.copy, 0, 1, 0, 512)
-        stage1(0, 0, nc.scalar.copy)
-        stage1(0, 1, nc.vector.tensor_copy)
-        stage1(1, 0, nc.scalar.copy)
-        stage1(1, 1, nc.scalar.copy)
+        stage1(0, 0, 3, nc.scalar.copy)
+        stage1(0, 1, 4, nc.vector.tensor_copy)
+        stage1(1, 0, 5, nc.scalar.copy)
+        stage1(1, 1, 0, nc.scalar.copy)
         zsum(0)
         regroup_w2(nc.vector.tensor_copy, 1, 0, 0, 512)
         quant_w2(0)
         tanh(0, 0)
         tanh(0, 1)
         regroup_w2(nc.scalar.copy, 1, 1, SPLIT2, 512)
+        stage1(2, 0, 4, nc.scalar.copy)
+        stage1(2, 1, 5, nc.scalar.copy)
         zsum(1)
         regroup_w2(nc.vector.tensor_copy, 1, 1, 0, SPLIT2)
         regroup_w2(nc.vector.tensor_copy, 2, 0, 0, 512)
@@ -390,41 +413,38 @@ def tile_joint_kernel(tc, h_pred, h_enc, W1, b1, W2, b2, out):
         quant_w2(1)
         mm(0, 1)
         regroup_w2(nc.scalar.copy, 2, 1, SPLIT2, 512)
+        stage1(3, 0, 4, nc.scalar.copy)
+        stage1(3, 1, 5, nc.scalar.copy)
         zsum(2)
         regroup_w2(nc.vector.tensor_copy, 2, 1, 0, SPLIT2)
         regroup_w2(nc.vector.tensor_copy, 3, 0, 0, 512)
         quant_x(1)
         new_y(0)
-        add_b2(0, 0)
-        stage1(2, 0, nc.scalar.copy)
         regroup_w2(nc.scalar.copy, 3, 1, SPLIT2, 512)
         quant_w2(2)
         mm(0, 2)
         mm(1, 0)
         regroup_w2(nc.vector.tensor_copy, 3, 1, 0, SPLIT2)
+        add_b2(0, 0)
         add_b2(0, 1)
-        stage1(2, 1, nc.scalar.copy)
-        stage1(3, 0, nc.scalar.copy)
         tanh(2, 0)
         tanh(2, 1)
         quant_w2(3)
         mm(0, 3)
         mm(1, 1)
-        stage1(3, 1, nc.scalar.copy)
         zsum(3)
 
         for s in range(N_B):
-            order = (3, 0, 1, 2) if s + 1 in SHARED else (0, 1, 2, 3)
             if s + 1 < N_B:
                 new_y(s + 1)
             if 0 < s < N_B - 1:
-                mm(s + 1, order[0])
-                mm(s + 1, order[1])
+                mm(s + 1, 0)
+                mm(s + 1, 1)
             for vb in range(3 if s in SHARED else 4):
                 if s > 0 or vb > 1:
                     add_b2(s, vb)
                 if vb < 2 and s + 1 < N_B:
-                    mm(s + 1, order[vb + 2])
+                    mm(s + 1, vb + 2)
             if s + 2 < N_B:
                 quant_x(s + 2)
             if 4 <= s < END:

@@ -21,12 +21,13 @@ LN2 = math.log(2.0)
 NEWTON = 4
 STEPS = 2 * NEWTON + 1
 SPLIT1 = 640
-SPLIT2 = 256
+SPLIT2 = {1: 128, 2: 192, 3: 256}
 NG = 4
 R_E = NG * U_P
 R_B = R_E + NG * T_E
 N_LG = 6
 SHARED = tuple(range(2, 13))
+FIRST_END = 640
 SPLIT_END = 1280
 END = N_B - 3
 LATE = {END: (END - 4, END - 3), END + 1: (END - 2, END - 1), END + 2: (END,)}
@@ -51,26 +52,27 @@ def tile_joint_kernel(tc, h_pred, h_enc, W1, b1, W2, b2, out):
             return psum.tile(shape, F32, name="bank%d" % i, tag="bank%d" % i)
 
         b1row = const.tile([P, J], BF16, name="b1row")
-        nc.scalar.dma_start(out=b1row[R_B : R_B + 1, :], in_=b1.rearrange("(a m) -> a m", a=1))
-        b2row = const.tile([P, V], BF16, name="b2row")
-        nc.vector.memset(b2row[:].bitcast(I32), 0)
-        nc.scalar.dma_start(out=b2row[R_B : R_B + 1, :], in_=b2.rearrange("(a m) -> a m", a=1))
-        pick = const.tile([P, P], BF16, name="pick")
-        nc.vector.memset(pick[:].bitcast(I32), 0)
-        nc.vector.memset(pick[R_B : R_B + 1, :], 1.0)
+        nc.sync.dma_start(out=b1row[R_B : R_B + 1, :], in_=b1.rearrange("(a m) -> a m", a=1))
+        brows = const.tile([P, P], BF16, name="brows")
+        nc.sync.dma_start(out=brows[0:16, :], in_=b2.rearrange("(a m) -> a m", a=16))
+        nc.sync.dma_start(out=brows[16:32, :], in_=b2.rearrange("(a m) -> a m", a=16))
+        nc.vector.memset(brows[32:64, :].bitcast(I32), 0)
+        nc.vector.memset(brows[64:128, :].bitcast(I32), 0)
         stack = const.tile([P, NG, J], F32, name="stack")
         nc.vector.memset(stack[R_B:P, :, :], 0.0)
         kb = const.tile([P, NEWTON + 1], F32, name="kb")
         for k in range(NEWTON):
             nc.vector.memset(kb[:, k : k + 1], float(k - NEWTON))
         nc.vector.memset(kb[:, NEWTON : NEWTON + 1], LN2 * (0.043 - 127.0) - float(NEWTON))
-        hp_g = const.tile([P, NG, P, 2], F32, name="hp_g", align_bytes=64)
-        he_g = const.tile([P, NG, P, 2], F32, name="he_g", align_bytes=64)
-        nc.gpsimd.memset(hp_g[:, :, R_E:P, :], 0.0)
-        nc.gpsimd.memset(he_g[:, :, 0:R_E, :], 0.0)
-        nc.gpsimd.memset(he_g[:, :, R_B:P, :], 0.0)
+        identb = const.tile([P, P], BF16, name="identb")
+        make_identity(nc, identb[:])
         identf = const.tile([P, P], F32, name="identf")
         make_identity(nc, identf[:])
+        hp_g = const.tile([P, NG, P, 2], F32, name="hp_g", align_bytes=64)
+        he_g = const.tile([P, NG, P, 2], F32, name="he_g", align_bytes=64)
+        nc.vector.memset(hp_g[:, :, R_E:P, :], 0.0)
+        nc.vector.memset(he_g[:, :, 0:R_E, :], 0.0)
+        nc.vector.memset(he_g[:, :, R_B:P, :], 0.0)
         sel = const.tile([P, NG, T_E, U_P], F32, name="sel")
         nc.vector.tensor_tensor(
             out=sel[:],
@@ -127,6 +129,11 @@ def tile_joint_kernel(tc, h_pred, h_enc, W1, b1, W2, b2, out):
         b1_to_stack(nc.scalar.copy, 0, 2)
         b1_to_stack(nc.vector.tensor_copy, 2, NG)
 
+        bps = psum.tile([P, P], BF16, name="bps", tag="bank7")
+        nc.tensor.transpose(bps[:], brows[:], identb[:])
+        b2T = const.tile([P, 16], BF16, name="b2T")
+        nc.vector.tensor_copy(out=b2T[:], in_=bps[:, 0:16])
+
         w1_q = const.tile([P, 2, J], U32, name="w1_q", align_bytes=64)
         w1_s = const.tile([P, 2, J], U8, name="w1_s", align_bytes=64)
         grp1 = []
@@ -151,10 +158,17 @@ def tile_joint_kernel(tc, h_pred, h_enc, W1, b1, W2, b2, out):
 
         b2bc = const.tile([P, V], BF16, name="b2bc")
         for vb in range(4):
-            cols = slice(vb * 512, (vb + 1) * 512)
-            acc = bank(3 + vb, [P, 512])
-            nc.tensor.matmul(out=acc[:], lhsT=pick[:], rhs=b2row[:, cols], start=True, stop=True)
-            nc.scalar.copy(out=b2bc[:, cols], in_=acc[:])
+            acc = bank(3 + vb, [P, 4, P])
+            for a in range(4):
+                nc.tensor.matmul(
+                    out=acc[:, a, :],
+                    lhsT=b2T[:, 4 * vb + a : 4 * vb + a + 1].to_broadcast([P, P]),
+                    rhs=identb[:],
+                    start=True, stop=True,
+                )
+            nc.scalar.copy(
+                out=b2bc[:, vb * 512 : (vb + 1) * 512], in_=acc[:].rearrange("p a m -> p (a m)")
+            )
 
         hpT = bank(0, [P, 2, P])
         for u in range(2):
@@ -386,11 +400,12 @@ def tile_joint_kernel(tc, h_pred, h_enc, W1, b1, W2, b2, out):
                 op0=ALU.add,
             )
 
-        def store(n):
-            nc.sync.dma_start(out=out_rows[n * P : (n + 1) * P, :], in_=y_t[n][:])
+        def store(n, c0=0, c1=V):
+            nc.sync.dma_start(out=out_rows[n * P : (n + 1) * P, c0:c1], in_=y_t[n][:, c0:c1])
 
         regroup_w2(nc.vector.tensor_copy, 0, 0, 0, 512)
         regroup_w2(nc.scalar.copy, 0, 1, 0, 512)
+        regroup_w2(nc.scalar.copy, 1, 1, SPLIT2[1], 512)
         stage1(0, 0, 3, nc.scalar.copy)
         stage1(0, 1, 4, nc.vector.tensor_copy)
         stage1(1, 0, 5, nc.scalar.copy)
@@ -400,11 +415,11 @@ def tile_joint_kernel(tc, h_pred, h_enc, W1, b1, W2, b2, out):
         quant_w2(0)
         tanh(0, 0)
         tanh(0, 1)
-        regroup_w2(nc.scalar.copy, 1, 1, SPLIT2, 512)
         stage1(2, 0, 4, nc.scalar.copy)
         stage1(2, 1, 5, nc.scalar.copy)
+        regroup_w2(nc.scalar.copy, 2, 1, SPLIT2[2], 512)
         zsum(1)
-        regroup_w2(nc.vector.tensor_copy, 1, 1, 0, SPLIT2)
+        regroup_w2(nc.vector.tensor_copy, 1, 1, 0, SPLIT2[1])
         regroup_w2(nc.vector.tensor_copy, 2, 0, 0, 512)
         quant_x(0)
         mm(0, 0)
@@ -412,20 +427,19 @@ def tile_joint_kernel(tc, h_pred, h_enc, W1, b1, W2, b2, out):
         tanh(1, 1)
         quant_w2(1)
         mm(0, 1)
-        regroup_w2(nc.scalar.copy, 2, 1, SPLIT2, 512)
         stage1(3, 0, 4, nc.scalar.copy)
         stage1(3, 1, 5, nc.scalar.copy)
+        regroup_w2(nc.scalar.copy, 3, 1, SPLIT2[3], 512)
         zsum(2)
-        regroup_w2(nc.vector.tensor_copy, 2, 1, 0, SPLIT2)
+        regroup_w2(nc.vector.tensor_copy, 2, 1, 0, SPLIT2[2])
         regroup_w2(nc.vector.tensor_copy, 3, 0, 0, 512)
         quant_x(1)
         new_y(0)
-        regroup_w2(nc.scalar.copy, 3, 1, SPLIT2, 512)
         quant_w2(2)
         mm(0, 2)
         mm(1, 0)
-        regroup_w2(nc.vector.tensor_copy, 3, 1, 0, SPLIT2)
         add_b2(0, 0)
+        regroup_w2(nc.vector.tensor_copy, 3, 1, 0, SPLIT2[3])
         add_b2(0, 1)
         tanh(2, 0)
         tanh(2, 1)
@@ -491,6 +505,8 @@ def tile_joint_kernel(tc, h_pred, h_enc, W1, b1, W2, b2, out):
         store(N_B - 2)
         exp_sum(N_B - 1)
         finish(range(N_B - 1, N_B))
-        sub_vec(N_B - 1, 0, SPLIT_END)
+        sub_vec(N_B - 1, 0, FIRST_END)
+        store(N_B - 1, 0, FIRST_END)
+        sub_vec(N_B - 1, FIRST_END, SPLIT_END)
         sub_act(N_B - 1, SPLIT_END, V)
-        store(N_B - 1)
+        store(N_B - 1, FIRST_END, V)

@@ -21,7 +21,7 @@ LN2 = math.log(2.0)
 NEWTON = 4
 STEPS = 2 * NEWTON + 1
 SPLIT1 = 640
-SPLIT2 = {1: 128, 2: 192, 3: 256}
+SPLIT2 = {1: 192, 2: 256, 3: 256}
 NG = 4
 R_E = NG * U_P
 R_B = R_E + NG * T_E
@@ -127,7 +127,6 @@ def tile_joint_kernel(tc, h_pred, h_enc, W1, b1, W2, b2, out):
             )
 
         b1_to_stack(nc.scalar.copy, 0, 2)
-        b1_to_stack(nc.vector.tensor_copy, 2, NG)
 
         bps = psum.tile([P, P], BF16, name="bps", tag="bank7")
         nc.tensor.transpose(bps[:], brows[:], identb[:])
@@ -156,20 +155,6 @@ def tile_joint_kernel(tc, h_pred, h_enc, W1, b1, W2, b2, out):
         regroup_w1(nc.vector.tensor_copy, 0, 0, SPLIT1)
         regroup_w1(nc.scalar.copy, 0, SPLIT1, J)
 
-        b2bc = const.tile([P, V], BF16, name="b2bc")
-        for vb in range(4):
-            acc = bank(3 + vb, [P, 4, P])
-            for a in range(4):
-                nc.tensor.matmul(
-                    out=acc[:, a, :],
-                    lhsT=b2T[:, 4 * vb + a : 4 * vb + a + 1].to_broadcast([P, P]),
-                    rhs=identb[:],
-                    start=True, stop=True,
-                )
-            nc.scalar.copy(
-                out=b2bc[:, vb * 512 : (vb + 1) * 512], in_=acc[:].rearrange("p a m -> p (a m)")
-            )
-
         hpT = bank(0, [P, 2, P])
         for u in range(2):
             nc.tensor.transpose(
@@ -194,6 +179,20 @@ def tile_joint_kernel(tc, h_pred, h_enc, W1, b1, W2, b2, out):
         hp_s = const.tile([P, NG * P], U8, name="hp_s", align_bytes=64)
         he_q = const.tile([P, NG * P], U32, name="he_q", align_bytes=64)
         he_s = const.tile([P, NG * P], U8, name="he_s", align_bytes=64)
+        b2bc = const.tile([P, V], BF16, name="b2bc")
+        for vb in range(4):
+            acc = bank(3 + vb, [P, 4, P])
+            for a in range(4):
+                nc.tensor.matmul(
+                    out=acc[:, a, :],
+                    lhsT=b2T[:, 4 * vb + a : 4 * vb + a + 1].to_broadcast([P, P]),
+                    rhs=identb[:],
+                    start=True, stop=True,
+                )
+            nc.scalar.copy(
+                out=b2bc[:, vb * 512 : (vb + 1) * 512], in_=acc[:].rearrange("p a m -> p (a m)")
+            )
+
         quant_w1(0)
         nc.vector.quantize_mx(
             out=hp_q[:].bitcast(FP8X4),
@@ -433,9 +432,9 @@ def tile_joint_kernel(tc, h_pred, h_enc, W1, b1, W2, b2, out):
         zsum(2)
         regroup_w2(nc.vector.tensor_copy, 2, 1, 0, SPLIT2[2])
         regroup_w2(nc.vector.tensor_copy, 3, 0, 0, 512)
-        quant_x(1)
         new_y(0)
         quant_w2(2)
+        quant_x(1)
         mm(0, 2)
         mm(1, 0)
         add_b2(0, 0)
@@ -447,6 +446,7 @@ def tile_joint_kernel(tc, h_pred, h_enc, W1, b1, W2, b2, out):
         mm(0, 3)
         mm(1, 1)
         zsum(3)
+        b1_to_stack(nc.scalar.copy, 2, NG)
 
         for s in range(N_B):
             if s + 1 < N_B:
@@ -504,7 +504,13 @@ def tile_joint_kernel(tc, h_pred, h_enc, W1, b1, W2, b2, out):
         sub_vec(N_B - 2, 0, V)
         store(N_B - 2)
         exp_sum(N_B - 1)
-        finish(range(N_B - 1, N_B))
+        lse = st.tile([P, 1], F32, name="lse", tag="lse")
+        nc.scalar.activation(out=lse[:], in_=ssum_t[N_B - 1][:], func=ACT.Ln)
+        negk = st.tile([P, 1], F32, name="negk", tag="negk")
+        nc.scalar.activation(
+            out=negk[:], in_=lse[:], func=ACT.Identity, bias=negm_t[N_B - 1][:, 0:1], scale=-1.0
+        )
+        negk_t[N_B - 1] = negk
         sub_vec(N_B - 1, 0, FIRST_END)
         store(N_B - 1, 0, FIRST_END)
         sub_vec(N_B - 1, FIRST_END, SPLIT_END)

@@ -28,9 +28,10 @@ R_B = R_E + NG * T_E
 N_LG = 6
 SHARED = tuple(range(2, 13))
 FIRST_END = 640
+HALF = P // 2
 SPLIT_END = 1280
 END = N_B - 3
-LATE = {END: (END - 4, END - 3), END + 1: (END - 2, END - 1), END + 2: (END,)}
+LATE = {END: (END - 3, END - 2, END - 1), END + 1: (END,)}
 
 
 def tile_joint_kernel(tc, h_pred, h_enc, W1, b1, W2, b2, out):
@@ -264,11 +265,13 @@ def tile_joint_kernel(tc, h_pred, h_enc, W1, b1, W2, b2, out):
                         start=True, stop=True,
                     )
 
-        def tanh(n, c):
-            if c == 0:
+        def tanh(n, c, r0=0, r1=P):
+            if c == 0 and r0 == 0:
                 x_t[n] = xp.tile([P, 2, P, 4], BF16, name="x", tag="x", align_bytes=64)
             nc.scalar.activation(
-                out=x_t[n][:, c], in_=z_t[(n, c)][:].rearrange("p t r -> p r t"), func=ACT.Tanh
+                out=x_t[n][:, c, r0:r1],
+                in_=z_t[(n, c)][:, :, r0:r1].rearrange("p t r -> p r t"),
+                func=ACT.Tanh,
             )
 
         def quant_x(n):
@@ -461,43 +464,29 @@ def tile_joint_kernel(tc, h_pred, h_enc, W1, b1, W2, b2, out):
                     mm(s + 1, vb + 2)
             if s + 2 < N_B:
                 quant_x(s + 2)
-            if 4 <= s < END:
-                minus_lse(s - 4)
+            if 3 <= s <= END:
+                minus_lse(s - 3)
             row_max(s)
             if s >= 1:
                 exp_sum(s - 1)
             if s < END:
-                if s < END - 1:
-                    step(s - 2, 4)
-                    step(s - 3, 8)
-                tanh(s + 3, 0)
-                step(s - 1, 1)
-                if s < END - 1:
-                    step(s - 2, 5)
-                    step(s - 3, 9)
-                tanh(s + 3, 1)
-                step(s - 1, 2)
-                if s < END - 1:
-                    step(s - 2, 6)
+                step(s - 2, 6)
+                for i in range(4):
+                    tanh(s + 3, i // 2, i % 2 * HALF, (i % 2 + 1) * HALF)
+                    step(s - 1, i + 1)
+                    if i < 3:
+                        step(s - 2, i + 7)
             if s + 1 in SHARED:
                 copy_last(s + 1)
             if s + 4 < N_B:
                 zsum(s + 4)
             if s < END:
-                step(s - 1, 3)
-            if s < END - 1:
-                step(s - 2, 7)
-            if s == END - 1:
-                finish(range(s - 3, s - 1))
-            if s >= END:
+                step(s - 1, 5)
+            else:
                 finish(range(END - 2, s))
-            if 4 <= s < END:
-                sub_gps(s - 4, 0, V)
-                store(s - 4)
-            elif s >= END:
-                for n in LATE[s]:
-                    sub_gps(n, 0, V)
-                    store(n)
+            for n in LATE.get(s, (s - 3,) if 3 <= s < END else ()):
+                sub_gps(n, 0, V)
+                store(n)
             if s + 1 in SHARED:
                 add_last(s + 1)
 

@@ -20,6 +20,7 @@ FLOPS = 2 * (N_B * U_P * H * J + N_B * T_E * H * J + N_B * T_E * U_P * J * V)
 LN2 = math.log(2.0)
 NEWTON = 4
 STEPS = 2 * NEWTON + 1
+RUN = 8
 SPLIT1 = 640
 SPLIT2 = {1: 192, 2: 256, 3: 256}
 NG = 4
@@ -142,8 +143,8 @@ def tile_joint_kernel(tc, h_pred, h_enc, W1, b1, W2, b2, out):
 
         def regroup_w1(eng_copy, half, c0, c1):
             eng_copy(
-                out=grp1[half][:, c0:c1, :].rearrange("p (c i) t -> p c t i", i=4),
-                in_=raw1[half][:, :, c0:c1].rearrange("p t (c i) -> p c t i", i=4),
+                out=grp1[half][:, c0:c1, :].rearrange("p (c i) t -> p c t i", i=RUN),
+                in_=raw1[half][:, :, c0:c1].rearrange("p t (c i) -> p c t i", i=RUN),
             )
 
         def quant_w1(half):
@@ -219,8 +220,8 @@ def tile_joint_kernel(tc, h_pred, h_enc, W1, b1, W2, b2, out):
                     [P, 2, 512, 4], BF16, name="grp2_%d" % vb, tag="grp", align_bytes=64
                 )
             eng_copy(
-                out=grp2[vb][:, c, v0:v1, :].rearrange("p (v i) t -> p v t i", i=4),
-                in_=raw2[vb][:, 4 * c : 4 * c + 4, v0:v1].rearrange("p t (v i) -> p v t i", i=4),
+                out=grp2[vb][:, c, v0:v1, :].rearrange("p (v i) t -> p v t i", i=RUN),
+                in_=raw2[vb][:, 4 * c : 4 * c + 4, v0:v1].rearrange("p t (v i) -> p v t i", i=RUN),
             )
 
         def quant_w2(vb):

import math
from contextlib import ExitStack

import concourse.mybir as mybir
from concourse.masks import make_identity

F32 = mybir.dt.float32
BF16 = mybir.dt.bfloat16
U32 = mybir.dt.uint32
U8 = mybir.dt.uint8
I32 = mybir.dt.int32
FP8X4 = mybir.dt.float8_e4m3fn_x4
ALU = mybir.AluOpType
ACT = mybir.ActivationFunctionType
AX = mybir.AxisListType

P = 128
N_B, T_E, U_P, H, J, V = 16, 16, 8, 512, 1024, 2048
FLOPS = 2 * (N_B * U_P * H * J + N_B * T_E * H * J + N_B * T_E * U_P * J * V)
LN2 = math.log(2.0)
NEWTON = 4
STEPS = 2 * NEWTON + 1
RUN = 8
SPLIT1 = 640
SPLIT2 = {1: 192, 2: 256, 3: 256}
NG = 4
R_E = NG * U_P
R_B = R_E + NG * T_E
N_LG = 6
SHARED = tuple(range(2, 13))
FIRST_END = 640
HALF = P // 2
SPLIT_END = 1280
END = N_B - 3
LATE = {END: (END - 3, END - 2, END - 1), END + 1: (END,)}


def tile_joint_kernel(tc, h_pred, h_enc, W1, b1, W2, b2, out):
    nc = tc.nc
    out_rows = out.rearrange("n t u v -> (n t u) v")
    with ExitStack() as ctx:
        const = ctx.enter_context(tc.tile_pool(name="const", bufs=1))
        rawp = ctx.enter_context(tc.tile_pool(name="rawp", bufs=6))
        grpp = ctx.enter_context(tc.tile_pool(name="grpp", bufs=3))
        xp = ctx.enter_context(tc.tile_pool(name="xp", bufs=3))
        xqp = ctx.enter_context(tc.tile_pool(name="xqp", bufs=4))
        yp = ctx.enter_context(tc.tile_pool(name="yp", bufs=7))
        jp = ctx.enter_context(tc.tile_pool(name="jp", bufs=2))
        st = ctx.enter_context(tc.tile_pool(name="st", bufs=8))
        psum = ctx.enter_context(tc.psum_pool(name="psum", bufs=1))
        ctx.enter_context(tc.manual_schedule())

        def bank(i, shape):
            return psum.tile(shape, F32, name="bank%d" % i, tag="bank%d" % i)

        b1row = const.tile([P, J], BF16, name="b1row")
        nc.sync.dma_start(out=b1row[R_B : R_B + 1, :], in_=b1.rearrange("(a m) -> a m", a=1))
        brows = const.tile([P, P], BF16, name="brows")
        nc.sync.dma_start(out=brows[0:16, :], in_=b2.rearrange("(a m) -> a m", a=16))
        nc.sync.dma_start(out=brows[16:32, :], in_=b2.rearrange("(a m) -> a m", a=16))
        nc.vector.memset(brows[32:64, :].bitcast(I32), 0)
        nc.vector.memset(brows[64:128, :].bitcast(I32), 0)
        stack = const.tile([P, NG, J], F32, name="stack")
        nc.vector.memset(stack[R_B:P, :, :], 0.0)
        kb = const.tile([P, NEWTON + 1], F32, name="kb")
        for k in range(NEWTON):
            nc.vector.memset(kb[:, k : k + 1], float(k - NEWTON))
        nc.vector.memset(kb[:, NEWTON : NEWTON + 1], LN2 * (0.043 - 127.0) - float(NEWTON))
        identb = const.tile([P, P], BF16, name="identb")
        make_identity(nc, identb[:])
        identf = const.tile([P, P], F32, name="identf")
        make_identity(nc, identf[:])
        hp_g = const.tile([P, NG, P, 2], F32, name="hp_g", align_bytes=64)
        he_g = const.tile([P, NG, P, 2], F32, name="he_g", align_bytes=64)
        nc.vector.memset(hp_g[:, :, R_E:P, :], 0.0)
        nc.vector.memset(he_g[:, :, 0:R_E, :], 0.0)
        nc.vector.memset(he_g[:, :, R_B:P, :], 0.0)
        sel = const.tile([P, NG, T_E, U_P], F32, name="sel")
        nc.vector.tensor_tensor(
            out=sel[:],
            in0=identf[:, 0:R_E]
            .rearrange("p (q u) -> p q u", q=NG)
            .unsqueeze(2)
            .to_broadcast([P, NG, T_E, U_P]),
            in1=identf[:, R_E:R_B]
            .rearrange("p (q t) -> p q t", q=NG)
            .unsqueeze(3)
            .to_broadcast([P, NG, T_E, U_P]),
            op=ALU.add,
        )
        nc.vector.tensor_scalar(
            out=sel[:].rearrange("p q t u -> p (q t u)"),
            in0=sel[:].rearrange("p q t u -> p (q t u)"),
            scalar1=identf[:, R_B : R_B + 1], scalar2=None, op0=ALU.add,
        )

        def load_w1(half):
            raw = rawp.tile([P, 4, J], BF16, name="raw1_%d" % half, tag="raw")
            nc.sync.dma_start(
                out=raw[:].rearrange("p (u e) c -> p u (e c)", u=2),
                in_=W1[half * H : (half + 1) * H, :].rearrange(
                    "(u q e) c -> q u (e c)", u=2, q=P, e=2
                ),
            )
            return raw

        raw1 = [load_w1(0)]
        hp_sb = const.tile([P, H], BF16, name="hp_sb")
        nc.sync.dma_start(out=hp_sb[:], in_=h_pred.rearrange("n u h -> (n u) h"))
        he_sb = const.tile([P, 2, H], BF16, name="he_sb")
        nc.sync.dma_start(
            out=he_sb[:],
            in_=h_enc.rearrange("n t h -> (n t) h").rearrange("(a p) h -> p a h", p=P),
        )
        raw1.append(load_w1(1))
        raw2 = []
        for vb in range(4):
            raw = rawp.tile([P, 8, 512], BF16, name="raw2_%d" % vb, tag="raw")
            nc.sync.dma_start(
                out=raw[:],
                in_=W2[:, vb * 512 : (vb + 1) * 512].rearrange("(g p) v -> p g v", p=P),
            )
            raw2.append(raw)

        def b1_to_stack(copy, g0, g1):
            copy(
                out=stack[R_B : R_B + 1, g0:g1, :],
                in_=b1row[R_B : R_B + 1, :].unsqueeze(1).to_broadcast([1, g1 - g0, J]),
            )

        b1_to_stack(nc.scalar.copy, 0, 2)

        bps = psum.tile([P, P], BF16, name="bps", tag="bank7")
        nc.tensor.transpose(bps[:], brows[:], identb[:])
        b2T = const.tile([P, 16], BF16, name="b2T")
        nc.vector.tensor_copy(out=b2T[:], in_=bps[:, 0:16])

        w1_q = const.tile([P, 2, J], U32, name="w1_q", align_bytes=64)
        w1_s = const.tile([P, 2, J], U8, name="w1_s", align_bytes=64)
        grp1 = []
        for half in range(2):
            grp1.append(grpp.tile([P, J, 4], BF16, name="grp1_%d" % half, tag="grp", align_bytes=64))

        def regroup_w1(eng_copy, half, c0, c1):
            eng_copy(
                out=grp1[half][:, c0:c1, :].rearrange("p (c i) t -> p c t i", i=RUN),
                in_=raw1[half][:, :, c0:c1].rearrange("p t (c i) -> p c t i", i=RUN),
            )

        def quant_w1(half):
            nc.vector.quantize_mx(
                out=w1_q[:, half, :].bitcast(FP8X4),
                scales=w1_s[:, half, :],
                in_=grp1[half][:].rearrange("p c t -> p (c t)"),
            )

        regroup_w1(nc.vector.tensor_copy, 0, 0, SPLIT1)
        regroup_w1(nc.scalar.copy, 0, SPLIT1, J)

        hpT = bank(0, [P, 2, P])
        for u in range(2):
            nc.tensor.transpose(
                hpT[:, u, :], hp_sb[:].bitcast(F32)[:, u * P : (u + 1) * P], identf[:]
            )
        nc.vector.tensor_copy(
            out=hp_g[:, :, 0:R_E, :], in_=hpT[:].rearrange("p u (g r) -> p g r u", g=NG)
        )
        for a in range(2):
            heT = bank(1 + a, [P, 2, P])
            for u in range(2):
                nc.tensor.transpose(
                    heT[:, u, :],
                    he_sb[:, a, :].bitcast(F32)[:, u * P : (u + 1) * P],
                    identf[:],
                )
            nc.vector.tensor_copy(
                out=he_g[:, 2 * a : 2 * a + 2, R_E:R_B, :],
                in_=heT[:].rearrange("p u (g r) -> p g r u", g=2),
            )
        hp_q = const.tile([P, NG * P], U32, name="hp_q", align_bytes=64)
        hp_s = const.tile([P, NG * P], U8, name="hp_s", align_bytes=64)
        he_q = const.tile([P, NG * P], U32, name="he_q", align_bytes=64)
        he_s = const.tile([P, NG * P], U8, name="he_s", align_bytes=64)
        b2bc = const.tile([P, V], BF16, name="b2bc")
        for vb in range(4):
            acc = bank(3 + vb, [P, 4, P])
            for a in range(4):
                nc.tensor.matmul(
                    out=acc[:, a, :],
                    lhsT=b2T[:, 4 * vb + a : 4 * vb + a + 1].to_broadcast([P, P]),
                    rhs=identb[:],
                    start=True, stop=True,
                )
            nc.scalar.copy(
                out=b2bc[:, vb * 512 : (vb + 1) * 512], in_=acc[:].rearrange("p a m -> p (a m)")
            )

        quant_w1(0)
        nc.vector.quantize_mx(
            out=hp_q[:].bitcast(FP8X4),
            scales=hp_s[:],
            in_=hp_g[:].rearrange("p g r u -> p (g r u)").bitcast(BF16),
        )
        regroup_w1(nc.vector.tensor_copy, 1, 0, SPLIT1)
        regroup_w1(nc.scalar.copy, 1, SPLIT1, J)
        nc.vector.quantize_mx(
            out=he_q[:].bitcast(FP8X4),
            scales=he_s[:],
            in_=he_g[:].rearrange("p g r u -> p (g r u)").bitcast(BF16),
        )
        quant_w1(1)

        w2_q = const.tile([P, 4, 2, 512], U32, name="w2_q", align_bytes=64)
        w2_s = const.tile([P, 4, 2, 512], U8, name="w2_s", align_bytes=64)
        grp2 = {}

        def regroup_w2(eng_copy, vb, c, v0, v1):
            if vb not in grp2:
                grp2[vb] = grpp.tile(
                    [P, 2, 512, 4], BF16, name="grp2_%d" % vb, tag="grp", align_bytes=64
                )
            eng_copy(
                out=grp2[vb][:, c, v0:v1, :].rearrange("p (v i) t -> p v t i", i=RUN),
                in_=raw2[vb][:, 4 * c : 4 * c + 4, v0:v1].rearrange("p t (v i) -> p v t i", i=RUN),
            )

        def quant_w2(vb):
            nc.vector.quantize_mx(
                out=w2_q[:, vb].rearrange("p c v -> p (c v)").bitcast(FP8X4),
                scales=w2_s[:, vb].rearrange("p c v -> p (c v)"),
                in_=grp2[vb][:].rearrange("p c v t -> p (c v t)"),
            )

        def stage1(g, half, b, eng_copy):
            acc = bank(b, [P, 512])
            cols = slice(half * 512, (half + 1) * 512)
            rows = slice(g * P, (g + 1) * P)
            nc.tensor.matmul_mx(
                out=acc[:],
                lhsT=hp_q[:, rows].bitcast(FP8X4), lhsT_scale=hp_s[:, rows],
                rhs=w1_q[:, 0, cols].bitcast(FP8X4), rhs_scale=w1_s[:, 0, cols],
                start=True, stop=False,
            )
            nc.tensor.matmul_mx(
                out=acc[:],
                lhsT=he_q[:, rows].bitcast(FP8X4), lhsT_scale=he_s[:, rows],
                rhs=w1_q[:, 1, cols].bitcast(FP8X4), rhs_scale=w1_s[:, 1, cols],
                start=False, stop=True,
            )
            eng_copy(out=stack[0:R_B, g, cols], in_=acc[0:R_B, :])

        done_t = {}
        z_t, x_t, xq_t, bank_t, y_t, negm_t, ssum_t, chain_t, negk_t = {}, {}, {}, {}, {}, {}, {}, {}, {}

        def zsum(n):
            g, q = n // NG, n % NG
            for c in range(2):
                acc = bank(N_LG + c, [P, 4, P])
                z_t[(n, c)] = acc
                for t in range(4):
                    j0 = (4 * c + t) * P
                    nc.tensor.matmul(
                        out=acc[:, t, :],
                        lhsT=stack[:, g, j0 : j0 + P],
                        rhs=sel[:, q].rearrange("p t u -> p (t u)"),
                        start=True, stop=True,
                    )

        def tanh(n, c, r0=0, r1=P):
            if c == 0 and r0 == 0:
                x_t[n] = xp.tile([P, 2, P, 4], BF16, name="x", tag="x", align_bytes=64)
            nc.scalar.activation(
                out=x_t[n][:, c, r0:r1],
                in_=z_t[(n, c)][:, :, r0:r1].rearrange("p t r -> p r t"),
                func=ACT.Tanh,
            )

        def quant_x(n):
            xq = xqp.tile([P, 2 * P], U32, name="xq", tag="xq", align_bytes=64)
            xs = xqp.tile([P, 2 * P], U8, name="xs", tag="xs", align_bytes=64)
            nc.vector.quantize_mx(
                out=xq[:].bitcast(FP8X4), scales=xs[:],
                in_=x_t[n][:].rearrange("p c r t -> p (c r t)"),
            )
            xq_t[n] = (xq, xs)

        def order(n):
            return (3, 0, 1, 2) if n in SHARED else (0, 1, 2, 3)

        def mm(n, k):
            vb = order(n)[k]
            xq, xs = xq_t[n]
            acc = bank((4 * n + k) % N_LG, [P, 512])
            bank_t[(n, vb)] = acc
            for c in range(2):
                nc.tensor.matmul_mx(
                    out=acc[:],
                    lhsT=xq[:, c * P : (c + 1) * P].bitcast(FP8X4),
                    lhsT_scale=xs[:, c * P : (c + 1) * P],
                    rhs=w2_q[:, vb, c, :].bitcast(FP8X4),
                    rhs_scale=w2_s[:, vb, c, :],
                    start=(c == 0),
                    stop=(c == 1),
                )

        def new_y(n):
            y_t[n] = yp.tile([P, V], F32, name="y", tag="y")

        def copy_last(n):
            nc.scalar.copy(out=y_t[n][:, 1536:V], in_=bank_t[(n, 3)][:])

        def add_last(n):
            nc.gpsimd.tensor_tensor(
                out=y_t[n][:, 1536:V], in0=y_t[n][:, 1536:V], in1=b2bc[:, 1536:V], op=ALU.add
            )

        def add_b2(n, vb):
            nc.vector.tensor_tensor(
                out=y_t[n][:, vb * 512 : (vb + 1) * 512],
                in0=bank_t[(n, vb)][:],
                in1=b2bc[:, vb * 512 : (vb + 1) * 512],
                op=ALU.add,
            )

        def row_max(n):
            negm = st.tile([P, 1], F32, name="negm", tag="negm")
            negm_t[n] = negm
            nc.vector.tensor_reduce(out=negm[:], in_=y_t[n][:], axis=AX.X, op=ALU.max, negate=True)

        def exp_sum(n):
            junk = jp.tile([P, V], BF16, name="junk", tag="junk")
            ssum = st.tile([P, 1], F32, name="ssum", tag="ssum")
            ssum_t[n] = ssum
            nc.scalar.activation(
                out=junk[:], in_=y_t[n][:], func=ACT.Exp, bias=negm_t[n][:, 0:1], scale=1.0,
                accum_out=ssum[:, 0:1],
            )

        def step(n, k):
            if n < 0:
                return
            done_t[n] = k
            if k == 1:
                r = st.tile([P, 1], F32, name="nr", tag="nr")
                nc.scalar.activation(
                    out=r[:], in_=ssum_t[n][:].bitcast(U32), func=ACT.Identity,
                    bias=kb[:, NEWTON : NEWTON + 1], scale=LN2 / 8388608.0,
                )
                chain_t[n] = (r, None)
            elif k % 2 == 0:
                r, e = chain_t[n]
                i = k // 2 - 1
                e = st.tile([P, 1], F32, name="ne", tag="ne")
                nc.scalar.activation(
                    out=e[:], in_=r[:], func=ACT.Exp, bias=kb[:, i : i + 1], scale=-1.0
                )
                chain_t[n] = (r, e)
            else:
                r, e = chain_t[n]
                r2 = st.tile([P, 1], F32, name="nr", tag="nr")
                nc.scalar.activation(
                    out=r2[:], in_=e[:], func=ACT.Identity, bias=r[:, 0:1], scale=ssum_t[n][:, 0:1]
                )
                chain_t[n] = (r2, None)

        def finish(rows):
            for i in range(STEPS + 1):
                for n in rows:
                    k = done_t.get(n, 0) + 1
                    if k <= STEPS:
                        step(n, k)
                    elif k == STEPS + 1:
                        done_t[n] = k
                        negk = st.tile([P, 1], F32, name="negk", tag="negk")
                        nc.scalar.activation(
                            out=negk[:], in_=chain_t[n][0][:], func=ACT.Identity,
                            bias=negm_t[n][:, 0:1], scale=-1.0,
                        )
                        negk_t[n] = negk

        def minus_lse(n):
            negk = st.tile([P, 1], F32, name="negk", tag="negk")
            nc.vector.tensor_tensor(
                out=negk[:], in0=negm_t[n][:], in1=chain_t[n][0][:], op=ALU.subtract
            )
            negk_t[n] = negk

        def sub_gps(n, c0, c1):
            nc.gpsimd.tensor_scalar(
                out=y_t[n][:, c0:c1], in0=y_t[n][:, c0:c1], scalar1=negk_t[n][:, 0:1], scalar2=1.0,
                op0=ALU.add, op1=ALU.mult,
            )

        def sub_act(n, c0, c1):
            nc.scalar.activation(
                out=y_t[n][:, c0:c1], in_=y_t[n][:, c0:c1], func=ACT.Identity,
                bias=negk_t[n][:, 0:1], scale=1.0,
            )

        def sub_vec(n, c0, c1):
            nc.vector.tensor_scalar(
                out=y_t[n][:, c0:c1], in0=y_t[n][:, c0:c1], scalar1=negk_t[n][:, 0:1], scalar2=None,
                op0=ALU.add,
            )

        def store(n, c0=0, c1=V):
            nc.sync.dma_start(out=out_rows[n * P : (n + 1) * P, c0:c1], in_=y_t[n][:, c0:c1])

        regroup_w2(nc.vector.tensor_copy, 0, 0, 0, 512)
        regroup_w2(nc.scalar.copy, 0, 1, 0, 512)
        regroup_w2(nc.scalar.copy, 1, 1, SPLIT2[1], 512)
        stage1(0, 0, 3, nc.scalar.copy)
        stage1(0, 1, 4, nc.vector.tensor_copy)
        stage1(1, 0, 5, nc.scalar.copy)
        stage1(1, 1, 0, nc.scalar.copy)
        zsum(0)
        regroup_w2(nc.vector.tensor_copy, 1, 0, 0, 512)
        quant_w2(0)
        tanh(0, 0)
        tanh(0, 1)
        stage1(2, 0, 4, nc.scalar.copy)
        stage1(2, 1, 5, nc.scalar.copy)
        regroup_w2(nc.scalar.copy, 2, 1, SPLIT2[2], 512)
        zsum(1)
        regroup_w2(nc.vector.tensor_copy, 1, 1, 0, SPLIT2[1])
        regroup_w2(nc.vector.tensor_copy, 2, 0, 0, 512)
        quant_x(0)
        mm(0, 0)
        tanh(1, 0)
        tanh(1, 1)
        quant_w2(1)
        mm(0, 1)
        stage1(3, 0, 4, nc.scalar.copy)
        stage1(3, 1, 5, nc.scalar.copy)
        regroup_w2(nc.scalar.copy, 3, 1, SPLIT2[3], 512)
        zsum(2)
        regroup_w2(nc.vector.tensor_copy, 2, 1, 0, SPLIT2[2])
        regroup_w2(nc.vector.tensor_copy, 3, 0, 0, 512)
        new_y(0)
        quant_w2(2)
        quant_x(1)
        mm(0, 2)
        mm(1, 0)
        add_b2(0, 0)
        regroup_w2(nc.vector.tensor_copy, 3, 1, 0, SPLIT2[3])
        add_b2(0, 1)
        tanh(2, 0)
        tanh(2, 1)
        quant_w2(3)
        mm(0, 3)
        mm(1, 1)
        zsum(3)
        b1_to_stack(nc.scalar.copy, 2, NG)

        for s in range(N_B):
            if s + 1 < N_B:
                new_y(s + 1)
            if 0 < s < N_B - 1:
                mm(s + 1, 0)
                mm(s + 1, 1)
            for vb in range(3 if s in SHARED else 4):
                if s > 0 or vb > 1:
                    add_b2(s, vb)
                if vb < 2 and s + 1 < N_B:
                    mm(s + 1, vb + 2)
            if s + 2 < N_B:
                quant_x(s + 2)
            if 3 <= s <= END:
                minus_lse(s - 3)
            row_max(s)
            if s >= 1:
                exp_sum(s - 1)
            if s < END:
                step(s - 2, 6)
                for i in range(4):
                    tanh(s + 3, i // 2, i % 2 * HALF, (i % 2 + 1) * HALF)
                    step(s - 1, i + 1)
                    if i < 3:
                        step(s - 2, i + 7)
            if s + 1 in SHARED:
                copy_last(s + 1)
            if s + 4 < N_B:
                zsum(s + 4)
            if s < END:
                step(s - 1, 5)
            else:
                finish(range(END - 2, s))
            for n in LATE.get(s, (s - 3,) if 3 <= s < END else ()):
                sub_gps(n, 0, V)
                store(n)
            if s + 1 in SHARED:
                add_last(s + 1)

        sub_vec(N_B - 2, 0, V)
        store(N_B - 2)
        exp_sum(N_B - 1)
        lse = st.tile([P, 1], F32, name="lse", tag="lse")
        nc.scalar.activation(out=lse[:], in_=ssum_t[N_B - 1][:], func=ACT.Ln)
        negk = st.tile([P, 1], F32, name="negk", tag="negk")
        nc.scalar.activation(
            out=negk[:], in_=lse[:], func=ACT.Identity, bias=negm_t[N_B - 1][:, 0:1], scale=-1.0
        )
        negk_t[N_B - 1] = negk
        sub_vec(N_B - 1, 0, FIRST_END)
        store(N_B - 1, 0, FIRST_END)
        sub_vec(N_B - 1, FIRST_END, SPLIT_END)
        sub_act(N_B - 1, SPLIT_END, V)
        store(N_B - 1, FIRST_END, V)
